import numpy as np
import ml_dtypes


def mxq(x, axis, fmt="e4m3"):
    dtype, down = {"e4m3": (ml_dtypes.float8_e4m3fn, 7), "e5m2": (ml_dtypes.float8_e5m2, 14)}[fmt]
    v = np.moveaxis(np.asarray(x, np.float32).astype(ml_dtypes.bfloat16).astype(np.float64), axis, -1)
    blocks = v.reshape(v.shape[:-1] + (-1, 32))
    amax = np.abs(blocks).max(-1, keepdims=True)
    byte = np.maximum(np.where(amax > 0, np.frexp(amax)[1] - 1 + 127, 0) - down, 1)
    scale = np.exp2(byte - 127.0)
    codes = (blocks / scale).astype(np.float32).astype(dtype).astype(np.float64)
    return np.moveaxis((codes * scale).reshape(v.shape), -1, axis)


WIDE = False


def mx_kscale(k):
    if not WIDE:
        return np.ones(k)
    levels = np.array([10, -10, 5, -5, 0])
    if k % 512:
        return np.exp2(np.random.permutation(np.resize(levels, k // 32))).repeat(32)
    a = np.empty((k // 512, 16))
    for p in range(k // 512):
        a[p, :8] = np.random.permutation(np.resize(levels, 8))
        for g in range(8):
            far = levels[np.abs(levels - a[p, g]) >= 10]
            a[p, g + 8] = far[np.random.randint(len(far))]
    return np.exp2(a.ravel()).repeat(32)


BF16 = ml_dtypes.bfloat16


def bf(x):
    return np.asarray(x, np.float32).astype(BF16)


def f64(x):
    return np.asarray(x).astype(np.float64)


B, I, H = 8192, 512, 128
EPS = 1e-5


def sigmoid(v):
    return 1.0 / (1.0 + np.exp(-v))


def _bn(v, gamma, beta):
    m = np.mean(v, axis=0)
    var = np.var(v, axis=0)
    return (v - m) * (gamma / np.sqrt(var + EPS)) + beta


def setup_inputs():
    rn = np.random.standard_normal
    s = mx_kscale(I)
    return {"x": bf(rn((B, I)) * s),
            "c": bf(rn((B, H))),
            "h": bf(rn((B, H))),
            "w_ih": bf(rn((4 * H, I)) / np.sqrt(I) / s),
            "w_hh": bf(rn((4 * H, H)) / np.sqrt(H)),
            "b": bf(0.3 * rn(4 * H)),
            "g_ih": bf(1.0 + 0.1 * rn(4 * H)),
            "b_ih": bf(0.3 * rn(4 * H)),
            "g_hh": bf(1.0 + 0.1 * rn(4 * H)),
            "b_hh": bf(0.3 * rn(4 * H)),
            "g_c": bf(1.0 + 0.1 * rn(H)),
            "b_c": bf(0.3 * rn(H))}


def reference(x, c, h, w_ih, w_hh, b, g_ih, b_ih, g_hh, b_hh, g_c, b_c):
    ih = mxq(f64(x), 1, "e4m3") @ mxq(f64(w_ih), 1, "e4m3").T
    hh = f64(h) @ f64(w_hh).T
    ih = _bn(ih, f64(g_ih), f64(b_ih))
    hh = _bn(hh, f64(g_hh), f64(b_hh))
    gates = ih + hh + f64(b)
    f, i, o, g = np.split(gates, 4, axis=1)
    f = sigmoid(f)
    i = sigmoid(i)
    o = sigmoid(o)
    g = np.tanh(g)
    c_next = f * f64(c) + i * g
    c_next = _bn(c_next, f64(g_c), f64(b_c))
    h_next = o * np.tanh(c_next)
    return (c_next, h_next)

@@ -1,0 +1,485 @@
+from contextlib import ExitStack
+
+import concourse.mybir as mybir
+from concourse.masks import make_identity
+
+F32 = mybir.dt.float32
+BF16 = mybir.dt.bfloat16
+U32 = mybir.dt.uint32
+U8 = mybir.dt.uint8
+FP8X4 = mybir.dt.float8_e4m3fn_x4
+ACT = mybir.ActivationFunctionType
+ALU = mybir.AluOpType
+AX = mybir.AxisListType
+
+P = 128
+B, I, H = 8192, 512, 128
+NB = 4
+TILES = B // P
+TPC = 4
+CH = TILES // TPC
+CW = TPC * P
+EPS = 1e-5
+DIRECT = 2
+HG = 16
+HPAD = 144
+GW = P + 2
+OLAG = 6
+CFILL = 8
+FLOPS = 2 * B * I * NB * H + 2 * B * H * NB * H
+
+
+def tile_lstmcell_t_kernel(
+    tc, x, c, h, w_ih, w_hh, b, g_ih, b_ih, g_hh, b_hh, g_c, b_c, out_0, out_1
+):
+    nc = tc.nc
+    xv = x.rearrange("(p s) k -> p s k", s=TILES)
+    cv = c.rearrange("(p s) k -> p s k", s=TILES)
+    hv = h.rearrange("(p s) k -> p s k", s=TILES)
+    outv = (
+        out_0.rearrange("(p s) k -> p s k", s=TILES),
+        out_1.rearrange("(p s) k -> p s k", s=TILES),
+    )
+    with ExitStack() as ctx:
+        ctx.enter_context(tc.manual_schedule())
+        keep = ctx.enter_context(tc.tile_pool(name="keep", bufs=1))
+        psum = ctx.enter_context(tc.psum_pool(name="psum", bufs=1))
+        cpool = ctx.enter_context(tc.tile_pool(name="cpool", bufs=2))
+
+        gate = [keep.tile([P, B], F32, name="gate%d" % jb) for jb in range(NB)]
+        hT = keep.tile([P, B], BF16)
+        hh01 = keep.tile([P, NB, DIRECT, CW], F32)
+        h_nat = [keep.tile([P, HG, HPAD], BF16, name="h_nat%d" % g) for g in range(TILES // HG)]
+        w_codes = keep.tile([P, NB * P], U32, align_bytes=64)
+        w_scales = keep.tile([P, NB * P], U8, align_bytes=64)
+        whh_nat = keep.tile([P, NB, H], BF16)
+        whhT_b = keep.tile([P, NB * P], BF16)
+        whhT_f = keep.tile([P, NB * P], F32)
+        ident_f = keep.tile([P, P], F32)
+        ident_b = keep.tile([P, P], BF16)
+        rows = keep.tile([P, P], BF16)
+        par = keep.tile([P, 24], F32)
+        gs = keep.tile([P, GW], F32)
+        st_ih = keep.tile([P, NB, CH, 6], F32)
+        hsum = keep.tile([P, DIRECT], F32)
+        sq01 = keep.tile([P, DIRECT, NB], F32)
+        csum = keep.tile([P, CH], F32)
+        csq = keep.tile([P, CH], F32)
+        junk = keep.tile([P, CW], BF16)
+        prod = keep.tile([P, P], F32)
+        neghalf = keep.tile([P, NB], F32)
+        warm = keep.tile([P, 1], F32)
+        mv = keep.tile([P, NB, 2], F32)
+
+        def small(name, width=NB):
+            return keep.tile([P, width], F32, name=name)
+
+        def cols(ci):
+            return slice(ci * CW, (ci + 1) * CW)
+
+        def blk(jb):
+            return slice(jb * P, (jb + 1) * P)
+
+        def htile(ci, t):
+            s = ci * TPC + t
+            return h_nat[s // HG][:, s % HG, :]
+
+        def transpose_bf16(tag, tiles):
+            bank = psum.tile([P, CW], BF16, tag=tag, name="bt")
+            for t, src in enumerate(tiles):
+                nc.tensor.transpose(bank[:, t * P : (t + 1) * P], src, ident_b[:])
+            return bank
+
+        def hh_matmul(ci, jb):
+            acc = psum.tile([P, CW], F32, tag="m%d" % jb, name="acc")
+            nc.tensor.matmul(out=acc[:], lhsT=whhT_b[:, blk(jb)], rhs=hT[:, cols(ci)], start=True, stop=True)
+            return acc
+
+        nc.vector.memset(warm[:], 0.0)
+        nc.scalar.activation(out=warm[:], in_=warm[:], func=ACT.Sigmoid)
+        make_identity(nc, ident_f[:])
+        make_identity(nc, ident_b[:])
+        nc.vector.memset(rows[:], 0.0)
+        nc.vector.memset(neghalf[:], -0.5)
+        for g in range(TILES // HG):
+            nc.vector.memset(h_nat[g][:, :, H:HPAD], 1.0)
+
+        with tc.tile_pool(name="stage", bufs=2) as stage:
+            x_sb = {}
+            banks = {}
+            grp = {}
+            codes = {}
+            scales = {}
+            acc_ih = {}
+
+            def load_x(ci):
+                x_sb[ci] = stage.tile([P, TPC, I], BF16, tag="xs", bufs=4, name="x_sb")
+                nc.sync.dma_start(out=x_sb[ci][:], in_=xv[:, ci * TPC : (ci + 1) * TPC, :])
+
+            def load_h(g):
+                nc.sync.dma_start(out=h_nat[g][:, :, 0:H], in_=hv[:, g * HG : (g + 1) * HG, :])
+
+            def t1(key, src, tags=("ta", "tb")):
+                pair = []
+                for half, tag in enumerate(tags):
+                    xt = psum.tile([P, 2, 2 * P], F32, tag=tag, name="xt")
+                    for a in range(2):
+                        sw = src[:, 2 * half + a, :].bitcast(F32)
+                        for u in range(2):
+                            nc.tensor.transpose(
+                                xt[:, u, a * P : (a + 1) * P], sw[:, u : 2 * P : 2], ident_f[:]
+                            )
+                    pair.append(xt)
+                banks[key] = pair
+
+            def new_grp(key):
+                grp[key] = stage.tile([P, 4 * CW], BF16, tag="grp", bufs=2, align_bytes=64, name="grp")
+
+            def evac(key, half, on_scalar):
+                words = grp[key][:].bitcast(F32).rearrange("p (r u) -> p r u", u=2)
+                dst = words[:, half * 2 * P : (half + 1) * 2 * P, :]
+                src = banks[key][half][:].rearrange("p u r -> p r u")
+                if on_scalar:
+                    nc.scalar.copy(out=dst, in_=src)
+                else:
+                    nc.vector.tensor_copy(out=dst, in_=src)
+
+            def quant(key):
+                codes[key] = stage.tile([P, CW], U32, tag="codes", bufs=2, align_bytes=64, name="codes")
+                scales[key] = stage.tile([P, CW], U8, tag="scales", bufs=2, align_bytes=64, name="scales")
+                nc.vector.quantize_mx(
+                    out=codes[key][:].bitcast(FP8X4), scales=scales[key][:], in_=grp[key][:]
+                )
+
+            def mx(ci):
+                acc_ih[ci] = []
+                for jb in range(NB):
+                    acc = psum.tile([P, CW], F32, tag="m%d" % jb, name="acc")
+                    nc.tensor.matmul_mx(
+                        out=acc[:],
+                        lhsT=w_codes[:, blk(jb)].bitcast(FP8X4),
+                        lhsT_scale=w_scales[:, blk(jb)],
+                        rhs=codes[ci][:].bitcast(FP8X4),
+                        rhs_scale=scales[ci][:],
+                        start=True,
+                        stop=True,
+                    )
+                    acc_ih[ci].append(acc)
+
+            def copy_ih(ci):
+                for jb in range(NB):
+                    nc.scalar.copy(out=gate[jb][:, cols(ci)], in_=acc_ih[ci][jb][:])
+
+            def stat_ih(ci, jb):
+                nc.vector.bn_stats(out=st_ih[:, jb, ci, :], in_=gate[jb][:, cols(ci)])
+
+            def v_takes_half(ci):
+                return ci % 4 == 1
+
+            w_sb = stage.tile([P, NB, I], BF16, tag="xs", bufs=4, name="w_sb")
+            nc.sync.dma_start(out=w_sb[:], in_=w_ih.rearrange("(jb m) k -> m jb k", m=P))
+            load_x(0)
+            load_x(1)
+            load_x(2)
+            for v, vec in enumerate((b, g_ih, b_ih, g_hh, b_hh)):
+                nc.scalar.dma_start(
+                    out=rows[NB * v : NB * (v + 1), :], in_=vec.rearrange("(r m) -> r m", m=P)
+                )
+            nc.scalar.dma_start(out=rows[20:21, :], in_=g_c.rearrange("(r m) -> r m", m=P))
+            nc.scalar.dma_start(out=rows[21:22, :], in_=b_c.rearrange("(r m) -> r m", m=P))
+            nc.sync.dma_start(out=whh_nat[:], in_=w_hh.rearrange("(jb m) k -> m jb k", m=P))
+
+            t1("w", w_sb)
+            load_x(3)
+            load_h(0)
+            t1(0, x_sb[0], ("th", "g"))
+            load_x(4)
+            new_grp("w")
+            evac("w", 0, True)
+            evac("w", 1, False)
+            nc.vector.quantize_mx(out=w_codes[:].bitcast(FP8X4), scales=w_scales[:], in_=grp["w"][:])
+            new_grp(0)
+            evac(0, 0, True)
+            evac(0, 1, False)
+            quant(0)
+            t1(1, x_sb[1])
+            load_x(5)
+            mx(0)
+
+            c_nat = {}
+
+            def load_c(cg):
+                c_nat[cg] = cpool.tile([P, HG, H], BF16, tag="cn", bufs=2, name="c_nat")
+                nc.sync.dma_start(out=c_nat[cg][:], in_=cv[:, cg * HG : (cg + 1) * HG, :])
+
+            gram = None
+            for ci in range(CH):
+                nxt = ci + 1
+                if nxt < CH:
+                    new_grp(nxt)
+                    evac(nxt, 0, True)
+                    if not v_takes_half(nxt):
+                        evac(nxt, 1, True)
+                if ci >= 1:
+                    for jb in range(3):
+                        stat_ih(ci - 1, jb)
+                if nxt < CH and v_takes_half(nxt):
+                    evac(nxt, 1, False)
+                if ci >= 1:
+                    stat_ih(ci - 1, 3)
+                if nxt < CH:
+                    quant(nxt)
+                if ci + 2 < CH:
+                    t1(ci + 2, x_sb[ci + 2])
+                    if ci + 6 < CH:
+                        load_x(ci + 6)
+                if ci in (0, 2, 4):
+                    load_h(ci // 2 + 1)
+                if ci in (8, 9):
+                    load_c(ci - 8)
+                if ci == 0:
+                    wt = transpose_bf16("g", [whh_nat[:, jb, :] for jb in range(NB)])
+                    nc.vector.tensor_copy(out=whhT_b[:], in_=wt[:])
+                    nc.vector.tensor_copy(out=whhT_f[:], in_=wt[:])
+                    pt = psum.tile([P, P], BF16, tag="th", name="pt")
+                    nc.tensor.transpose(pt[:], rows[:], ident_b[:])
+                    nc.vector.tensor_copy(out=par[:], in_=pt[:, 0:24])
+                copy_ih(ci)
+                if ci == 1:
+                    for q, tag in enumerate(("th", "g")):
+                        ht = transpose_bf16(tag, [htile(q, t)[:, 0:H] for t in range(TPC)])
+                        nc.scalar.activation(
+                            out=hT[:, cols(q)], in_=ht[:], func=ACT.Copy, accum_out=hsum[:, q : q + 1]
+                        )
+                if 3 <= ci <= 9:
+                    if ci == 3:
+                        gram = psum.tile([P, GW], F32, tag="g", name="gram")
+                    for q in (2 * ci - 4, 2 * ci - 3):
+                        for t in range(TPC):
+                            nc.tensor.matmul(
+                                out=gram[:],
+                                lhsT=htile(q, t)[:, 0:H],
+                                rhs=htile(q, t)[:, 0:GW],
+                                start=(q == DIRECT and t == 0),
+                                stop=(q == CH - 1 and t == TPC - 1),
+                            )
+                if ci in (2, 5):
+                    q = (ci - 2) // 3
+                    for jb in range(NB):
+                        acc = hh_matmul(q, jb)
+                        nc.vector.tensor_copy(out=hh01[:, jb, q, :], in_=acc[:])
+                        nc.scalar.activation(
+                            out=junk[:], in_=acc[:], func=ACT.Square, accum_out=sq01[:, q, jb : jb + 1]
+                        )
+                if nxt < CH:
+                    mx(nxt)
+                if ci == 10:
+                    nc.vector.tensor_copy(out=gs[:], in_=gram[:])
+                    for q in range(DIRECT):
+                        nc.vector.tensor_tensor(
+                            out=gs[:, P : P + 1], in0=gs[:, P : P + 1], in1=hsum[:, q : q + 1], op=ALU.add
+                        )
+                    ys = []
+                    for pair, tag in enumerate(("th", "g")):
+                        y = psum.tile([P, 2, GW], F32, tag=tag, name="y")
+                        for a in range(2):
+                            nc.tensor.matmul(
+                                out=y[:, a, :], lhsT=whhT_f[:, blk(2 * pair + a)], rhs=gs[:],
+                                start=True, stop=True,
+                            )
+                        ys.append(y)
+                if ci == 11:
+                    t2 = small("t2")
+                    s1 = small("s1")
+                    for jb in range(NB):
+                        y = ys[jb // 2]
+                        a = jb % 2
+                        nc.vector.tensor_tensor(
+                            out=prod[:], in0=y[:, a, 0:P], in1=whh_nat[:, jb, :], op=ALU.mult
+                        )
+                        nc.vector.reduce_sum(out=t2[:, jb : jb + 1], in_=prod[:], axis=AX.X)
+                        nc.vector.tensor_copy(out=s1[:, jb : jb + 1], in_=y[:, a, P : P + 1])
+                    for q in range(DIRECT):
+                        nc.vector.tensor_tensor(out=t2[:], in0=t2[:], in1=sq01[:, q, :], op=ALU.add)
+                    bsum = small("bsum")
+                    nc.vector.tensor_tensor(out=bsum[:], in0=par[:, 0:4], in1=par[:, 8:12], op=ALU.add)
+                    nc.vector.tensor_tensor(out=bsum[:], in0=bsum[:], in1=par[:, 16:20], op=ALU.add)
+                    mean_hh = small("mean_hh")
+                    nc.vector.tensor_scalar(
+                        out=mean_hh[:], in0=s1[:], scalar1=1.0 / B, scalar2=None, op0=ALU.mult
+                    )
+                    msq = small("msq")
+                    nc.vector.tensor_tensor(out=msq[:], in0=mean_hh[:], in1=mean_hh[:], op=ALU.mult)
+                    var_hh = small("var_hh")
+                    nc.vector.scalar_tensor_tensor(
+                        out=var_hh[:], in0=t2[:], scalar=1.0 / B, in1=msq[:], op0=ALU.mult, op1=ALU.subtract
+                    )
+                    nc.vector.tensor_scalar(
+                        out=var_hh[:], in0=var_hh[:], scalar1=0.0, scalar2=EPS, op0=ALU.max, op1=ALU.add
+                    )
+                    rstd_hh = small("rstd_hh")
+                    nc.gpsimd.tensor_tensor(out=rstd_hh[:], in0=var_hh[:], in1=neghalf[:], op=ALU.pow)
+                if ci == 12:
+                    a_hh = small("a_hh")
+                    nc.vector.tensor_tensor(out=a_hh[:], in0=par[:, 12:16], in1=rstd_hh[:], op=ALU.mult)
+                    cst = small("cst")
+                    nc.vector.tensor_tensor(out=cst[:], in0=a_hh[:], in1=mean_hh[:], op=ALU.mult)
+                    nc.vector.tensor_tensor(out=cst[:], in0=bsum[:], in1=cst[:], op=ALU.subtract)
+
+        late = ctx.enter_context(tc.tile_pool(name="late", bufs=3))
+        cT = late.tile([P, B], BF16, tag="cT", bufs=1, name="cT")
+        for jb in range(NB):
+            nc.vector.bn_stats(out=st_ih[:, jb, CH - 1, :], in_=gate[jb][:, cols(CH - 1)])
+        for jb in range(NB):
+            nc.vector.bn_aggr(out=mv[:, jb, :], in_=st_ih[:, jb, :, :].rearrange("p c s -> p (c s)"))
+        ve_ih = small("ve_ih")
+        nc.vector.tensor_scalar(out=ve_ih[:], in0=mv[:, :, 1], scalar1=EPS, scalar2=None, op0=ALU.add)
+        rstd_ih = small("rstd_ih")
+        nc.gpsimd.tensor_tensor(out=rstd_ih[:], in0=ve_ih[:], in1=neghalf[:], op=ALU.pow)
+        a_ih = small("a_ih")
+        nc.vector.tensor_tensor(out=a_ih[:], in0=par[:, 4:8], in1=rstd_ih[:], op=ALU.mult)
+        zfix = small("zfix")
+        nc.vector.tensor_scalar(
+            out=zfix[:], in0=a_ih[:], scalar1=0.0, scalar2=1e-30, op0=ALU.is_equal, op1=ALU.mult
+        )
+        sc = small("sc")
+        nc.vector.tensor_tensor(out=sc[:], in0=a_ih[:], in1=zfix[:], op=ALU.add)
+        ratio = small("ratio")
+        nc.vector.reciprocal(out=ratio[:], in_=sc[:])
+        nc.vector.tensor_tensor(out=ratio[:], in0=ratio[:], in1=a_hh[:], op=ALU.mult)
+        am = small("am")
+        nc.vector.tensor_tensor(out=am[:], in0=a_ih[:], in1=mv[:, :, 0], op=ALU.mult)
+        nc.vector.tensor_tensor(out=cst[:], in0=cst[:], in1=am[:], op=ALU.subtract)
+
+        def c_transposed(q, tag):
+            ct = transpose_bf16(tag, [c_nat[q // TPC][:, (q % TPC) * TPC + t, :] for t in range(TPC)])
+            nc.scalar.copy(out=cT[:, cols(q)], in_=ct[:])
+
+        fill_tags = ("ta", "tb", "th", "g")
+        n_fill = 0
+        for q in range(DIRECT, CH):
+            ht = transpose_bf16(fill_tags[n_fill % 4], [htile(q, t)[:, 0:H] for t in range(TPC)])
+            nc.scalar.copy(out=hT[:, cols(q)], in_=ht[:])
+            n_fill += 1
+            if q - DIRECT < CFILL:
+                c_transposed(q - DIRECT, fill_tags[n_fill % 4])
+                n_fill += 1
+        load_c(2)
+        load_c(3)
+
+        negm0 = small("negm0", 1)
+
+        def gate_block(ci, jb):
+            if ci < DIRECT:
+                hh = hh01[:, jb, ci, :]
+            else:
+                hh = hh_matmul(ci, jb)[:]
+            nc.vector.scalar_tensor_tensor(
+                out=gate[jb][:, cols(ci)], in0=hh, scalar=ratio[:, jb : jb + 1], in1=gate[jb][:, cols(ci)],
+                op0=ALU.mult, op1=ALU.add,
+            )
+            nc.scalar.activation(
+                out=gate[jb][:, cols(ci)], in_=gate[jb][:, cols(ci)],
+                func=(ACT.Tanh if jb == 3 else ACT.Sigmoid),
+                scale=sc[:, jb : jb + 1], bias=cst[:, jb : jb + 1],
+            )
+
+        def cell_add(ci):
+            nc.vector.scalar_tensor_tensor(
+                out=gate[0][:, cols(ci)], in0=gate[0][:, cols(ci)], scalar=1.0, in1=gate[1][:, cols(ci)],
+                op0=ALU.mult, op1=ALU.add, accum_out=csum[:, ci : ci + 1],
+            )
+            if ci == 0:
+                nc.vector.tensor_scalar(
+                    out=negm0[:], in0=csum[:, 0:1], scalar1=-1.0 / CW, scalar2=None, op0=ALU.mult
+                )
+
+        def cell_square(ci):
+            nc.scalar.activation(
+                out=junk[:], in_=gate[0][:, cols(ci)], func=ACT.Square, bias=negm0[:], scale=1.0,
+                accum_out=csq[:, ci : ci + 1],
+            )
+
+        for ci in range(CH):
+            for jb in (0, 1, 3):
+                gate_block(ci, jb)
+            nc.gpsimd.tensor_tensor(
+                out=gate[0][:, cols(ci)], in0=gate[0][:, cols(ci)], in1=cT[:, cols(ci)], op=ALU.mult
+            )
+            nc.gpsimd.tensor_tensor(
+                out=gate[1][:, cols(ci)], in0=gate[1][:, cols(ci)], in1=gate[3][:, cols(ci)], op=ALU.mult
+            )
+            if ci >= OLAG:
+                gate_block(ci - OLAG, 2)
+            if ci >= 2:
+                cell_add(ci - 2)
+            if ci >= 3:
+                cell_square(ci - 3)
+            if ci < CH - CFILL:
+                c_transposed(ci + CFILL, ("ta", "tb")[ci % 2])
+
+        gate_block(CH - 6, 2)
+        cell_add(CH - 2)
+        cell_square(CH - 3)
+        gate_block(CH - 5, 2)
+        gate_block(CH - 4, 2)
+        cell_add(CH - 1)
+        cell_square(CH - 2)
+        cell_square(CH - 1)
+        gate_block(CH - 3, 2)
+        s1c = small("s1c", 1)
+        nc.vector.reduce_sum(out=s1c[:], in_=csum[:], axis=AX.X)
+        mean_c = small("mean_c", 1)
+        nc.vector.tensor_scalar(out=mean_c[:], in0=s1c[:], scalar1=1.0 / B, scalar2=None, op0=ALU.mult)
+        dlt = small("dlt", 1)
+        nc.vector.tensor_tensor(out=dlt[:], in0=mean_c[:], in1=negm0[:], op=ALU.add)
+        nc.vector.tensor_tensor(out=dlt[:], in0=dlt[:], in1=dlt[:], op=ALU.mult)
+        s2c = small("s2c", 1)
+        nc.vector.reduce_sum(out=s2c[:], in_=csq[:], axis=AX.X)
+        ve_c = small("ve_c", 1)
+        nc.vector.scalar_tensor_tensor(
+            out=ve_c[:], in0=s2c[:], scalar=1.0 / B, in1=dlt[:], op0=ALU.mult, op1=ALU.subtract
+        )
+        nc.vector.tensor_scalar(out=ve_c[:], in0=ve_c[:], scalar1=0.0, scalar2=EPS, op0=ALU.max, op1=ALU.add)
+        rstd_c = small("rstd_c", 1)
+        nc.gpsimd.tensor_tensor(out=rstd_c[:], in0=ve_c[:], in1=neghalf[:, 0:1], op=ALU.pow)
+        gate_block(CH - 2, 2)
+        gate_block(CH - 1, 2)
+        a_c = small("a_c", 1)
+        nc.vector.tensor_tensor(out=a_c[:], in0=par[:, 20:21], in1=rstd_c[:], op=ALU.mult)
+        k_c = small("k_c", 1)
+        nc.vector.tensor_tensor(out=k_c[:], in0=a_c[:], in1=mean_c[:], op=ALU.mult)
+        nc.vector.tensor_tensor(out=k_c[:], in0=par[:, 21:22], in1=k_c[:], op=ALU.subtract)
+
+        out_tags = (("ta", "m0", "m2", "g"), ("tb", "m1", "m3", "th"))
+        out_banks = {}
+        LAG = 2
+        for ci in range(CH + LAG):
+            if ci < CH:
+                nc.gpsimd.tensor_scalar(
+                    out=gate[1][:, cols(ci)], in0=gate[0][:, cols(ci)], scalar1=a_c[:], scalar2=k_c[:],
+                    op0=ALU.mult, op1=ALU.add,
+                )
+                nc.scalar.activation(
+                    out=gate[3][:, cols(ci)], in_=gate[0][:, cols(ci)], func=ACT.Tanh,
+                    scale=a_c[:], bias=k_c[:],
+                )
+                nc.vector.tensor_tensor(
+                    out=gate[2][:, cols(ci)], in0=gate[2][:, cols(ci)], in1=gate[3][:, cols(ci)], op=ALU.mult
+                )
+                for o, src in enumerate((gate[1], gate[2])):
+                    ot = psum.tile([P, TPC, P], F32, tag=out_tags[o][ci % 4], name="ot")
+                    for t in range(TPC):
+                        nc.tensor.transpose(
+                            ot[:, t, :], src[:, ci * CW + t * P : ci * CW + (t + 1) * P], ident_f[:]
+                        )
+                    out_banks[(ci, o)] = ot
+            cj = ci - LAG
+            if cj >= 0:
+                for o in range(2):
+                    ob = late.tile([P, TPC, P], F32, tag="ob%d" % o, bufs=3, name="ob")
+                    if o == 0:
+                        nc.scalar.copy(out=ob[:], in_=out_banks[(cj, o)][:])
+                    else:
+                        nc.vector.tensor_copy(out=ob[:], in_=out_banks[(cj, o)][:])
+                    nc.sync.dma_start(out=outv[o][:, cj * TPC : (cj + 1) * TPC, :], in_=ob[:])

@@ -26,6 +26,8 @@ HPAD = 144
 GW = P + 2
 OLAG = 6
 CFILL = 8
+GCH = 12
+JB_ORDER = (0, 3, 1, 2)
 FLOPS = 2 * B * I * NB * H + 2 * B * H * NB * H
 
 
@@ -60,13 +62,17 @@ def tile_lstmcell_t_kernel(
         rows = keep.tile([P, P], BF16)
         par = keep.tile([P, 24], F32)
         gs = keep.tile([P, GW], F32)
-        st_ih = keep.tile([P, NB, CH, 6], F32)
+        st_ih = keep.tile([P, NB - 1, CH, 6], F32)
+        st_g = keep.tile([P, 1 + CH - GCH, 6], F32)
+        gsum = keep.tile([P, GCH], F32)
+        gacc = keep.tile([P, CW], F32)
+        gred = keep.tile([P, 4], F32)
         hsum = keep.tile([P, DIRECT], F32)
         sq01 = keep.tile([P, DIRECT, NB], F32)
         csum = keep.tile([P, CH], F32)
         csq = keep.tile([P, CH], F32)
         junk = keep.tile([P, CW], BF16)
-        prod = keep.tile([P, P], F32)
+        prod = keep.tile([P, NB, P], F32)
         neghalf = keep.tile([P, NB], F32)
         warm = keep.tile([P, 1], F32)
         mv = keep.tile([P, NB, 2], F32)
@@ -90,8 +96,8 @@ def tile_lstmcell_t_kernel(
                 nc.tensor.transpose(bank[:, t * P : (t + 1) * P], src, ident_b[:])
             return bank
 
-        def hh_matmul(ci, jb):
-            acc = psum.tile([P, CW], F32, tag="m%d" % jb, name="acc")
+        def hh_matmul(ci, jb, tag):
+            acc = psum.tile([P, CW], F32, tag=tag, name="acc")
             nc.tensor.matmul(out=acc[:], lhsT=whhT_b[:, blk(jb)], rhs=hT[:, cols(ci)], start=True, stop=True)
             return acc
 
@@ -101,6 +107,7 @@ def tile_lstmcell_t_kernel(
         make_identity(nc, ident_b[:])
         nc.vector.memset(rows[:], 0.0)
         nc.vector.memset(neghalf[:], -0.5)
+        nc.vector.memset(st_g[:, 0, :], 0.5 * GCH * CW)
         for g in range(TILES // HG):
             nc.vector.memset(h_nat[g][:, :, H:HPAD], 1.0)
 
@@ -152,8 +159,8 @@ def tile_lstmcell_t_kernel(
                 )
 
             def mx(ci):
-                acc_ih[ci] = []
-                for jb in range(NB):
+                acc_ih[ci] = {}
+                for jb in JB_ORDER:
                     acc = psum.tile([P, CW], F32, tag="m%d" % jb, name="acc")
                     nc.tensor.matmul_mx(
                         out=acc[:],
@@ -164,29 +171,58 @@ def tile_lstmcell_t_kernel(
                         start=True,
                         stop=True,
                     )
-                    acc_ih[ci].append(acc)
+                    acc_ih[ci][jb] = acc
 
             def copy_ih(ci):
-                for jb in range(NB):
-                    nc.scalar.copy(out=gate[jb][:, cols(ci)], in_=acc_ih[ci][jb][:])
+                for jb in JB_ORDER:
+                    if jb == 3 and ci < GCH:
+                        nc.scalar.activation(
+                            out=gate[jb][:, cols(ci)], in_=acc_ih[ci][jb][:], func=ACT.Copy,
+                            accum_out=gsum[:, ci : ci + 1],
+                        )
+                    else:
+                        nc.scalar.copy(out=gate[jb][:, cols(ci)], in_=acc_ih[ci][jb][:])
 
             def stat_ih(ci, jb):
-                nc.vector.bn_stats(out=st_ih[:, jb, ci, :], in_=gate[jb][:, cols(ci)])
+                if jb < 3:
+                    nc.vector.bn_stats(out=st_ih[:, jb, ci, :], in_=gate[jb][:, cols(ci)])
+                elif ci >= GCH:
+                    nc.vector.bn_stats(out=st_g[:, 1 + ci - GCH, :], in_=gate[jb][:, cols(ci)])
+                else:
+                    src = gate[jb][:, cols(ci)]
+                    if ci == 0:
+                        nc.gpsimd.tensor_tensor(out=gacc[:], in0=src, in1=src, op=ALU.mult)
+                    else:
+                        sq = stage.tile([P, CW], F32, tag="gsq", bufs=2, name="gsq")
+                        nc.gpsimd.tensor_tensor(out=sq[:], in0=src, in1=src, op=ALU.mult)
+                        nc.gpsimd.tensor_tensor(out=gacc[:], in0=gacc[:], in1=sq[:], op=ALU.add)
 
-            def v_takes_half(ci):
-                return ci % 4 == 1
+            def stat_g_tuple():
+                n = GCH * CW
+                nc.vector.reduce_sum(out=gred[:, 0:1], in_=gsum[:], axis=AX.X)
+                nc.vector.reduce_sum(out=gred[:, 1:2], in_=gacc[:], axis=AX.X)
+                for col in (1, 4):
+                    nc.vector.tensor_scalar(
+                        out=st_g[:, 0, col : col + 1], in0=gred[:, 0:1], scalar1=1.0 / n, scalar2=None, op0=ALU.mult
+                    )
+                nc.vector.tensor_tensor(out=gred[:, 2:3], in0=gred[:, 0:1], in1=st_g[:, 0, 1:2], op=ALU.mult)
+                nc.vector.tensor_tensor(out=gred[:, 3:4], in0=gred[:, 1:2], in1=gred[:, 2:3], op=ALU.subtract)
+                for col in (2, 5):
+                    nc.vector.tensor_scalar(
+                        out=st_g[:, 0, col : col + 1], in0=gred[:, 3:4], scalar1=0.5, scalar2=None, op0=ALU.mult
+                    )
 
             w_sb = stage.tile([P, NB, I], BF16, tag="xs", bufs=4, name="w_sb")
             nc.sync.dma_start(out=w_sb[:], in_=w_ih.rearrange("(jb m) k -> m jb k", m=P))
             load_x(0)
             load_x(1)
-            load_x(2)
             for v, vec in enumerate((b, g_ih, b_ih, g_hh, b_hh)):
-                nc.scalar.dma_start(
+                nc.sync.dma_start(
                     out=rows[NB * v : NB * (v + 1), :], in_=vec.rearrange("(r m) -> r m", m=P)
                 )
-            nc.scalar.dma_start(out=rows[20:21, :], in_=g_c.rearrange("(r m) -> r m", m=P))
-            nc.scalar.dma_start(out=rows[21:22, :], in_=b_c.rearrange("(r m) -> r m", m=P))
+            nc.sync.dma_start(out=rows[20:21, :], in_=g_c.rearrange("(r m) -> r m", m=P))
+            nc.sync.dma_start(out=rows[21:22, :], in_=b_c.rearrange("(r m) -> r m", m=P))
+            load_x(2)
             nc.sync.dma_start(out=whh_nat[:], in_=w_hh.rearrange("(jb m) k -> m jb k", m=P))
 
             t1("w", w_sb)
@@ -212,23 +248,69 @@ def tile_lstmcell_t_kernel(
                 c_nat[cg] = cpool.tile([P, HG, H], BF16, tag="cn", bufs=2, name="c_nat")
                 nc.sync.dma_start(out=c_nat[cg][:], in_=cv[:, cg * HG : (cg + 1) * HG, :])
 
+            t2 = small("t2")
+            s1 = small("s1")
+            bsum = small("bsum")
+            mean_hh = small("mean_hh")
+            msq = small("msq")
+            var_hh = small("var_hh")
+            rstd_hh = small("rstd_hh")
+            a_hh = small("a_hh")
+            zfix = small("zfix")
+            sc = small("sc")
+            ratio = small("ratio")
+            cst = small("cst")
+
+            def hh_small_ops():
+                def tt(out, in0, in1, op):
+                    return lambda: nc.vector.tensor_tensor(out=out, in0=in0, in1=in1, op=op)
+
+                return [
+                    tt(t2[:], t2[:], sq01[:, 0, :], ALU.add),
+                    lambda: nc.vector.tensor_scalar(
+                        out=mean_hh[:], in0=s1[:], scalar1=1.0 / B, scalar2=None, op0=ALU.mult
+                    ),
+                    tt(bsum[:], par[:, 0:4], par[:, 8:12], ALU.add),
+                    tt(t2[:], t2[:], sq01[:, 1, :], ALU.add),
+                    tt(msq[:], mean_hh[:], mean_hh[:], ALU.mult),
+                    tt(bsum[:], bsum[:], par[:, 16:20], ALU.add),
+                    lambda: nc.vector.scalar_tensor_tensor(
+                        out=var_hh[:], in0=t2[:], scalar=1.0 / B, in1=msq[:], op0=ALU.mult, op1=ALU.subtract
+                    ),
+                    lambda: nc.vector.tensor_scalar(
+                        out=var_hh[:], in0=var_hh[:], scalar1=0.0, scalar2=EPS, op0=ALU.max, op1=ALU.add
+                    ),
+                    lambda: nc.gpsimd.tensor_tensor(out=rstd_hh[:], in0=var_hh[:], in1=neghalf[:], op=ALU.pow),
+                ]
+
             gram = None
+            smalls = []
+
+            def few_smalls(ci):
+                for op in smalls[:3]:
+                    op()
+                smalls[:] = smalls[3:]
+
             for ci in range(CH):
                 nxt = ci + 1
                 if nxt < CH:
                     new_grp(nxt)
                     evac(nxt, 0, True)
-                    if not v_takes_half(nxt):
-                        evac(nxt, 1, True)
-                if ci >= 1:
-                    for jb in range(3):
-                        stat_ih(ci - 1, jb)
-                if nxt < CH and v_takes_half(nxt):
                     evac(nxt, 1, False)
                 if ci >= 1:
-                    stat_ih(ci - 1, 3)
+                    stat_ih(ci - 1, 0)
+                    few_smalls(ci)
                 if nxt < CH:
                     quant(nxt)
+                direct = 2 <= ci < 2 + DIRECT * NB
+                if direct:
+                    dq, djb = divmod(ci - 2, NB)
+                    dacc = hh_matmul(dq, djb, "th")
+                    nc.vector.tensor_copy(out=hh01[:, djb, dq, :], in_=dacc[:])
+                if ci >= 1:
+                    for jb in range(1, NB):
+                        stat_ih(ci - 1, jb)
+                        few_smalls(ci)
                 if ci + 2 < CH:
                     t1(ci + 2, x_sb[ci + 2])
                     if ci + 6 < CH:
@@ -244,6 +326,17 @@ def tile_lstmcell_t_kernel(
                     pt = psum.tile([P, P], BF16, tag="th", name="pt")
                     nc.tensor.transpose(pt[:], rows[:], ident_b[:])
                     nc.vector.tensor_copy(out=par[:], in_=pt[:, 0:24])
+                if ci == CH - 1:
+                    nc.vector.tensor_tensor(out=a_hh[:], in0=par[:, 12:16], in1=rstd_hh[:], op=ALU.mult)
+                    nc.vector.tensor_scalar(
+                        out=zfix[:], in0=a_hh[:], scalar1=0.0, scalar2=1e-30, op0=ALU.is_equal, op1=ALU.mult
+                    )
+                    nc.vector.tensor_tensor(out=cst[:], in0=a_hh[:], in1=mean_hh[:], op=ALU.mult)
+                    nc.vector.tensor_tensor(out=sc[:], in0=a_hh[:], in1=zfix[:], op=ALU.add)
+                    nc.vector.tensor_tensor(out=cst[:], in0=bsum[:], in1=cst[:], op=ALU.subtract)
+                    nc.vector.reciprocal(out=ratio[:], in_=sc[:])
+                    stat_g_tuple()
+                    nc.vector.tensor_tensor(out=ratio[:], in0=ratio[:], in1=par[:, 4:8], op=ALU.mult)
                 copy_ih(ci)
                 if ci == 1:
                     for q, tag in enumerate(("th", "g")):
@@ -263,22 +356,19 @@ def tile_lstmcell_t_kernel(
                                 start=(q == DIRECT and t == 0),
                                 stop=(q == CH - 1 and t == TPC - 1),
                             )
-                if ci in (2, 5):
-                    q = (ci - 2) // 3
-                    for jb in range(NB):
-                        acc = hh_matmul(q, jb)
-                        nc.vector.tensor_copy(out=hh01[:, jb, q, :], in_=acc[:])
-                        nc.scalar.activation(
-                            out=junk[:], in_=acc[:], func=ACT.Square, accum_out=sq01[:, q, jb : jb + 1]
-                        )
                 if nxt < CH:
                     mx(nxt)
+                if direct:
+                    nc.scalar.activation(
+                        out=junk[:], in_=dacc[:], func=ACT.Square, accum_out=sq01[:, dq, djb : djb + 1]
+                    )
                 if ci == 10:
                     nc.vector.tensor_copy(out=gs[:], in_=gram[:])
                     for q in range(DIRECT):
                         nc.vector.tensor_tensor(
                             out=gs[:, P : P + 1], in0=gs[:, P : P + 1], in1=hsum[:, q : q + 1], op=ALU.add
                         )
+                if ci == 11:
                     ys = []
                     for pair, tag in enumerate(("th", "g")):
                         y = psum.tile([P, 2, GW], F32, tag=tag, name="y")
@@ -288,68 +378,30 @@ def tile_lstmcell_t_kernel(
                                 start=True, stop=True,
                             )
                         ys.append(y)
-                if ci == 11:
-                    t2 = small("t2")
-                    s1 = small("s1")
-                    for jb in range(NB):
-                        y = ys[jb // 2]
-                        a = jb % 2
-                        nc.vector.tensor_tensor(
-                            out=prod[:], in0=y[:, a, 0:P], in1=whh_nat[:, jb, :], op=ALU.mult
-                        )
-                        nc.vector.reduce_sum(out=t2[:, jb : jb + 1], in_=prod[:], axis=AX.X)
-                        nc.vector.tensor_copy(out=s1[:, jb : jb + 1], in_=y[:, a, P : P + 1])
-                    for q in range(DIRECT):
-                        nc.vector.tensor_tensor(out=t2[:], in0=t2[:], in1=sq01[:, q, :], op=ALU.add)
-                    bsum = small("bsum")
-                    nc.vector.tensor_tensor(out=bsum[:], in0=par[:, 0:4], in1=par[:, 8:12], op=ALU.add)
-                    nc.vector.tensor_tensor(out=bsum[:], in0=bsum[:], in1=par[:, 16:20], op=ALU.add)
-                    mean_hh = small("mean_hh")
-                    nc.vector.tensor_scalar(
-                        out=mean_hh[:], in0=s1[:], scalar1=1.0 / B, scalar2=None, op0=ALU.mult
-                    )
-                    msq = small("msq")
-                    nc.vector.tensor_tensor(out=msq[:], in0=mean_hh[:], in1=mean_hh[:], op=ALU.mult)
-                    var_hh = small("var_hh")
-                    nc.vector.scalar_tensor_tensor(
-                        out=var_hh[:], in0=t2[:], scalar=1.0 / B, in1=msq[:], op0=ALU.mult, op1=ALU.subtract
-                    )
-                    nc.vector.tensor_scalar(
-                        out=var_hh[:], in0=var_hh[:], scalar1=0.0, scalar2=EPS, op0=ALU.max, op1=ALU.add
-                    )
-                    rstd_hh = small("rstd_hh")
-                    nc.gpsimd.tensor_tensor(out=rstd_hh[:], in0=var_hh[:], in1=neghalf[:], op=ALU.pow)
                 if ci == 12:
-                    a_hh = small("a_hh")
-                    nc.vector.tensor_tensor(out=a_hh[:], in0=par[:, 12:16], in1=rstd_hh[:], op=ALU.mult)
-                    cst = small("cst")
-                    nc.vector.tensor_tensor(out=cst[:], in0=a_hh[:], in1=mean_hh[:], op=ALU.mult)
-                    nc.vector.tensor_tensor(out=cst[:], in0=bsum[:], in1=cst[:], op=ALU.subtract)
+                    for pair in range(2):
+                        nc.vector.tensor_tensor(
+                            out=prod[:, 2 * pair : 2 * pair + 2, :], in0=ys[pair][:, :, 0:P],
+                            in1=whh_nat[:, 2 * pair : 2 * pair + 2, :], op=ALU.mult,
+                        )
+                        nc.vector.tensor_copy(out=s1[:, 2 * pair : 2 * pair + 2], in_=ys[pair][:, :, P])
+                    nc.vector.reduce_sum(out=t2[:], in_=prod[:], axis=AX.X)
+                    smalls.extend(hh_small_ops())
 
         late = ctx.enter_context(tc.tile_pool(name="late", bufs=3))
         cT = late.tile([P, B], BF16, tag="cT", bufs=1, name="cT")
         for jb in range(NB):
-            nc.vector.bn_stats(out=st_ih[:, jb, CH - 1, :], in_=gate[jb][:, cols(CH - 1)])
+            out = st_g[:, CH - GCH, :] if jb == 3 else st_ih[:, jb, CH - 1, :]
+            nc.vector.bn_stats(out=out, in_=gate[jb][:, cols(CH - 1)])
         for jb in range(NB):
-            nc.vector.bn_aggr(out=mv[:, jb, :], in_=st_ih[:, jb, :, :].rearrange("p c s -> p (c s)"))
+            tuples = st_g[:] if jb == 3 else st_ih[:, jb, :, :]
+            nc.vector.bn_aggr(out=mv[:, jb, :], in_=tuples.rearrange("p c s -> p (c s)"))
         ve_ih = small("ve_ih")
         nc.vector.tensor_scalar(out=ve_ih[:], in0=mv[:, :, 1], scalar1=EPS, scalar2=None, op0=ALU.add)
         rstd_ih = small("rstd_ih")
         nc.gpsimd.tensor_tensor(out=rstd_ih[:], in0=ve_ih[:], in1=neghalf[:], op=ALU.pow)
-        a_ih = small("a_ih")
-        nc.vector.tensor_tensor(out=a_ih[:], in0=par[:, 4:8], in1=rstd_ih[:], op=ALU.mult)
-        zfix = small("zfix")
-        nc.vector.tensor_scalar(
-            out=zfix[:], in0=a_ih[:], scalar1=0.0, scalar2=1e-30, op0=ALU.is_equal, op1=ALU.mult
-        )
-        sc = small("sc")
-        nc.vector.tensor_tensor(out=sc[:], in0=a_ih[:], in1=zfix[:], op=ALU.add)
-        ratio = small("ratio")
-        nc.vector.reciprocal(out=ratio[:], in_=sc[:])
-        nc.vector.tensor_tensor(out=ratio[:], in0=ratio[:], in1=a_hh[:], op=ALU.mult)
         am = small("am")
-        nc.vector.tensor_tensor(out=am[:], in0=a_ih[:], in1=mv[:, :, 0], op=ALU.mult)
-        nc.vector.tensor_tensor(out=cst[:], in0=cst[:], in1=am[:], op=ALU.subtract)
+        nc.vector.tensor_tensor(out=am[:], in0=par[:, 4:8], in1=mv[:, :, 0], op=ALU.mult)
 
         def c_transposed(q, tag):
             ct = transpose_bf16(tag, [c_nat[q // TPC][:, (q % TPC) * TPC + t, :] for t in range(TPC)])
@@ -359,7 +411,10 @@ def tile_lstmcell_t_kernel(
         n_fill = 0
         for q in range(DIRECT, CH):
             ht = transpose_bf16(fill_tags[n_fill % 4], [htile(q, t)[:, 0:H] for t in range(TPC)])
-            nc.scalar.copy(out=hT[:, cols(q)], in_=ht[:])
+            if q < DIRECT + 2:
+                nc.vector.tensor_copy(out=hT[:, cols(q)], in_=ht[:])
+            else:
+                nc.scalar.copy(out=hT[:, cols(q)], in_=ht[:])
             n_fill += 1
             if q - DIRECT < CFILL:
                 c_transposed(q - DIRECT, fill_tags[n_fill % 4])
@@ -367,17 +422,22 @@ def tile_lstmcell_t_kernel(
         load_c(2)
         load_c(3)
 
+        nc.vector.tensor_tensor(out=ratio[:], in0=ratio[:], in1=rstd_ih[:], op=ALU.mult)
+
         negm0 = small("negm0", 1)
 
         def gate_block(ci, jb):
             if ci < DIRECT:
                 hh = hh01[:, jb, ci, :]
             else:
-                hh = hh_matmul(ci, jb)[:]
+                hh = hh_matmul(ci, jb, "m%d" % jb)[:]
             nc.vector.scalar_tensor_tensor(
-                out=gate[jb][:, cols(ci)], in0=hh, scalar=ratio[:, jb : jb + 1], in1=gate[jb][:, cols(ci)],
+                out=gate[jb][:, cols(ci)], in0=gate[jb][:, cols(ci)], scalar=ratio[:, jb : jb + 1], in1=hh,
                 op0=ALU.mult, op1=ALU.add,
             )
+            if ci == 0 and jb == 0:
+                nc.vector.tensor_tensor(out=am[:], in0=am[:], in1=rstd_ih[:], op=ALU.mult)
+                nc.vector.tensor_tensor(out=cst[:], in0=cst[:], in1=am[:], op=ALU.subtract)
             nc.scalar.activation(
                 out=gate[jb][:, cols(ci)], in_=gate[jb][:, cols(ci)],
                 func=(ACT.Tanh if jb == 3 else ACT.Sigmoid),

@@ -411,10 +411,7 @@ def tile_lstmcell_t_kernel(
         n_fill = 0
         for q in range(DIRECT, CH):
             ht = transpose_bf16(fill_tags[n_fill % 4], [htile(q, t)[:, 0:H] for t in range(TPC)])
-            if q < DIRECT + 2:
-                nc.vector.tensor_copy(out=hT[:, cols(q)], in_=ht[:])
-            else:
-                nc.scalar.copy(out=hT[:, cols(q)], in_=ht[:])
+            nc.scalar.copy(out=hT[:, cols(q)], in_=ht[:])
             n_fill += 1
             if q - DIRECT < CFILL:
                 c_transposed(q - DIRECT, fill_tags[n_fill % 4])
@@ -461,8 +458,11 @@ def tile_lstmcell_t_kernel(
             )
 
         for ci in range(CH):
-            for jb in (0, 1, 3):
-                gate_block(ci, jb)
+            gate_block(ci, 0)
+            if ci >= 2:
+                cell_add(ci - 2)
+            gate_block(ci, 1)
+            gate_block(ci, 3)
             nc.gpsimd.tensor_tensor(
                 out=gate[0][:, cols(ci)], in0=gate[0][:, cols(ci)], in1=cT[:, cols(ci)], op=ALU.mult
             )
@@ -471,8 +471,6 @@ def tile_lstmcell_t_kernel(
             )
             if ci >= OLAG:
                 gate_block(ci - OLAG, 2)
-            if ci >= 2:
-                cell_add(ci - 2)
             if ci >= 3:
                 cell_square(ci - 3)
             if ci < CH - CFILL:

@@ -25,7 +25,7 @@ HG = 16
 HPAD = 144
 GW = P + 2
 OLAG = 6
-CFILL = 8
+CST = 3
 GCH = 12
 JB_ORDER = (0, 3, 1, 2)
 FLOPS = 2 * B * I * NB * H + 2 * B * H * NB * H
@@ -46,7 +46,7 @@ def tile_lstmcell_t_kernel(
         ctx.enter_context(tc.manual_schedule())
         keep = ctx.enter_context(tc.tile_pool(name="keep", bufs=1))
         psum = ctx.enter_context(tc.psum_pool(name="psum", bufs=1))
-        cpool = ctx.enter_context(tc.tile_pool(name="cpool", bufs=2))
+        cpool = ctx.enter_context(tc.tile_pool(name="cpool", bufs=3))
 
         gate = [keep.tile([P, B], F32, name="gate%d" % jb) for jb in range(NB)]
         hT = keep.tile([P, B], BF16)
@@ -106,6 +106,8 @@ def tile_lstmcell_t_kernel(
         make_identity(nc, ident_f[:])
         make_identity(nc, ident_b[:])
         nc.vector.memset(rows[:], 0.0)
+        nc.vector.memset(csum[:], 0.0)
+        nc.vector.memset(csq[:], 0.0)
         nc.vector.memset(neghalf[:], -0.5)
         nc.vector.memset(st_g[:, 0, :], 0.5 * GCH * CW)
         for g in range(TILES // HG):
@@ -245,7 +247,7 @@ def tile_lstmcell_t_kernel(
             c_nat = {}
 
             def load_c(cg):
-                c_nat[cg] = cpool.tile([P, HG, H], BF16, tag="cn", bufs=2, name="c_nat")
+                c_nat[cg] = cpool.tile([P, HG, H], BF16, tag="cn", bufs=3, name="c_nat")
                 nc.sync.dma_start(out=c_nat[cg][:], in_=cv[:, cg * HG : (cg + 1) * HG, :])
 
             t2 = small("t2")
@@ -317,7 +319,7 @@ def tile_lstmcell_t_kernel(
                         load_x(ci + 6)
                 if ci in (0, 2, 4):
                     load_h(ci // 2 + 1)
-                if ci in (8, 9):
+                if 8 <= ci < 11:
                     load_c(ci - 8)
                 if ci == 0:
                     wt = transpose_bf16("g", [whh_nat[:, jb, :] for jb in range(NB)])
@@ -389,7 +391,6 @@ def tile_lstmcell_t_kernel(
                     smalls.extend(hh_small_ops())
 
         late = ctx.enter_context(tc.tile_pool(name="late", bufs=3))
-        cT = late.tile([P, B], BF16, tag="cT", bufs=1, name="cT")
         for jb in range(NB):
             out = st_g[:, CH - GCH, :] if jb == 3 else st_ih[:, jb, CH - 1, :]
             nc.vector.bn_stats(out=out, in_=gate[jb][:, cols(CH - 1)])
@@ -403,9 +404,11 @@ def tile_lstmcell_t_kernel(
         am = small("am")
         nc.vector.tensor_tensor(out=am[:], in0=par[:, 4:8], in1=mv[:, :, 0], op=ALU.mult)
 
-        def c_transposed(q, tag):
-            ct = transpose_bf16(tag, [c_nat[q // TPC][:, (q % TPC) * TPC + t, :] for t in range(TPC)])
-            nc.scalar.copy(out=cT[:, cols(q)], in_=ct[:])
+        c_bank = {}
+
+        def c_transposed(q):
+            tiles = [c_nat[q // TPC][:, (q % TPC) * TPC + t, :] for t in range(TPC)]
+            c_bank[q] = transpose_bf16(("ta", "tb")[q % 2], tiles)
 
         fill_tags = ("ta", "tb", "th", "g")
         n_fill = 0
@@ -413,15 +416,14 @@ def tile_lstmcell_t_kernel(
             ht = transpose_bf16(fill_tags[n_fill % 4], [htile(q, t)[:, 0:H] for t in range(TPC)])
             nc.scalar.copy(out=hT[:, cols(q)], in_=ht[:])
             n_fill += 1
-            if q - DIRECT < CFILL:
-                c_transposed(q - DIRECT, fill_tags[n_fill % 4])
-                n_fill += 1
-        load_c(2)
-        load_c(3)
+        c_transposed(0)
 
         nc.vector.tensor_tensor(out=ratio[:], in0=ratio[:], in1=rstd_ih[:], op=ALU.mult)
 
         negm0 = small("negm0", 1)
+        dlt = small("dlt", 1)
+        mvc = small("mvc", 2)
+        st_c = keep.tile([P, (CH - 2) // CST + 1, 6], F32)
 
         def gate_block(ci, jb):
             if ci < DIRECT:
@@ -441,15 +443,54 @@ def tile_lstmcell_t_kernel(
                 scale=sc[:, jb : jb + 1], bias=cst[:, jb : jb + 1],
             )
 
-        def cell_add(ci):
+        def cell_products(ci):
+            nc.vector.tensor_tensor(
+                out=gate[0][:, cols(ci)], in0=c_bank[ci][:], in1=gate[0][:, cols(ci)], op=ALU.mult
+            )
+            nc.gpsimd.tensor_tensor(
+                out=gate[1][:, cols(ci)], in0=gate[1][:, cols(ci)], in1=gate[3][:, cols(ci)], op=ALU.mult
+            )
+            if ci < CH - 1:
+                nc.gpsimd.tensor_tensor(
+                    out=gate[0][:, cols(ci)], in0=gate[0][:, cols(ci)], in1=gate[1][:, cols(ci)], op=ALU.add
+                )
+
+        def last_cell_add(ci):
             nc.vector.scalar_tensor_tensor(
                 out=gate[0][:, cols(ci)], in0=gate[0][:, cols(ci)], scalar=1.0, in1=gate[1][:, cols(ci)],
                 op0=ALU.mult, op1=ALU.add, accum_out=csum[:, ci : ci + 1],
             )
-            if ci == 0:
-                nc.vector.tensor_scalar(
-                    out=negm0[:], in0=csum[:, 0:1], scalar1=-1.0 / CW, scalar2=None, op0=ALU.mult
-                )
+
+        def by_vector(ci):
+            return ci % CST == 0 and ci < CH - 1
+
+        vstat = [ci for ci in range(CH) if by_vector(ci)]
+        nv = len(vstat) * CW
+
+        def cell_stats(ci):
+            src = gate[0][:, cols(ci)]
+            if by_vector(ci):
+                k = vstat.index(ci)
+                nc.vector.bn_stats(out=st_c[:, k, :], in_=src)
+                if k == 0:
+                    nc.vector.bn_aggr(out=mvc[:], in_=st_c[:, 0, :])
+                    nc.vector.tensor_scalar(
+                        out=negm0[:], in0=mvc[:, 0:1], scalar1=-1.0, scalar2=None, op0=ALU.mult
+                    )
+            else:
+                if ci < CH - 1:
+                    nc.scalar.activation(
+                        out=junk[:], in_=src, func=ACT.Copy, accum_out=csum[:, ci : ci + 1]
+                    )
+                cell_square(ci)
+
+        def vector_cell_stats():
+            nc.vector.bn_aggr(out=mvc[:], in_=st_c[:].rearrange("p k s -> p (k s)"))
+            nc.vector.tensor_scalar(out=csum[:, 0:1], in0=mvc[:, 0:1], scalar1=float(nv), scalar2=None, op0=ALU.mult)
+            nc.vector.tensor_tensor(out=dlt[:], in0=mvc[:, 0:1], in1=negm0[:], op=ALU.add)
+            nc.vector.tensor_tensor(out=dlt[:], in0=dlt[:], in1=dlt[:], op=ALU.mult)
+            nc.vector.tensor_tensor(out=dlt[:], in0=dlt[:], in1=mvc[:, 1:2], op=ALU.add)
+            nc.vector.tensor_scalar(out=csq[:, 0:1], in0=dlt[:], scalar1=float(nv), scalar2=None, op0=ALU.mult)
 
         def cell_square(ci):
             nc.scalar.activation(
@@ -459,38 +500,43 @@ def tile_lstmcell_t_kernel(
 
         for ci in range(CH):
             gate_block(ci, 0)
-            if ci >= 2:
-                cell_add(ci - 2)
             gate_block(ci, 1)
             gate_block(ci, 3)
-            nc.gpsimd.tensor_tensor(
-                out=gate[0][:, cols(ci)], in0=gate[0][:, cols(ci)], in1=cT[:, cols(ci)], op=ALU.mult
-            )
-            nc.gpsimd.tensor_tensor(
-                out=gate[1][:, cols(ci)], in0=gate[1][:, cols(ci)], in1=gate[3][:, cols(ci)], op=ALU.mult
-            )
+            cell_products(ci)
             if ci >= OLAG:
                 gate_block(ci - OLAG, 2)
             if ci >= 3:
-                cell_square(ci - 3)
-            if ci < CH - CFILL:
-                c_transposed(ci + CFILL, ("ta", "tb")[ci % 2])
+                cell_stats(ci - 3)
+            if ci + 1 < CH:
+                c_transposed(ci + 1)
+            if ci == 4:
+                load_c(3)
+
+        o_bank = {}
+
+        def transposed_f32(tag, src, ci):
+            bank = psum.tile([P, TPC, P], F32, tag=tag, name="ot")
+            for t in range(TPC):
+                nc.tensor.transpose(bank[:, t, :], src[:, ci * CW + t * P : ci * CW + (t + 1) * P], ident_f[:])
+            return bank
+
+        def o_transposed(ci):
+            o_bank[ci] = transposed_f32("m%d" % (ci % 4), gate[2], ci)
 
         gate_block(CH - 6, 2)
-        cell_add(CH - 2)
-        cell_square(CH - 3)
+        cell_stats(CH - 3)
+        last_cell_add(CH - 1)
+        vector_cell_stats()
         gate_block(CH - 5, 2)
         gate_block(CH - 4, 2)
-        cell_add(CH - 1)
-        cell_square(CH - 2)
-        cell_square(CH - 1)
+        cell_stats(CH - 2)
+        cell_stats(CH - 1)
         gate_block(CH - 3, 2)
         s1c = small("s1c", 1)
         nc.vector.reduce_sum(out=s1c[:], in_=csum[:], axis=AX.X)
-        mean_c = small("mean_c", 1)
-        nc.vector.tensor_scalar(out=mean_c[:], in0=s1c[:], scalar1=1.0 / B, scalar2=None, op0=ALU.mult)
-        dlt = small("dlt", 1)
-        nc.vector.tensor_tensor(out=dlt[:], in0=mean_c[:], in1=negm0[:], op=ALU.add)
+        nc.vector.scalar_tensor_tensor(
+            out=dlt[:], in0=s1c[:], scalar=1.0 / B, in1=negm0[:], op0=ALU.mult, op1=ALU.add
+        )
         nc.vector.tensor_tensor(out=dlt[:], in0=dlt[:], in1=dlt[:], op=ALU.mult)
         s2c = small("s2c", 1)
         nc.vector.reduce_sum(out=s2c[:], in_=csq[:], axis=AX.X)
@@ -501,43 +547,35 @@ def tile_lstmcell_t_kernel(
         nc.vector.tensor_scalar(out=ve_c[:], in0=ve_c[:], scalar1=0.0, scalar2=EPS, op0=ALU.max, op1=ALU.add)
         rstd_c = small("rstd_c", 1)
         nc.gpsimd.tensor_tensor(out=rstd_c[:], in0=ve_c[:], in1=neghalf[:, 0:1], op=ALU.pow)
+        negmean = small("negmean", 1)
+        nc.vector.tensor_scalar(out=negmean[:], in0=s1c[:], scalar1=-1.0 / B, scalar2=None, op0=ALU.mult)
         gate_block(CH - 2, 2)
         gate_block(CH - 1, 2)
+        o_transposed(0)
+        o_transposed(1)
         a_c = small("a_c", 1)
         nc.vector.tensor_tensor(out=a_c[:], in0=par[:, 20:21], in1=rstd_c[:], op=ALU.mult)
         k_c = small("k_c", 1)
-        nc.vector.tensor_tensor(out=k_c[:], in0=a_c[:], in1=mean_c[:], op=ALU.mult)
-        nc.vector.tensor_tensor(out=k_c[:], in0=par[:, 21:22], in1=k_c[:], op=ALU.subtract)
+        nc.vector.scalar_tensor_tensor(
+            out=k_c[:], in0=a_c[:], scalar=negmean[:], in1=par[:, 21:22], op0=ALU.mult, op1=ALU.add
+        )
 
-        out_tags = (("ta", "m0", "m2", "g"), ("tb", "m1", "m3", "th"))
-        out_banks = {}
-        LAG = 2
-        for ci in range(CH + LAG):
-            if ci < CH:
-                nc.gpsimd.tensor_scalar(
-                    out=gate[1][:, cols(ci)], in0=gate[0][:, cols(ci)], scalar1=a_c[:], scalar2=k_c[:],
-                    op0=ALU.mult, op1=ALU.add,
-                )
-                nc.scalar.activation(
-                    out=gate[3][:, cols(ci)], in_=gate[0][:, cols(ci)], func=ACT.Tanh,
-                    scale=a_c[:], bias=k_c[:],
-                )
-                nc.vector.tensor_tensor(
-                    out=gate[2][:, cols(ci)], in0=gate[2][:, cols(ci)], in1=gate[3][:, cols(ci)], op=ALU.mult
-                )
-                for o, src in enumerate((gate[1], gate[2])):
-                    ot = psum.tile([P, TPC, P], F32, tag=out_tags[o][ci % 4], name="ot")
-                    for t in range(TPC):
-                        nc.tensor.transpose(
-                            ot[:, t, :], src[:, ci * CW + t * P : ci * CW + (t + 1) * P], ident_f[:]
-                        )
-                    out_banks[(ci, o)] = ot
-            cj = ci - LAG
-            if cj >= 0:
-                for o in range(2):
-                    ob = late.tile([P, TPC, P], F32, tag="ob%d" % o, bufs=3, name="ob")
-                    if o == 0:
-                        nc.scalar.copy(out=ob[:], in_=out_banks[(cj, o)][:])
-                    else:
-                        nc.vector.tensor_copy(out=ob[:], in_=out_banks[(cj, o)][:])
-                    nc.sync.dma_start(out=outv[o][:, cj * TPC : (cj + 1) * TPC, :], in_=ob[:])
+        for ci in range(CH):
+            nc.gpsimd.tensor_scalar(
+                out=gate[1][:, cols(ci)], in0=gate[0][:, cols(ci)], scalar1=a_c[:], scalar2=k_c[:],
+                op0=ALU.mult, op1=ALU.add,
+            )
+            cbank = transposed_f32(("ta", "tb", "th", "g")[ci % 4], gate[1], ci)
+            if ci + 2 < CH:
+                o_transposed(ci + 2)
+            tanh_c = gate[3][:, cols(ci)].rearrange("p (t h) -> p t h", t=TPC)
+            nc.scalar.activation(out=tanh_c, in_=cbank[:], func=ACT.Tanh)
+            c_out = late.tile([P, TPC, P], F32, tag="c_out", bufs=3, name="c_out")
+            if ci % 2 == 0:
+                nc.scalar.copy(out=c_out[:], in_=cbank[:])
+            else:
+                nc.vector.tensor_copy(out=c_out[:], in_=cbank[:])
+            nc.sync.dma_start(out=outv[0][:, ci * TPC : (ci + 1) * TPC, :], in_=c_out[:])
+            h_out = late.tile([P, TPC, P], F32, tag="h_out", bufs=3, name="h_out")
+            nc.vector.tensor_tensor(out=h_out[:], in0=o_bank[ci][:], in1=tanh_c, op=ALU.mult)
+            nc.sync.dma_start(out=outv[1][:, ci * TPC : (ci + 1) * TPC, :], in_=h_out[:])

@@ -20,13 +20,18 @@ TPC = 4
 CH = TILES // TPC
 CW = TPC * P
 EPS = 1e-5
-DIRECT = 2
+DT = TPC + 1
+D0 = 3
+GPI = 6
 HG = 16
 HPAD = 144
 GW = P + 2
-OLAG = 6
-CST = 3
 GCH = 12
+SX = 14
+HGAP = 14
+OGAP = 3
+AV = 1
+CST = 2
 JB_ORDER = (0, 3, 1, 2)
 FLOPS = 2 * B * I * NB * H + 2 * B * H * NB * H
 
@@ -46,11 +51,11 @@ def tile_lstmcell_t_kernel(
         ctx.enter_context(tc.manual_schedule())
         keep = ctx.enter_context(tc.tile_pool(name="keep", bufs=1))
         psum = ctx.enter_context(tc.psum_pool(name="psum", bufs=1))
-        cpool = ctx.enter_context(tc.tile_pool(name="cpool", bufs=3))
+        cpool = ctx.enter_context(tc.tile_pool(name="cpool", bufs=4))
 
         gate = [keep.tile([P, B], F32, name="gate%d" % jb) for jb in range(NB)]
         hT = keep.tile([P, B], BF16)
-        hh01 = keep.tile([P, NB, DIRECT, CW], F32)
+        hh_dir = keep.tile([P, NB, DT * P], F32)
         h_nat = [keep.tile([P, HG, HPAD], BF16, name="h_nat%d" % g) for g in range(TILES // HG)]
         w_codes = keep.tile([P, NB * P], U32, align_bytes=64)
         w_scales = keep.tile([P, NB * P], U8, align_bytes=64)
@@ -63,12 +68,13 @@ def tile_lstmcell_t_kernel(
         par = keep.tile([P, 24], F32)
         gs = keep.tile([P, GW], F32)
         st_ih = keep.tile([P, NB - 1, CH, 6], F32)
-        st_g = keep.tile([P, 1 + CH - GCH, 6], F32)
+        st_g = keep.tile([P, 2 + 6 * (1 + CH - GCH)], F32)
         gsum = keep.tile([P, GCH], F32)
         gacc = keep.tile([P, CW], F32)
-        gred = keep.tile([P, 4], F32)
-        hsum = keep.tile([P, DIRECT], F32)
-        sq01 = keep.tile([P, DIRECT, NB], F32)
+        gred = keep.tile([P, 2], F32)
+        gtmp = keep.tile([P, 2], F32)
+        hsum = keep.tile([P, 2], F32)
+        sq_dir = keep.tile([P, 2, NB], F32)
         csum = keep.tile([P, CH], F32)
         csq = keep.tile([P, CH], F32)
         junk = keep.tile([P, CW], BF16)
@@ -86,8 +92,7 @@ def tile_lstmcell_t_kernel(
         def blk(jb):
             return slice(jb * P, (jb + 1) * P)
 
-        def htile(ci, t):
-            s = ci * TPC + t
+        def htile(s):
             return h_nat[s // HG][:, s % HG, :]
 
         def transpose_bf16(tag, tiles):
@@ -96,9 +101,11 @@ def tile_lstmcell_t_kernel(
                 nc.tensor.transpose(bank[:, t * P : (t + 1) * P], src, ident_b[:])
             return bank
 
-        def hh_matmul(ci, jb, tag):
+        def hh_matmul(b0, b1, jb, tag):
             acc = psum.tile([P, CW], F32, tag=tag, name="acc")
-            nc.tensor.matmul(out=acc[:], lhsT=whhT_b[:, blk(jb)], rhs=hT[:, cols(ci)], start=True, stop=True)
+            nc.tensor.matmul(
+                out=acc[:, 0 : b1 - b0], lhsT=whhT_b[:, blk(jb)], rhs=hT[:, b0:b1], start=True, stop=True
+            )
             return acc
 
         nc.vector.memset(warm[:], 0.0)
@@ -109,7 +116,7 @@ def tile_lstmcell_t_kernel(
         nc.vector.memset(csum[:], 0.0)
         nc.vector.memset(csq[:], 0.0)
         nc.vector.memset(neghalf[:], -0.5)
-        nc.vector.memset(st_g[:, 0, :], 0.5 * GCH * CW)
+        nc.vector.memset(st_g[:, 0:8], 0.5 * GCH * CW)
         for g in range(TILES // HG):
             nc.vector.memset(h_nat[g][:, :, H:HPAD], 1.0)
 
@@ -135,9 +142,7 @@ def tile_lstmcell_t_kernel(
                     for a in range(2):
                         sw = src[:, 2 * half + a, :].bitcast(F32)
                         for u in range(2):
-                            nc.tensor.transpose(
-                                xt[:, u, a * P : (a + 1) * P], sw[:, u : 2 * P : 2], ident_f[:]
-                            )
+                            nc.tensor.transpose(xt[:, u, a * P : (a + 1) * P], sw[:, u : 2 * P : 2], ident_f[:])
                     pair.append(xt)
                 banks[key] = pair
 
@@ -189,7 +194,8 @@ def tile_lstmcell_t_kernel(
                 if jb < 3:
                     nc.vector.bn_stats(out=st_ih[:, jb, ci, :], in_=gate[jb][:, cols(ci)])
                 elif ci >= GCH:
-                    nc.vector.bn_stats(out=st_g[:, 1 + ci - GCH, :], in_=gate[jb][:, cols(ci)])
+                    k = 8 + 6 * (ci - GCH)
+                    nc.vector.bn_stats(out=st_g[:, k : k + 6], in_=gate[jb][:, cols(ci)])
                 else:
                     src = gate[jb][:, cols(ci)]
                     if ci == 0:
@@ -199,19 +205,19 @@ def tile_lstmcell_t_kernel(
                         nc.gpsimd.tensor_tensor(out=sq[:], in0=src, in1=src, op=ALU.mult)
                         nc.gpsimd.tensor_tensor(out=gacc[:], in0=gacc[:], in1=sq[:], op=ALU.add)
 
-            def stat_g_tuple():
+            def stat_g_record():
                 n = GCH * CW
                 nc.vector.reduce_sum(out=gred[:, 0:1], in_=gsum[:], axis=AX.X)
                 nc.vector.reduce_sum(out=gred[:, 1:2], in_=gacc[:], axis=AX.X)
-                for col in (1, 4):
-                    nc.vector.tensor_scalar(
-                        out=st_g[:, 0, col : col + 1], in0=gred[:, 0:1], scalar1=1.0 / n, scalar2=None, op0=ALU.mult
+                for k in (3, 6):
+                    nc.gpsimd.tensor_scalar(
+                        out=st_g[:, k : k + 1], in0=gred[:, 0:1], scalar1=1.0 / n, scalar2=0.0, op0=ALU.mult, op1=ALU.add
                     )
-                nc.vector.tensor_tensor(out=gred[:, 2:3], in0=gred[:, 0:1], in1=st_g[:, 0, 1:2], op=ALU.mult)
-                nc.vector.tensor_tensor(out=gred[:, 3:4], in0=gred[:, 1:2], in1=gred[:, 2:3], op=ALU.subtract)
-                for col in (2, 5):
-                    nc.vector.tensor_scalar(
-                        out=st_g[:, 0, col : col + 1], in0=gred[:, 3:4], scalar1=0.5, scalar2=None, op0=ALU.mult
+                nc.gpsimd.tensor_tensor(out=gtmp[:, 0:1], in0=gred[:, 0:1], in1=st_g[:, 3:4], op=ALU.mult)
+                nc.gpsimd.tensor_tensor(out=gtmp[:, 1:2], in0=gred[:, 1:2], in1=gtmp[:, 0:1], op=ALU.subtract)
+                for k in (4, 7):
+                    nc.gpsimd.tensor_scalar(
+                        out=st_g[:, k : k + 1], in0=gtmp[:, 1:2], scalar1=0.5, scalar2=0.0, op0=ALU.mult, op1=ALU.add
                     )
 
             w_sb = stage.tile([P, NB, I], BF16, tag="xs", bufs=4, name="w_sb")
@@ -247,7 +253,7 @@ def tile_lstmcell_t_kernel(
             c_nat = {}
 
             def load_c(cg):
-                c_nat[cg] = cpool.tile([P, HG, H], BF16, tag="cn", bufs=3, name="c_nat")
+                c_nat[cg] = cpool.tile([P, HG, H], BF16, tag="cn", bufs=4, name="c_nat")
                 nc.sync.dma_start(out=c_nat[cg][:], in_=cv[:, cg * HG : (cg + 1) * HG, :])
 
             t2 = small("t2")
@@ -264,123 +270,113 @@ def tile_lstmcell_t_kernel(
             cst = small("cst")
 
             def hh_small_ops():
-                def tt(out, in0, in1, op):
-                    return lambda: nc.vector.tensor_tensor(out=out, in0=in0, in1=in1, op=op)
-
-                return [
-                    tt(t2[:], t2[:], sq01[:, 0, :], ALU.add),
-                    lambda: nc.vector.tensor_scalar(
-                        out=mean_hh[:], in0=s1[:], scalar1=1.0 / B, scalar2=None, op0=ALU.mult
-                    ),
-                    tt(bsum[:], par[:, 0:4], par[:, 8:12], ALU.add),
-                    tt(t2[:], t2[:], sq01[:, 1, :], ALU.add),
-                    tt(msq[:], mean_hh[:], mean_hh[:], ALU.mult),
-                    tt(bsum[:], bsum[:], par[:, 16:20], ALU.add),
-                    lambda: nc.vector.scalar_tensor_tensor(
-                        out=var_hh[:], in0=t2[:], scalar=1.0 / B, in1=msq[:], op0=ALU.mult, op1=ALU.subtract
-                    ),
-                    lambda: nc.vector.tensor_scalar(
-                        out=var_hh[:], in0=var_hh[:], scalar1=0.0, scalar2=EPS, op0=ALU.max, op1=ALU.add
-                    ),
-                    lambda: nc.gpsimd.tensor_tensor(out=rstd_hh[:], in0=var_hh[:], in1=neghalf[:], op=ALU.pow),
-                ]
+                e = nc.gpsimd
+                e.tensor_tensor(out=t2[:], in0=t2[:], in1=sq_dir[:, 0, :], op=ALU.add)
+                e.tensor_tensor(out=t2[:], in0=t2[:], in1=sq_dir[:, 1, :], op=ALU.add)
+                e.tensor_scalar(out=mean_hh[:], in0=s1[:], scalar1=1.0 / B, scalar2=0.0, op0=ALU.mult, op1=ALU.add)
+                e.tensor_tensor(out=msq[:], in0=mean_hh[:], in1=mean_hh[:], op=ALU.mult)
+                e.tensor_scalar(out=t2[:], in0=t2[:], scalar1=1.0 / B, scalar2=0.0, op0=ALU.mult, op1=ALU.add)
+                e.tensor_tensor(out=var_hh[:], in0=t2[:], in1=msq[:], op=ALU.subtract)
+                e.tensor_scalar(out=var_hh[:], in0=var_hh[:], scalar1=0.0, scalar2=EPS, op0=ALU.max, op1=ALU.add)
+                e.tensor_tensor(out=rstd_hh[:], in0=var_hh[:], in1=neghalf[:], op=ALU.pow)
+                e.tensor_tensor(out=a_hh[:], in0=par[:, 12:16], in1=rstd_hh[:], op=ALU.mult)
+                e.tensor_scalar(
+                    out=zfix[:], in0=a_hh[:], scalar1=0.0, scalar2=1e-30, op0=ALU.is_equal, op1=ALU.mult
+                )
+                e.tensor_tensor(out=sc[:], in0=a_hh[:], in1=zfix[:], op=ALU.add)
+                e.tensor_tensor(out=bsum[:], in0=par[:, 0:4], in1=par[:, 8:12], op=ALU.add)
+                e.tensor_tensor(out=bsum[:], in0=bsum[:], in1=par[:, 16:20], op=ALU.add)
+                e.tensor_tensor(out=cst[:], in0=a_hh[:], in1=mean_hh[:], op=ALU.mult)
+                e.tensor_tensor(out=cst[:], in0=bsum[:], in1=cst[:], op=ALU.subtract)
 
             gram = None
-            smalls = []
-
-            def few_smalls(ci):
-                for op in smalls[:3]:
-                    op()
-                smalls[:] = smalls[3:]
-
             for ci in range(CH):
                 nxt = ci + 1
                 if nxt < CH:
                     new_grp(nxt)
                     evac(nxt, 0, True)
-                    evac(nxt, 1, False)
+                    evac(nxt, 1, nxt >= SX)
                 if ci >= 1:
                     stat_ih(ci - 1, 0)
-                    few_smalls(ci)
                 if nxt < CH:
                     quant(nxt)
-                direct = 2 <= ci < 2 + DIRECT * NB
-                if direct:
-                    dq, djb = divmod(ci - 2, NB)
-                    dacc = hh_matmul(dq, djb, "th")
-                    nc.vector.tensor_copy(out=hh01[:, djb, dq, :], in_=dacc[:])
+                if D0 <= ci < D0 + NB:
+                    dacc = hh_matmul(0, CW, ci - D0, "th")
+                    nc.vector.tensor_copy(out=hh_dir[:, ci - D0, 0:CW], in_=dacc[:])
+                if ci == D0 + NB:
+                    dacc = psum.tile([P, NB, P], F32, tag="th", name="dacc")
+                    for jb in range(NB):
+                        nc.tensor.matmul(
+                            out=dacc[:, jb, :], lhsT=whhT_b[:, blk(jb)], rhs=hT[:, CW : DT * P], start=True, stop=True
+                        )
+                    nc.vector.tensor_copy(out=hh_dir[:, :, CW : DT * P], in_=dacc[:])
                 if ci >= 1:
                     for jb in range(1, NB):
                         stat_ih(ci - 1, jb)
-                        few_smalls(ci)
                 if ci + 2 < CH:
                     t1(ci + 2, x_sb[ci + 2])
                     if ci + 6 < CH:
                         load_x(ci + 6)
                 if ci in (0, 2, 4):
                     load_h(ci // 2 + 1)
-                if 8 <= ci < 11:
+                if 8 <= ci < 12:
                     load_c(ci - 8)
-                if ci == 0:
+                if ci == 1:
                     wt = transpose_bf16("g", [whh_nat[:, jb, :] for jb in range(NB)])
                     nc.vector.tensor_copy(out=whhT_b[:], in_=wt[:])
-                    nc.vector.tensor_copy(out=whhT_f[:], in_=wt[:])
+                    nc.gpsimd.tensor_copy(out=whhT_f[:], in_=whhT_b[:])
                     pt = psum.tile([P, P], BF16, tag="th", name="pt")
                     nc.tensor.transpose(pt[:], rows[:], ident_b[:])
                     nc.vector.tensor_copy(out=par[:], in_=pt[:, 0:24])
+                if ci == CH - 2:
+                    stat_g_record()
                 if ci == CH - 1:
-                    nc.vector.tensor_tensor(out=a_hh[:], in0=par[:, 12:16], in1=rstd_hh[:], op=ALU.mult)
-                    nc.vector.tensor_scalar(
-                        out=zfix[:], in0=a_hh[:], scalar1=0.0, scalar2=1e-30, op0=ALU.is_equal, op1=ALU.mult
-                    )
-                    nc.vector.tensor_tensor(out=cst[:], in0=a_hh[:], in1=mean_hh[:], op=ALU.mult)
-                    nc.vector.tensor_tensor(out=sc[:], in0=a_hh[:], in1=zfix[:], op=ALU.add)
-                    nc.vector.tensor_tensor(out=cst[:], in0=bsum[:], in1=cst[:], op=ALU.subtract)
                     nc.vector.reciprocal(out=ratio[:], in_=sc[:])
-                    stat_g_tuple()
                     nc.vector.tensor_tensor(out=ratio[:], in0=ratio[:], in1=par[:, 4:8], op=ALU.mult)
                 copy_ih(ci)
-                if ci == 1:
-                    for q, tag in enumerate(("th", "g")):
-                        ht = transpose_bf16(tag, [htile(q, t)[:, 0:H] for t in range(TPC)])
+                if ci == 2:
+                    for k, (tag, s0, s9) in enumerate((("th", 0, TPC), ("g", TPC, DT))):
+                        ht = transpose_bf16(tag, [htile(s)[:, 0:H] for s in range(s0, s9)])
                         nc.scalar.activation(
-                            out=hT[:, cols(q)], in_=ht[:], func=ACT.Copy, accum_out=hsum[:, q : q + 1]
+                            out=hT[:, s0 * P : s9 * P], in_=ht[:, 0 : (s9 - s0) * P], func=ACT.Copy,
+                            accum_out=hsum[:, k : k + 1],
                         )
-                if 3 <= ci <= 9:
-                    if ci == 3:
+                s0 = DT + GPI * (ci - 2)
+                if ci >= 2 and s0 < TILES:
+                    if ci == 2:
                         gram = psum.tile([P, GW], F32, tag="g", name="gram")
-                    for q in (2 * ci - 4, 2 * ci - 3):
-                        for t in range(TPC):
-                            nc.tensor.matmul(
-                                out=gram[:],
-                                lhsT=htile(q, t)[:, 0:H],
-                                rhs=htile(q, t)[:, 0:GW],
-                                start=(q == DIRECT and t == 0),
-                                stop=(q == CH - 1 and t == TPC - 1),
-                            )
+                    for s in range(s0, min(s0 + GPI, TILES)):
+                        nc.tensor.matmul(
+                            out=gram[:], lhsT=htile(s)[:, 0:H], rhs=htile(s)[:, 0:GW],
+                            start=(s == DT), stop=(s == TILES - 1),
+                        )
                 if nxt < CH:
                     mx(nxt)
-                if direct:
+                if D0 <= ci < D0 + NB:
                     nc.scalar.activation(
-                        out=junk[:], in_=dacc[:], func=ACT.Square, accum_out=sq01[:, dq, djb : djb + 1]
+                        out=junk[:], in_=dacc[:], func=ACT.Square, accum_out=sq_dir[:, 0, ci - D0 : ci - D0 + 1]
                     )
-                if ci == 10:
-                    nc.vector.tensor_copy(out=gs[:], in_=gram[:])
-                    for q in range(DIRECT):
-                        nc.vector.tensor_tensor(
-                            out=gs[:, P : P + 1], in0=gs[:, P : P + 1], in1=hsum[:, q : q + 1], op=ALU.add
+                if ci == D0 + NB:
+                    for jb in range(NB):
+                        nc.scalar.activation(
+                            out=junk[:, 0:P], in_=dacc[:, jb, :], func=ACT.Square, accum_out=sq_dir[:, 1, jb : jb + 1]
                         )
                 if ci == 11:
+                    nc.vector.tensor_copy(out=gs[:], in_=gram[:])
+                    for k in range(2):
+                        nc.vector.tensor_tensor(
+                            out=gs[:, P : P + 1], in0=gs[:, P : P + 1], in1=hsum[:, k : k + 1], op=ALU.add
+                        )
+                if ci == 12:
                     ys = []
                     for pair, tag in enumerate(("th", "g")):
                         y = psum.tile([P, 2, GW], F32, tag=tag, name="y")
                         for a in range(2):
                             nc.tensor.matmul(
-                                out=y[:, a, :], lhsT=whhT_f[:, blk(2 * pair + a)], rhs=gs[:],
-                                start=True, stop=True,
+                                out=y[:, a, :], lhsT=whhT_f[:, blk(2 * pair + a)], rhs=gs[:], start=True, stop=True
                             )
                         ys.append(y)
-                if ci == 12:
+                if ci == 13:
                     for pair in range(2):
                         nc.vector.tensor_tensor(
                             out=prod[:, 2 * pair : 2 * pair + 2, :], in0=ys[pair][:, :, 0:P],
@@ -388,15 +384,14 @@ def tile_lstmcell_t_kernel(
                         )
                         nc.vector.tensor_copy(out=s1[:, 2 * pair : 2 * pair + 2], in_=ys[pair][:, :, P])
                     nc.vector.reduce_sum(out=t2[:], in_=prod[:], axis=AX.X)
-                    smalls.extend(hh_small_ops())
+                    hh_small_ops()
 
         late = ctx.enter_context(tc.tile_pool(name="late", bufs=3))
         for jb in range(NB):
-            out = st_g[:, CH - GCH, :] if jb == 3 else st_ih[:, jb, CH - 1, :]
-            nc.vector.bn_stats(out=out, in_=gate[jb][:, cols(CH - 1)])
+            stat_ih(CH - 1, jb)
         for jb in range(NB):
-            tuples = st_g[:] if jb == 3 else st_ih[:, jb, :, :]
-            nc.vector.bn_aggr(out=mv[:, jb, :], in_=tuples.rearrange("p c s -> p (c s)"))
+            records = st_g[:, 2:] if jb == 3 else st_ih[:, jb, :, :].rearrange("p c s -> p (c s)")
+            nc.vector.bn_aggr(out=mv[:, jb, :], in_=records)
         ve_ih = small("ve_ih")
         nc.vector.tensor_scalar(out=ve_ih[:], in0=mv[:, :, 1], scalar1=EPS, scalar2=None, op0=ALU.add)
         rstd_ih = small("rstd_ih")
@@ -408,14 +403,15 @@ def tile_lstmcell_t_kernel(
 
         def c_transposed(q):
             tiles = [c_nat[q // TPC][:, (q % TPC) * TPC + t, :] for t in range(TPC)]
-            c_bank[q] = transpose_bf16(("ta", "tb")[q % 2], tiles)
+            c_bank[q] = transpose_bf16(("ta", "tb", "th")[q % 3], tiles)
 
-        fill_tags = ("ta", "tb", "th", "g")
-        n_fill = 0
-        for q in range(DIRECT, CH):
-            ht = transpose_bf16(fill_tags[n_fill % 4], [htile(q, t)[:, 0:H] for t in range(TPC)])
-            nc.scalar.copy(out=hT[:, cols(q)], in_=ht[:])
-            n_fill += 1
+        def h_transposed(s0, s9, tag):
+            ht = transpose_bf16(tag, [htile(s)[:, 0:H] for s in range(s0, s9)])
+            nc.scalar.copy(out=hT[:, s0 * P : s9 * P], in_=ht[:, 0 : (s9 - s0) * P])
+
+        h_transposed(DT, 2 * TPC, "m2")
+        for q in range(2, 2 + HGAP):
+            h_transposed(q * TPC, (q + 1) * TPC, ("g", "tb", "th", "m2")[q % 4])
         c_transposed(0)
 
         nc.vector.tensor_tensor(out=ratio[:], in0=ratio[:], in1=rstd_ih[:], op=ALU.mult)
@@ -423,74 +419,66 @@ def tile_lstmcell_t_kernel(
         negm0 = small("negm0", 1)
         dlt = small("dlt", 1)
         mvc = small("mvc", 2)
-        st_c = keep.tile([P, (CH - 2) // CST + 1, 6], F32)
+        st_c = keep.tile([P, (CH - 3) // CST + 1, 6], F32)
 
-        def gate_block(ci, jb):
-            if ci < DIRECT:
-                hh = hh01[:, jb, ci, :]
-            else:
-                hh = hh_matmul(ci, jb, "m%d" % jb)[:]
-            nc.vector.scalar_tensor_tensor(
-                out=gate[jb][:, cols(ci)], in0=gate[jb][:, cols(ci)], scalar=ratio[:, jb : jb + 1], in1=hh,
-                op0=ALU.mult, op1=ALU.add,
-            )
+        def combine(ci, jb, tag):
+            b0, b9 = ci * CW, (ci + 1) * CW
+            pieces = []
+            if b0 < DT * P:
+                pieces.append((b0, min(b9, DT * P), hh_dir[:, jb, b0 : min(b9, DT * P)]))
+            if b9 > DT * P:
+                b1 = max(b0, DT * P)
+                pieces.append((b1, b9, hh_matmul(b1, b9, jb, tag)[:, 0 : b9 - b1]))
+            for b1, b2, hh in pieces:
+                nc.vector.scalar_tensor_tensor(
+                    out=gate[jb][:, b1:b2], in0=gate[jb][:, b1:b2], scalar=ratio[:, jb : jb + 1], in1=hh,
+                    op0=ALU.mult, op1=ALU.add,
+                )
             if ci == 0 and jb == 0:
                 nc.vector.tensor_tensor(out=am[:], in0=am[:], in1=rstd_ih[:], op=ALU.mult)
                 nc.vector.tensor_tensor(out=cst[:], in0=cst[:], in1=am[:], op=ALU.subtract)
+
+        def squash(ci, jb):
             nc.scalar.activation(
                 out=gate[jb][:, cols(ci)], in_=gate[jb][:, cols(ci)],
                 func=(ACT.Tanh if jb == 3 else ACT.Sigmoid),
                 scale=sc[:, jb : jb + 1], bias=cst[:, jb : jb + 1],
             )
 
-        def cell_products(ci):
+        def gate_block(ci, jb, tag):
+            combine(ci, jb, tag)
+            squash(ci, jb)
+
+        def o_combine(ci):
+            combine(ci, 2, ("m2", "m3")[ci % 2])
+
+        def o_gate(ci):
+            o_combine(ci)
+            squash(ci, 2)
+
+        def forget_product(ci):
             nc.vector.tensor_tensor(
                 out=gate[0][:, cols(ci)], in0=c_bank[ci][:], in1=gate[0][:, cols(ci)], op=ALU.mult
             )
-            nc.gpsimd.tensor_tensor(
+
+        def input_product(engine, ci):
+            engine.tensor_tensor(
                 out=gate[1][:, cols(ci)], in0=gate[1][:, cols(ci)], in1=gate[3][:, cols(ci)], op=ALU.mult
             )
-            if ci < CH - 1:
-                nc.gpsimd.tensor_tensor(
-                    out=gate[0][:, cols(ci)], in0=gate[0][:, cols(ci)], in1=gate[1][:, cols(ci)], op=ALU.add
-                )
 
-        def last_cell_add(ci):
+        def add_on_gpsimd(ci):
+            nc.gpsimd.tensor_tensor(
+                out=gate[0][:, cols(ci)], in0=gate[0][:, cols(ci)], in1=gate[1][:, cols(ci)], op=ALU.add
+            )
+
+        def add_on_vector(ci):
             nc.vector.scalar_tensor_tensor(
                 out=gate[0][:, cols(ci)], in0=gate[0][:, cols(ci)], scalar=1.0, in1=gate[1][:, cols(ci)],
                 op0=ALU.mult, op1=ALU.add, accum_out=csum[:, ci : ci + 1],
             )
 
-        def by_vector(ci):
-            return ci % CST == 0 and ci < CH - 1
-
-        vstat = [ci for ci in range(CH) if by_vector(ci)]
+        vstat = [ci for ci in range(CH - 2) if ci % CST == 0]
         nv = len(vstat) * CW
-
-        def cell_stats(ci):
-            src = gate[0][:, cols(ci)]
-            if by_vector(ci):
-                k = vstat.index(ci)
-                nc.vector.bn_stats(out=st_c[:, k, :], in_=src)
-                if k == 0:
-                    nc.vector.bn_aggr(out=mvc[:], in_=st_c[:, 0, :])
-                    nc.vector.tensor_scalar(
-                        out=negm0[:], in0=mvc[:, 0:1], scalar1=-1.0, scalar2=None, op0=ALU.mult
-                    )
-            else:
-                if ci < CH - 1:
-                    nc.scalar.activation(
-                        out=junk[:], in_=src, func=ACT.Copy, accum_out=csum[:, ci : ci + 1]
-                    )
-                cell_square(ci)
-
-        def vector_cell_stats():
-            nc.vector.bn_aggr(out=mvc[:], in_=st_c[:].rearrange("p k s -> p (k s)"))
-            nc.vector.tensor_scalar(out=csum[:, 0:1], in0=mvc[:, 0:1], scalar1=float(nv), scalar2=None, op0=ALU.mult)
-            nc.vector.tensor_tensor(out=dlt[:], in0=mvc[:, 0:1], in1=negm0[:], op=ALU.add)
-            nc.vector.tensor_tensor(out=dlt[:], in0=dlt[:], in1=dlt[:], op=ALU.mult)
-            nc.vector.tensor_tensor(out=dlt[:], in0=dlt[:], in1=mvc[:, 1:2], op=ALU.add)
-            nc.vector.tensor_scalar(out=csq[:, 0:1], in0=dlt[:], scalar1=float(nv), scalar2=None, op0=ALU.mult)
 
         def cell_square(ci):
             nc.scalar.activation(
@@ -498,19 +486,55 @@ def tile_lstmcell_t_kernel(
                 accum_out=csq[:, ci : ci + 1],
             )
 
+        def cell_stats(ci):
+            if ci in vstat:
+                k = vstat.index(ci)
+                nc.vector.bn_stats(out=st_c[:, k, :], in_=gate[0][:, cols(ci)])
+                if k == 0:
+                    nc.vector.bn_aggr(out=mvc[:], in_=st_c[:, 0, :])
+                    nc.vector.tensor_scalar(
+                        out=negm0[:], in0=mvc[:, 0:1], scalar1=-1.0, scalar2=None, op0=ALU.mult
+                    )
+            else:
+                nc.scalar.activation(
+                    out=junk[:], in_=gate[0][:, cols(ci)], func=ACT.Copy, accum_out=csum[:, ci : ci + 1]
+                )
+                cell_square(ci)
+
+        def vector_stats(step):
+            if step == 0:
+                nc.vector.bn_aggr(out=mvc[:], in_=st_c[:].rearrange("p k s -> p (k s)"))
+            if step == 1:
+                nc.vector.tensor_tensor(out=dlt[:], in0=mvc[:, 0:1], in1=negm0[:], op=ALU.add)
+            if step == 2:
+                nc.vector.tensor_tensor(out=dlt[:], in0=dlt[:], in1=dlt[:], op=ALU.mult)
+                nc.vector.tensor_scalar(
+                    out=csum[:, 0:1], in0=mvc[:, 0:1], scalar1=float(nv), scalar2=None, op0=ALU.mult
+                )
+            if step == 3:
+                nc.vector.tensor_tensor(out=dlt[:], in0=dlt[:], in1=mvc[:, 1:2], op=ALU.add)
+            if step == 4:
+                nc.vector.tensor_scalar(
+                    out=csq[:, 0:1], in0=dlt[:], scalar1=float(nv), scalar2=None, op0=ALU.mult
+                )
+
         for ci in range(CH):
-            gate_block(ci, 0)
-            gate_block(ci, 1)
-            gate_block(ci, 3)
-            cell_products(ci)
-            if ci >= OLAG:
-                gate_block(ci - OLAG, 2)
-            if ci >= 3:
-                cell_stats(ci - 3)
+            for k, (jb, tag) in enumerate(((0, "m0"), (1, "m1"), (3, "m3"))):
+                gate_block(ci, jb, tag)
+                if ci == CH - 1:
+                    vector_stats(k)
+            if ci >= 1:
+                forget_product(ci - 1)
+                input_product(nc.gpsimd, ci - 1)
+                if ci < CH - 1:
+                    add_on_gpsimd(ci - 1)
+            if ci >= 2:
+                cell_stats(ci - 2)
             if ci + 1 < CH:
                 c_transposed(ci + 1)
-            if ci == 4:
-                load_c(3)
+            q = 2 + HGAP + ci
+            if q < CH:
+                h_transposed(q * TPC, (q + 1) * TPC, ("g", "m2")[ci % 2])
 
         o_bank = {}
 
@@ -521,53 +545,55 @@ def tile_lstmcell_t_kernel(
             return bank
 
         def o_transposed(ci):
-            o_bank[ci] = transposed_f32("m%d" % (ci % 4), gate[2], ci)
+            o_bank[ci] = transposed_f32(("m0", "m1", "g")[ci % 3], gate[2], ci)
 
-        gate_block(CH - 6, 2)
-        cell_stats(CH - 3)
-        last_cell_add(CH - 1)
-        vector_cell_stats()
-        gate_block(CH - 5, 2)
-        gate_block(CH - 4, 2)
-        cell_stats(CH - 2)
-        cell_stats(CH - 1)
-        gate_block(CH - 3, 2)
         s1c = small("s1c", 1)
+        s2c = small("s2c", 1)
+        negmean = small("negmean", 1)
+        ve_c = small("ve_c", 1)
+        rstd_c = small("rstd_c", 1)
+        a_c = small("a_c", 1)
+        k_c = small("k_c", 1)
+        vector_stats(3)
+        add_on_vector(CH - 2)
+        vector_stats(4)
+        forget_product(CH - 1)
+        input_product(nc.vector, CH - 1)
+        add_on_vector(CH - 1)
+        cell_square(CH - 2)
+        cell_square(CH - 1)
+        o_gate(0)
         nc.vector.reduce_sum(out=s1c[:], in_=csum[:], axis=AX.X)
+        nc.vector.reduce_sum(out=s2c[:], in_=csq[:, 0 : CH - 1], axis=AX.X)
         nc.vector.scalar_tensor_tensor(
             out=dlt[:], in0=s1c[:], scalar=1.0 / B, in1=negm0[:], op0=ALU.mult, op1=ALU.add
         )
-        nc.vector.tensor_tensor(out=dlt[:], in0=dlt[:], in1=dlt[:], op=ALU.mult)
-        s2c = small("s2c", 1)
-        nc.vector.reduce_sum(out=s2c[:], in_=csq[:], axis=AX.X)
-        ve_c = small("ve_c", 1)
-        nc.vector.scalar_tensor_tensor(
-            out=ve_c[:], in0=s2c[:], scalar=1.0 / B, in1=dlt[:], op0=ALU.mult, op1=ALU.subtract
-        )
-        nc.vector.tensor_scalar(out=ve_c[:], in0=ve_c[:], scalar1=0.0, scalar2=EPS, op0=ALU.max, op1=ALU.add)
-        rstd_c = small("rstd_c", 1)
-        nc.gpsimd.tensor_tensor(out=rstd_c[:], in0=ve_c[:], in1=neghalf[:, 0:1], op=ALU.pow)
-        negmean = small("negmean", 1)
         nc.vector.tensor_scalar(out=negmean[:], in0=s1c[:], scalar1=-1.0 / B, scalar2=None, op0=ALU.mult)
-        gate_block(CH - 2, 2)
-        gate_block(CH - 1, 2)
+        nc.vector.tensor_tensor(out=dlt[:], in0=dlt[:], in1=dlt[:], op=ALU.mult)
+        nc.vector.tensor_scalar(out=s2c[:], in0=s2c[:], scalar1=1.0 / B, scalar2=EPS, op0=ALU.mult, op1=ALU.add)
+        nc.vector.tensor_tensor(out=s2c[:], in0=s2c[:], in1=dlt[:], op=ALU.subtract)
+        nc.vector.scalar_tensor_tensor(
+            out=ve_c[:], in0=csq[:, CH - 1 : CH], scalar=1.0 / B, in1=s2c[:], op0=ALU.mult, op1=ALU.add
+        )
+        nc.gpsimd.tensor_tensor(out=rstd_c[:], in0=ve_c[:], in1=neghalf[:, 0:1], op=ALU.pow)
+        for ci in range(1, OGAP):
+            o_gate(ci)
         o_transposed(0)
-        o_transposed(1)
-        a_c = small("a_c", 1)
         nc.vector.tensor_tensor(out=a_c[:], in0=par[:, 20:21], in1=rstd_c[:], op=ALU.mult)
-        k_c = small("k_c", 1)
         nc.vector.scalar_tensor_tensor(
             out=k_c[:], in0=a_c[:], scalar=negmean[:], in1=par[:, 21:22], op0=ALU.mult, op1=ALU.add
         )
 
         for ci in range(CH):
-            nc.gpsimd.tensor_scalar(
+            (nc.vector if ci < AV else nc.gpsimd).tensor_scalar(
                 out=gate[1][:, cols(ci)], in0=gate[0][:, cols(ci)], scalar1=a_c[:], scalar2=k_c[:],
                 op0=ALU.mult, op1=ALU.add,
             )
-            cbank = transposed_f32(("ta", "tb", "th", "g")[ci % 4], gate[1], ci)
-            if ci + 2 < CH:
-                o_transposed(ci + 2)
+            if ci + OGAP < CH:
+                o_combine(ci + OGAP)
+            cbank = transposed_f32(("ta", "tb", "th")[ci % 3], gate[1], ci)
+            if ci + 1 < CH:
+                o_transposed(ci + 1)
             tanh_c = gate[3][:, cols(ci)].rearrange("p (t h) -> p t h", t=TPC)
             nc.scalar.activation(out=tanh_c, in_=cbank[:], func=ACT.Tanh)
             c_out = late.tile([P, TPC, P], F32, tag="c_out", bufs=3, name="c_out")
@@ -576,6 +602,8 @@ def tile_lstmcell_t_kernel(
             else:
                 nc.vector.tensor_copy(out=c_out[:], in_=cbank[:])
             nc.sync.dma_start(out=outv[0][:, ci * TPC : (ci + 1) * TPC, :], in_=c_out[:])
+            if ci + OGAP < CH:
+                squash(ci + OGAP, 2)
             h_out = late.tile([P, TPC, P], F32, tag="h_out", bufs=3, name="h_out")
             nc.vector.tensor_tensor(out=h_out[:], in0=o_bank[ci][:], in1=tanh_c, op=ALU.mult)
             nc.sync.dma_start(out=outv[1][:, ci * TPC : (ci + 1) * TPC, :], in_=h_out[:])

@@ -22,16 +22,24 @@ CW = TPC * P
 EPS = 1e-5
 DT = TPC + 1
 D0 = 3
-GPI = 6
+GPI = 7
 HG = 16
 HPAD = 144
 GW = P + 2
-GCH = 12
-SX = 14
-HGAP = 14
-OGAP = 3
+GCH = 11
+SX = 15
+HGAP = 10
+HLAG = 0
+GB = 2
+QP = 2
+OGAP = 4
+OX = 0
+OA = 1
+OB = 4
+VADD = (4, 8, 12, 14, 15)
+OM = 0
+SC = 0
 AV = 1
-CST = 2
 JB_ORDER = (0, 3, 1, 2)
 FLOPS = 2 * B * I * NB * H + 2 * B * H * NB * H
 
@@ -66,18 +74,17 @@ def tile_lstmcell_t_kernel(
         ident_b = keep.tile([P, P], BF16)
         rows = keep.tile([P, P], BF16)
         par = keep.tile([P, 24], F32)
-        gs = keep.tile([P, GW], F32)
+        gs = keep.tile([P, GW + P], F32)
         st_ih = keep.tile([P, NB - 1, CH, 6], F32)
-        st_g = keep.tile([P, 2 + 6 * (1 + CH - GCH)], F32)
-        gsum = keep.tile([P, GCH], F32)
-        gacc = keep.tile([P, CW], F32)
+        gsum = keep.tile([P, CH], F32)
+        gsq = keep.tile([P, 1 + CH - GCH], F32)
         gred = keep.tile([P, 2], F32)
-        gtmp = keep.tile([P, 2], F32)
         hsum = keep.tile([P, 2], F32)
         sq_dir = keep.tile([P, 2, NB], F32)
         csum = keep.tile([P, CH], F32)
         csq = keep.tile([P, CH], F32)
-        junk = keep.tile([P, CW], BF16)
+        csq_last = keep.tile([P, 1], F32)
+        junk = keep.tile([P, 2 * CW], BF16)
         prod = keep.tile([P, NB, P], F32)
         neghalf = keep.tile([P, NB], F32)
         warm = keep.tile([P, 1], F32)
@@ -108,6 +115,9 @@ def tile_lstmcell_t_kernel(
             )
             return acc
 
+        BD = (TILES - DT) * P
+        BL = (CH - 1) * CW
+
         nc.vector.memset(warm[:], 0.0)
         nc.scalar.activation(out=warm[:], in_=warm[:], func=ACT.Sigmoid)
         make_identity(nc, ident_f[:])
@@ -116,7 +126,6 @@ def tile_lstmcell_t_kernel(
         nc.vector.memset(csum[:], 0.0)
         nc.vector.memset(csq[:], 0.0)
         nc.vector.memset(neghalf[:], -0.5)
-        nc.vector.memset(st_g[:, 0:8], 0.5 * GCH * CW)
         for g in range(TILES // HG):
             nc.vector.memset(h_nat[g][:, :, H:HPAD], 1.0)
 
@@ -128,9 +137,13 @@ def tile_lstmcell_t_kernel(
             scales = {}
             acc_ih = {}
 
-            def load_x(ci):
+            def load_x(ci, pieces=1):
                 x_sb[ci] = stage.tile([P, TPC, I], BF16, tag="xs", bufs=4, name="x_sb")
-                nc.sync.dma_start(out=x_sb[ci][:], in_=xv[:, ci * TPC : (ci + 1) * TPC, :])
+                n = TPC // pieces
+                for k in range(0, TPC, n):
+                    nc.sync.dma_start(
+                        out=x_sb[ci][:, k : k + n, :], in_=xv[:, ci * TPC + k : ci * TPC + k + n, :]
+                    )
 
             def load_h(g):
                 nc.sync.dma_start(out=h_nat[g][:, :, 0:H], in_=hv[:, g * HG : (g + 1) * HG, :])
@@ -180,49 +193,49 @@ def tile_lstmcell_t_kernel(
                     )
                     acc_ih[ci][jb] = acc
 
+            def square_ih(ci):
+                nc.scalar.activation(
+                    out=junk[:, 0:CW], in_=acc_ih[ci][3][:], func=ACT.Square, accum_out=gsq[:, 1 + ci - GCH : 2 + ci - GCH]
+                )
+
             def copy_ih(ci):
                 for jb in JB_ORDER:
-                    if jb == 3 and ci < GCH:
+                    if jb == 3:
                         nc.scalar.activation(
                             out=gate[jb][:, cols(ci)], in_=acc_ih[ci][jb][:], func=ACT.Copy,
                             accum_out=gsum[:, ci : ci + 1],
                         )
+                        if ci >= GCH:
+                            square_ih(ci)
                     else:
                         nc.scalar.copy(out=gate[jb][:, cols(ci)], in_=acc_ih[ci][jb][:])
 
-            def stat_ih(ci, jb):
-                if jb < 3:
-                    nc.vector.bn_stats(out=st_ih[:, jb, ci, :], in_=gate[jb][:, cols(ci)])
-                elif ci >= GCH:
-                    k = 8 + 6 * (ci - GCH)
-                    nc.vector.bn_stats(out=st_g[:, k : k + 6], in_=gate[jb][:, cols(ci)])
-                else:
-                    src = gate[jb][:, cols(ci)]
-                    if ci == 0:
-                        nc.gpsimd.tensor_tensor(out=gacc[:], in0=src, in1=src, op=ALU.mult)
-                    else:
-                        sq = stage.tile([P, CW], F32, tag="gsq", bufs=2, name="gsq")
-                        nc.gpsimd.tensor_tensor(out=sq[:], in0=src, in1=src, op=ALU.mult)
-                        nc.gpsimd.tensor_tensor(out=gacc[:], in0=gacc[:], in1=sq[:], op=ALU.add)
+            squares = {}
 
-            def stat_g_record():
-                n = GCH * CW
-                nc.vector.reduce_sum(out=gred[:, 0:1], in_=gsum[:], axis=AX.X)
-                nc.vector.reduce_sum(out=gred[:, 1:2], in_=gacc[:], axis=AX.X)
-                for k in (3, 6):
-                    nc.gpsimd.tensor_scalar(
-                        out=st_g[:, k : k + 1], in0=gred[:, 0:1], scalar1=1.0 / n, scalar2=0.0, op0=ALU.mult, op1=ALU.add
+            def on_gpsimd(ci, jb):
+                return ci < GCH and jb == 3
+
+            def add_squares(ci, last):
+                for t in range(TPC):
+                    nc.tensor.matmul(
+                        out=gram[:, GW:], lhsT=squares[ci][:, t * P : (t + 1) * P], rhs=ident_f[:],
+                        start=False, stop=(last and t == TPC - 1), is_transpose=True,
                     )
-                nc.gpsimd.tensor_tensor(out=gtmp[:, 0:1], in0=gred[:, 0:1], in1=st_g[:, 3:4], op=ALU.mult)
-                nc.gpsimd.tensor_tensor(out=gtmp[:, 1:2], in0=gred[:, 1:2], in1=gtmp[:, 0:1], op=ALU.subtract)
-                for k in (4, 7):
-                    nc.gpsimd.tensor_scalar(
-                        out=st_g[:, k : k + 1], in0=gtmp[:, 1:2], scalar1=0.5, scalar2=0.0, op0=ALU.mult, op1=ALU.add
-                    )
+
+            def stat_ih(ci, jb):
+                src = acc_ih[ci][jb][:] if ci == CH - 1 else gate[jb][:, cols(ci)]
+                if on_gpsimd(ci, jb):
+                    sq = stage.tile([P, CW], F32, tag="gsq", bufs=GB, name="gsq")
+                    nc.gpsimd.tensor_tensor(out=sq[:], in0=src, in1=src, op=ALU.mult)
+                    squares[ci] = sq
+                elif jb < 3:
+                    nc.vector.bn_stats(out=st_ih[:, jb, ci, :], in_=src)
 
             w_sb = stage.tile([P, NB, I], BF16, tag="xs", bufs=4, name="w_sb")
-            nc.sync.dma_start(out=w_sb[:], in_=w_ih.rearrange("(jb m) k -> m jb k", m=P))
-            load_x(0)
+            wv = w_ih.rearrange("(jb m) k -> m jb k", m=P)
+            for half in (slice(0, 2), slice(2, 4)):
+                nc.sync.dma_start(out=w_sb[:, half, :], in_=wv[:, half, :])
+            load_x(0, 2)
             load_x(1)
             for v, vec in enumerate((b, g_ih, b_ih, g_hh, b_hh)):
                 nc.sync.dma_start(
@@ -235,16 +248,16 @@ def tile_lstmcell_t_kernel(
 
             t1("w", w_sb)
             load_x(3)
-            load_h(0)
+            load_h(TILES // HG - 1)
             t1(0, x_sb[0], ("th", "g"))
             load_x(4)
             new_grp("w")
             evac("w", 0, True)
-            evac("w", 1, False)
-            nc.vector.quantize_mx(out=w_codes[:].bitcast(FP8X4), scales=w_scales[:], in_=grp["w"][:])
+            evac("w", 1, True)
             new_grp(0)
-            evac(0, 0, True)
-            evac(0, 1, False)
+            evac(0, 0, False)
+            nc.vector.quantize_mx(out=w_codes[:].bitcast(FP8X4), scales=w_scales[:], in_=grp["w"][:])
+            evac(0, 1, True)
             quant(0)
             t1(1, x_sb[1])
             load_x(5)
@@ -297,28 +310,29 @@ def tile_lstmcell_t_kernel(
                     evac(nxt, 0, True)
                     evac(nxt, 1, nxt >= SX)
                 if ci >= 1:
-                    stat_ih(ci - 1, 0)
+                    for jb in range(QP):
+                        stat_ih(ci - 1, jb)
                 if nxt < CH:
                     quant(nxt)
                 if D0 <= ci < D0 + NB:
-                    dacc = hh_matmul(0, CW, ci - D0, "th")
-                    nc.vector.tensor_copy(out=hh_dir[:, ci - D0, 0:CW], in_=dacc[:])
+                    dacc = hh_matmul(BL, B, ci - D0, "th")
+                    nc.vector.tensor_copy(out=hh_dir[:, ci - D0, BL - BD :], in_=dacc[:])
                 if ci == D0 + NB:
                     dacc = psum.tile([P, NB, P], F32, tag="th", name="dacc")
                     for jb in range(NB):
                         nc.tensor.matmul(
-                            out=dacc[:, jb, :], lhsT=whhT_b[:, blk(jb)], rhs=hT[:, CW : DT * P], start=True, stop=True
+                            out=dacc[:, jb, :], lhsT=whhT_b[:, blk(jb)], rhs=hT[:, BD:BL], start=True, stop=True
                         )
-                    nc.vector.tensor_copy(out=hh_dir[:, :, CW : DT * P], in_=dacc[:])
+                    nc.vector.tensor_copy(out=hh_dir[:, :, 0 : BL - BD], in_=dacc[:])
                 if ci >= 1:
-                    for jb in range(1, NB):
+                    for jb in range(QP, NB):
                         stat_ih(ci - 1, jb)
                 if ci + 2 < CH:
                     t1(ci + 2, x_sb[ci + 2])
                     if ci + 6 < CH:
                         load_x(ci + 6)
                 if ci in (0, 2, 4):
-                    load_h(ci // 2 + 1)
+                    load_h(ci // 2)
                 if 8 <= ci < 12:
                     load_c(ci - 8)
                 if ci == 1:
@@ -328,38 +342,42 @@ def tile_lstmcell_t_kernel(
                     pt = psum.tile([P, P], BF16, tag="th", name="pt")
                     nc.tensor.transpose(pt[:], rows[:], ident_b[:])
                     nc.vector.tensor_copy(out=par[:], in_=pt[:, 0:24])
-                if ci == CH - 2:
-                    stat_g_record()
+                if ci == 14:
+                    nc.vector.reduce_sum(out=gsq[:, 0:1], in_=turned[:], axis=AX.X)
                 if ci == CH - 1:
                     nc.vector.reciprocal(out=ratio[:], in_=sc[:])
                     nc.vector.tensor_tensor(out=ratio[:], in0=ratio[:], in1=par[:, 4:8], op=ALU.mult)
-                copy_ih(ci)
+                if ci < CH - 1:
+                    copy_ih(ci)
                 if ci == 2:
-                    for k, (tag, s0, s9) in enumerate((("th", 0, TPC), ("g", TPC, DT))):
+                    for k, (tag, s0, s9) in enumerate((("th", TILES - TPC, TILES), ("g", TILES - DT, TILES - TPC))):
                         ht = transpose_bf16(tag, [htile(s)[:, 0:H] for s in range(s0, s9)])
                         nc.scalar.activation(
                             out=hT[:, s0 * P : s9 * P], in_=ht[:, 0 : (s9 - s0) * P], func=ACT.Copy,
                             accum_out=hsum[:, k : k + 1],
                         )
-                s0 = DT + GPI * (ci - 2)
-                if ci >= 2 and s0 < TILES:
+                s0 = GPI * (ci - 2)
+                if ci >= 2 and s0 < TILES - DT:
                     if ci == 2:
-                        gram = psum.tile([P, GW], F32, tag="g", name="gram")
-                    for s in range(s0, min(s0 + GPI, TILES)):
+                        gram = psum.tile([P, GW + P], F32, tag="g", name="gram")
+                    for s in range(s0, min(s0 + GPI, TILES - DT)):
                         nc.tensor.matmul(
-                            out=gram[:], lhsT=htile(s)[:, 0:H], rhs=htile(s)[:, 0:GW],
-                            start=(s == DT), stop=(s == TILES - 1),
+                            out=gram[:, 0:GW], lhsT=htile(s)[:, 0:H], rhs=htile(s)[:, 0:GW], start=(s == 0), stop=False
                         )
+                if 2 <= ci:
+                    for k in ((0, 1) if ci == 2 else (ci - 1,)):
+                        if k < GCH:
+                            add_squares(k, k == GCH - 1)
                 if nxt < CH:
                     mx(nxt)
                 if D0 <= ci < D0 + NB:
                     nc.scalar.activation(
-                        out=junk[:], in_=dacc[:], func=ACT.Square, accum_out=sq_dir[:, 0, ci - D0 : ci - D0 + 1]
+                        out=junk[:, 0:CW], in_=dacc[:], func=ACT.Square, accum_out=sq_dir[:, 0, ci - D0 : ci - D0 + 1]
                     )
                 if ci == D0 + NB:
                     for jb in range(NB):
                         nc.scalar.activation(
-                            out=junk[:, 0:P], in_=dacc[:, jb, :], func=ACT.Square, accum_out=sq_dir[:, 1, jb : jb + 1]
+                            out=junk[:, blk(jb)], in_=dacc[:, jb, :], func=ACT.Square, accum_out=sq_dir[:, 1, jb : jb + 1]
                         )
                 if ci == 11:
                     nc.vector.tensor_copy(out=gs[:], in_=gram[:])
@@ -373,7 +391,7 @@ def tile_lstmcell_t_kernel(
                         y = psum.tile([P, 2, GW], F32, tag=tag, name="y")
                         for a in range(2):
                             nc.tensor.matmul(
-                                out=y[:, a, :], lhsT=whhT_f[:, blk(2 * pair + a)], rhs=gs[:], start=True, stop=True
+                                out=y[:, a, :], lhsT=whhT_f[:, blk(2 * pair + a)], rhs=gs[:, 0:GW], start=True, stop=True
                             )
                         ys.append(y)
                 if ci == 13:
@@ -385,58 +403,97 @@ def tile_lstmcell_t_kernel(
                         nc.vector.tensor_copy(out=s1[:, 2 * pair : 2 * pair + 2], in_=ys[pair][:, :, P])
                     nc.vector.reduce_sum(out=t2[:], in_=prod[:], axis=AX.X)
                     hh_small_ops()
+                    turned = psum.tile([P, P], F32, tag="th", name="turned")
+                    nc.tensor.transpose(turned[:], gs[:, GW:], ident_f[:])
 
         late = ctx.enter_context(tc.tile_pool(name="late", bufs=3))
-        for jb in range(NB):
-            stat_ih(CH - 1, jb)
-        for jb in range(NB):
-            records = st_g[:, 2:] if jb == 3 else st_ih[:, jb, :, :].rearrange("p c s -> p (c s)")
-            nc.vector.bn_aggr(out=mv[:, jb, :], in_=records)
         ve_ih = small("ve_ih")
-        nc.vector.tensor_scalar(out=ve_ih[:], in0=mv[:, :, 1], scalar1=EPS, scalar2=None, op0=ALU.add)
         rstd_ih = small("rstd_ih")
-        nc.gpsimd.tensor_tensor(out=rstd_ih[:], in0=ve_ih[:], in1=neghalf[:], op=ALU.pow)
         am = small("am")
-        nc.vector.tensor_tensor(out=am[:], in0=par[:, 4:8], in1=mv[:, :, 0], op=ALU.mult)
+
+        def ih_scale(first, last):
+            s = slice(first, last)
+            nc.vector.tensor_scalar(
+                out=ve_ih[:, s], in0=mv[:, s, 1], scalar1=0.0, scalar2=EPS, op0=ALU.max, op1=ALU.add
+            )
+            nc.gpsimd.tensor_tensor(out=rstd_ih[:, s], in0=ve_ih[:, s], in1=neghalf[:, s], op=ALU.pow)
+            nc.vector.tensor_tensor(out=am[:, s], in0=par[:, 4 + first : 4 + last], in1=mv[:, s, 0], op=ALU.mult)
+
+        def ih_ratio(first, last):
+            s = slice(first, last)
+            nc.vector.tensor_tensor(out=ratio[:, s], in0=ratio[:, s], in1=rstd_ih[:, s], op=ALU.mult)
+
+        def ih_bias(first, last):
+            s = slice(first, last)
+            nc.vector.tensor_tensor(out=am[:, s], in0=am[:, s], in1=rstd_ih[:, s], op=ALU.mult)
+            nc.vector.tensor_tensor(out=cst[:, s], in0=cst[:, s], in1=am[:, s], op=ALU.subtract)
+
+        nc.scalar.activation(out=junk[:, CW:], in_=acc_ih[CH - 1][3][:], func=ACT.Copy, accum_out=gsum[:, CH - 1 : CH])
+        square_ih(CH - 1)
+        stat_ih(CH - 1, 0)
+        stat_ih(CH - 1, 1)
+        nc.vector.bn_aggr(out=mv[:, 0, :], in_=st_ih[:, 0, :, :].rearrange("p c s -> p (c s)"))
+        nc.vector.bn_aggr(out=mv[:, 1, :], in_=st_ih[:, 1, :, :].rearrange("p c s -> p (c s)"))
+        ih_scale(0, 2)
+        stat_ih(CH - 1, 2)
+        nc.vector.reduce_sum(out=gred[:, 0:1], in_=gsum[:], axis=AX.X)
+        nc.vector.reduce_sum(out=gred[:, 1:2], in_=gsq[:], axis=AX.X)
+        nc.vector.tensor_scalar(
+            out=mv[:, 3, 0:1], in0=gred[:, 0:1], scalar1=1.0 / B, scalar2=None, op0=ALU.mult
+        )
+        ih_ratio(0, 2)
+        nc.vector.tensor_tensor(out=gred[:, 0:1], in0=mv[:, 3, 0:1], in1=mv[:, 3, 0:1], op=ALU.mult)
+        nc.vector.bn_aggr(out=mv[:, 2, :], in_=st_ih[:, 2, :, :].rearrange("p c s -> p (c s)"))
+        nc.vector.scalar_tensor_tensor(
+            out=mv[:, 3, 1:2], in0=gred[:, 1:2], scalar=1.0 / B, in1=gred[:, 0:1], op0=ALU.mult, op1=ALU.subtract
+        )
+        ih_scale(2, 4)
 
         c_bank = {}
 
         def c_transposed(q):
             tiles = [c_nat[q // TPC][:, (q % TPC) * TPC + t, :] for t in range(TPC)]
-            c_bank[q] = transpose_bf16(("ta", "tb", "th")[q % 3], tiles)
+            c_bank[q] = transpose_bf16(("ta", "tb", "th")[len(c_bank) % 3], tiles)
 
         def h_transposed(s0, s9, tag):
             ht = transpose_bf16(tag, [htile(s)[:, 0:H] for s in range(s0, s9)])
             nc.scalar.copy(out=hT[:, s0 * P : s9 * P], in_=ht[:, 0 : (s9 - s0) * P])
 
-        h_transposed(DT, 2 * TPC, "m2")
-        for q in range(2, 2 + HGAP):
-            h_transposed(q * TPC, (q + 1) * TPC, ("g", "tb", "th", "m2")[q % 4])
-        c_transposed(0)
+        c_transposed(CH - 1)
+        def h_chunk(q, tag):
+            h_transposed(q * TPC, min((q + 1) * TPC, TILES - DT), tag)
 
-        nc.vector.tensor_tensor(out=ratio[:], in0=ratio[:], in1=rstd_ih[:], op=ALU.mult)
+        for q in [CH - 2] + list(range(HGAP)):
+            h_chunk(q, ("g", "tb", "th")[q % 3])
 
         negm0 = small("negm0", 1)
         dlt = small("dlt", 1)
         mvc = small("mvc", 2)
-        st_c = keep.tile([P, (CH - 3) // CST + 1, 6], F32)
+        st_c = keep.tile([P, 6], F32)
+        part = keep.tile([P, P], F32)
+
+        ahead = {}
 
         def combine(ci, jb, tag):
             b0, b9 = ci * CW, (ci + 1) * CW
             pieces = []
-            if b0 < DT * P:
-                pieces.append((b0, min(b9, DT * P), hh_dir[:, jb, b0 : min(b9, DT * P)]))
-            if b9 > DT * P:
-                b1 = max(b0, DT * P)
-                pieces.append((b1, b9, hh_matmul(b1, b9, jb, tag)[:, 0 : b9 - b1]))
-            for b1, b2, hh in pieces:
+            if b0 < BD:
+                b1 = min(b9, BD)
+                hh = ahead.pop((ci, jb)) if (ci, jb) in ahead else hh_matmul(b0, b1, jb, tag)
+                pieces.append((b0, b1, gate[jb][:, b0:b1], hh[:, 0 : b1 - b0]))
+            if b9 > BD:
+                b1 = max(b0, BD)
+                ih = acc_ih[ci][jb][:] if ci == CH - 1 else gate[jb][:, b1:b9]
+                pieces.append((b1, b9, ih, hh_dir[:, jb, b1 - BD : b9 - BD]))
+            for b1, b2, ih, hh in pieces:
                 nc.vector.scalar_tensor_tensor(
-                    out=gate[jb][:, b1:b2], in0=gate[jb][:, b1:b2], scalar=ratio[:, jb : jb + 1], in1=hh,
-                    op0=ALU.mult, op1=ALU.add,
+                    out=gate[jb][:, b1:b2], in0=ih, scalar=ratio[:, jb : jb + 1], in1=hh, op0=ALU.mult, op1=ALU.add
                 )
-            if ci == 0 and jb == 0:
-                nc.vector.tensor_tensor(out=am[:], in0=am[:], in1=rstd_ih[:], op=ALU.mult)
-                nc.vector.tensor_tensor(out=cst[:], in0=cst[:], in1=am[:], op=ALU.subtract)
+            if ci == CH - 1 and jb == 0:
+                ih_bias(0, 2)
+            if ci == CH - 1 and jb == 1:
+                ih_ratio(2, 4)
+                ih_bias(2, 4)
 
         def squash(ci, jb):
             nc.scalar.activation(
@@ -448,6 +505,9 @@ def tile_lstmcell_t_kernel(
         def gate_block(ci, jb, tag):
             combine(ci, jb, tag)
             squash(ci, jb)
+
+        def o_ahead(ci):
+            ahead[(ci, 2)] = hh_matmul(ci * CW, (ci + 1) * CW, 2, ("m2", "m3")[ci % 2])
 
         def o_combine(ci):
             combine(ci, 2, ("m2", "m3")[ci % 2])
@@ -477,64 +537,85 @@ def tile_lstmcell_t_kernel(
                 op0=ALU.mult, op1=ALU.add, accum_out=csum[:, ci : ci + 1],
             )
 
-        vstat = [ci for ci in range(CH - 2) if ci % CST == 0]
-        nv = len(vstat) * CW
+        order = [CH - 1, CH - 2] + list(range(CH - 2))
+        first, vset = order[0], {order[n] for n in VADD}
+        pe_chunks = [ci for ci in order[1:] if ci not in vset]
+        nv = CW
 
         def cell_square(ci):
             nc.scalar.activation(
-                out=junk[:], in_=gate[0][:, cols(ci)], func=ACT.Square, bias=negm0[:], scale=1.0,
-                accum_out=csq[:, ci : ci + 1],
+                out=junk[:, 0:CW], in_=gate[0][:, cols(ci)], func=ACT.Square, bias=negm0[:], scale=1.0,
+                accum_out=csq_last[:] if ci == order[-1] else csq[:, ci : ci + 1],
             )
 
+        sums = {}
+
         def cell_stats(ci):
-            if ci in vstat:
-                k = vstat.index(ci)
-                nc.vector.bn_stats(out=st_c[:, k, :], in_=gate[0][:, cols(ci)])
-                if k == 0:
-                    nc.vector.bn_aggr(out=mvc[:], in_=st_c[:, 0, :])
-                    nc.vector.tensor_scalar(
-                        out=negm0[:], in0=mvc[:, 0:1], scalar1=-1.0, scalar2=None, op0=ALU.mult
-                    )
-            else:
-                nc.scalar.activation(
-                    out=junk[:], in_=gate[0][:, cols(ci)], func=ACT.Copy, accum_out=csum[:, ci : ci + 1]
+            if ci == first:
+                nc.vector.bn_stats(out=st_c[:], in_=gate[0][:, cols(ci)])
+                nc.vector.bn_aggr(out=mvc[:], in_=st_c[:])
+                nc.vector.tensor_scalar(out=negm0[:], in0=mvc[:, 0:1], scalar1=-1.0, scalar2=None, op0=ALU.mult)
+                return
+            cell_square(ci)
+
+        def cell_sum(ci):
+            if ci == pe_chunks[0]:
+                sums["acc"] = psum.tile([P, P], F32, tag="g", name="sums")
+            for t in range(TPC):
+                nc.tensor.matmul(
+                    out=sums["acc"][:], lhsT=gate[0][:, ci * CW + t * P : ci * CW + (t + 1) * P], rhs=ident_f[:],
+                    start=(ci == pe_chunks[0] and t == 0), stop=(ci == pe_chunks[-1] and t == TPC - 1),
+                    is_transpose=True,
                 )
-                cell_square(ci)
+
+        def sums_out():
+            nc.vector.tensor_copy(out=part[:], in_=sums["acc"][:])
+            sums["turned"] = psum.tile([P, P], F32, tag="g", name="turned")
+            nc.tensor.transpose(sums["turned"][:], part[:], ident_f[:])
+
+        def sums_reduced():
+            k = pe_chunks[0]
+            nc.vector.reduce_sum(out=csum[:, k : k + 1], in_=sums["turned"][:], axis=AX.X)
 
         def vector_stats(step):
-            if step == 0:
-                nc.vector.bn_aggr(out=mvc[:], in_=st_c[:].rearrange("p k s -> p (k s)"))
             if step == 1:
                 nc.vector.tensor_tensor(out=dlt[:], in0=mvc[:, 0:1], in1=negm0[:], op=ALU.add)
             if step == 2:
                 nc.vector.tensor_tensor(out=dlt[:], in0=dlt[:], in1=dlt[:], op=ALU.mult)
                 nc.vector.tensor_scalar(
-                    out=csum[:, 0:1], in0=mvc[:, 0:1], scalar1=float(nv), scalar2=None, op0=ALU.mult
+                    out=csum[:, first : first + 1], in0=mvc[:, 0:1], scalar1=float(nv), scalar2=None, op0=ALU.mult
                 )
             if step == 3:
                 nc.vector.tensor_tensor(out=dlt[:], in0=dlt[:], in1=mvc[:, 1:2], op=ALU.add)
             if step == 4:
                 nc.vector.tensor_scalar(
-                    out=csq[:, 0:1], in0=dlt[:], scalar1=float(nv), scalar2=None, op0=ALU.mult
+                    out=csq[:, first : first + 1], in0=dlt[:], scalar1=float(nv), scalar2=None, op0=ALU.mult
                 )
 
-        for ci in range(CH):
+        for n, ci in enumerate(order):
             for k, (jb, tag) in enumerate(((0, "m0"), (1, "m1"), (3, "m3"))):
                 gate_block(ci, jb, tag)
-                if ci == CH - 1:
-                    vector_stats(k)
-            if ci >= 1:
-                forget_product(ci - 1)
-                input_product(nc.gpsimd, ci - 1)
-                if ci < CH - 1:
-                    add_on_gpsimd(ci - 1)
-            if ci >= 2:
-                cell_stats(ci - 2)
-            if ci + 1 < CH:
-                c_transposed(ci + 1)
-            q = 2 + HGAP + ci
-            if q < CH:
-                h_transposed(q * TPC, (q + 1) * TPC, ("g", "m2")[ci % 2])
+                if n == 6:
+                    vector_stats(k + 1)
+                if n == 7 and k == 0:
+                    vector_stats(4)
+            if n == 0:
+                gate_block(ci, 2, "m2")
+            if n >= 1:
+                forget_product(order[n - 1])
+                input_product(nc.gpsimd, order[n - 1])
+                if order[n - 1] not in vset:
+                    add_on_gpsimd(order[n - 1])
+            if n >= 2 and order[n - 2] in vset:
+                add_on_vector(order[n - 2])
+            if n + 1 < CH:
+                c_transposed(order[n + 1])
+            if n >= 2:
+                cell_stats(order[n - 2])
+            if 4 <= n and order[n - 3] in pe_chunks:
+                cell_sum(order[n - 3])
+            if n + HGAP < CH - 2:
+                h_chunk(n + HGAP, "m2")
 
         o_bank = {}
 
@@ -554,56 +635,87 @@ def tile_lstmcell_t_kernel(
         rstd_c = small("rstd_c", 1)
         a_c = small("a_c", 1)
         k_c = small("k_c", 1)
-        vector_stats(3)
-        add_on_vector(CH - 2)
-        vector_stats(4)
-        forget_product(CH - 1)
-        input_product(nc.vector, CH - 1)
-        add_on_vector(CH - 1)
-        cell_square(CH - 2)
-        cell_square(CH - 1)
+        for ci in range(OA):
+            o_ahead(ci)
+        if order[-3] in pe_chunks:
+            cell_sum(order[-3])
+        add_on_vector(order[-2])
+        forget_product(order[-1])
+        input_product(nc.vector, order[-1])
+        sums_out()
+        add_on_vector(order[-1])
+        cell_square(order[-2])
+        cell_square(order[-1])
         o_gate(0)
+        sums_reduced()
         nc.vector.reduce_sum(out=s1c[:], in_=csum[:], axis=AX.X)
-        nc.vector.reduce_sum(out=s2c[:], in_=csq[:, 0 : CH - 1], axis=AX.X)
+        nc.vector.reduce_sum(out=s2c[:], in_=csq[:], axis=AX.X)
+        o_gate(1)
         nc.vector.scalar_tensor_tensor(
             out=dlt[:], in0=s1c[:], scalar=1.0 / B, in1=negm0[:], op0=ALU.mult, op1=ALU.add
         )
         nc.vector.tensor_scalar(out=negmean[:], in0=s1c[:], scalar1=-1.0 / B, scalar2=None, op0=ALU.mult)
-        nc.vector.tensor_tensor(out=dlt[:], in0=dlt[:], in1=dlt[:], op=ALU.mult)
         nc.vector.tensor_scalar(out=s2c[:], in0=s2c[:], scalar1=1.0 / B, scalar2=EPS, op0=ALU.mult, op1=ALU.add)
+        nc.vector.tensor_tensor(out=dlt[:], in0=dlt[:], in1=dlt[:], op=ALU.mult)
+        if OM:
+            o_gate(2)
         nc.vector.tensor_tensor(out=s2c[:], in0=s2c[:], in1=dlt[:], op=ALU.subtract)
         nc.vector.scalar_tensor_tensor(
-            out=ve_c[:], in0=csq[:, CH - 1 : CH], scalar=1.0 / B, in1=s2c[:], op0=ALU.mult, op1=ALU.add
+            out=ve_c[:], in0=csq_last[:], scalar=1.0 / B, in1=s2c[:], op0=ALU.mult, op1=ALU.add
         )
         nc.gpsimd.tensor_tensor(out=rstd_c[:], in0=ve_c[:], in1=neghalf[:, 0:1], op=ALU.pow)
-        for ci in range(1, OGAP):
+        for ci in range(2 + OM, OGAP):
             o_gate(ci)
-        o_transposed(0)
         nc.vector.tensor_tensor(out=a_c[:], in0=par[:, 20:21], in1=rstd_c[:], op=ALU.mult)
         nc.vector.scalar_tensor_tensor(
             out=k_c[:], in0=a_c[:], scalar=negmean[:], in1=par[:, 21:22], op0=ALU.mult, op1=ALU.add
         )
 
-        for ci in range(CH):
+        def tanh_c(ci):
+            return gate[3][:, cols(ci)].rearrange("p (t h) -> p t h", t=TPC)
+
+        def h_product(ci):
+            h_out = late.tile([P, TPC, P], F32, tag="h_out", bufs=OB, name="h_out")
+            nc.vector.tensor_tensor(out=h_out[:], in0=o_bank[ci][:], in1=tanh_c(ci), op=ALU.mult)
+            nc.sync.dma_start(out=outv[1][:, ci * TPC : (ci + 1) * TPC, :], in_=h_out[:])
+
+        c_next = {}
+
+        def cell_normalise(ci):
             (nc.vector if ci < AV else nc.gpsimd).tensor_scalar(
                 out=gate[1][:, cols(ci)], in0=gate[0][:, cols(ci)], scalar1=a_c[:], scalar2=k_c[:],
                 op0=ALU.mult, op1=ALU.add,
             )
-            if ci + OGAP < CH:
-                o_combine(ci + OGAP)
-            cbank = transposed_f32(("ta", "tb", "th")[ci % 3], gate[1], ci)
-            if ci + 1 < CH:
-                o_transposed(ci + 1)
-            tanh_c = gate[3][:, cols(ci)].rearrange("p (t h) -> p t h", t=TPC)
-            nc.scalar.activation(out=tanh_c, in_=cbank[:], func=ACT.Tanh)
-            c_out = late.tile([P, TPC, P], F32, tag="c_out", bufs=3, name="c_out")
-            if ci % 2 == 0:
-                nc.scalar.copy(out=c_out[:], in_=cbank[:])
+
+        def c_next_transposed(ci):
+            c_next[ci] = transposed_f32(("ta", "tb", "th")[ci % 3], gate[1], ci)
+
+        cell_normalise(0)
+        for cj in range(OGAP, OGAP + OX):
+            o_gate(cj)
+        def tanh_next(ci):
+            if ci < CH:
+                cell_normalise(ci)
+                c_next_transposed(ci)
+                nc.scalar.activation(out=tanh_c(ci), in_=c_next[ci][:], func=ACT.Tanh)
+
+        c_next_transposed(0)
+        nc.scalar.activation(out=tanh_c(0), in_=c_next[0][:], func=ACT.Tanh)
+        for ci in range(CH):
+            cj = ci + OGAP + OX
+            if cj < CH - 1:
+                o_combine(cj)
+            tanh_next(ci + 1)
+            o_transposed(ci)
+            c_out = late.tile([P, TPC, P], F32, tag="c_out", bufs=OB, name="c_out")
+            if ci % 2 == 0 or ci < SC:
+                nc.scalar.copy(out=c_out[:], in_=c_next[ci][:])
             else:
-                nc.vector.tensor_copy(out=c_out[:], in_=cbank[:])
+                nc.vector.tensor_copy(out=c_out[:], in_=c_next[ci][:])
             nc.sync.dma_start(out=outv[0][:, ci * TPC : (ci + 1) * TPC, :], in_=c_out[:])
-            if ci + OGAP < CH:
-                squash(ci + OGAP, 2)
-            h_out = late.tile([P, TPC, P], F32, tag="h_out", bufs=3, name="h_out")
-            nc.vector.tensor_tensor(out=h_out[:], in0=o_bank[ci][:], in1=tanh_c, op=ALU.mult)
-            nc.sync.dma_start(out=outv[1][:, ci * TPC : (ci + 1) * TPC, :], in_=h_out[:])
+            if cj < CH - 1:
+                squash(cj, 2)
+            if ci >= HLAG:
+                h_product(ci - HLAG)
+        for ci in range(CH - HLAG, CH):
+            h_product(ci)

@@ -22,18 +22,17 @@ CW = TPC * P
 EPS = 1e-5
 DT = TPC + 1
 D0 = 3
-GPI = 7
+GPI = 6
 HG = 16
 HPAD = 144
 GW = P + 2
 GCH = 11
-SX = 15
+SX = 14
 HGAP = 10
 HLAG = 0
 GB = 2
 QP = 2
 OGAP = 4
-OX = 0
 OA = 1
 OB = 4
 VADD = (4, 8, 12, 14, 15)
@@ -74,7 +73,8 @@ def tile_lstmcell_t_kernel(
         ident_b = keep.tile([P, P], BF16)
         rows = keep.tile([P, P], BF16)
         par = keep.tile([P, 24], F32)
-        gs = keep.tile([P, GW + P], F32)
+        gs = keep.tile([P, GW], F32)
+        gacc = keep.tile([P, CW], F32)
         st_ih = keep.tile([P, NB - 1, CH, 6], F32)
         gsum = keep.tile([P, CH], F32)
         gsq = keep.tile([P, 1 + CH - GCH], F32)
@@ -225,9 +225,13 @@ def tile_lstmcell_t_kernel(
             def stat_ih(ci, jb):
                 src = acc_ih[ci][jb][:] if ci == CH - 1 else gate[jb][:, cols(ci)]
                 if on_gpsimd(ci, jb):
-                    sq = stage.tile([P, CW], F32, tag="gsq", bufs=GB, name="gsq")
-                    nc.gpsimd.tensor_tensor(out=sq[:], in0=src, in1=src, op=ALU.mult)
-                    squares[ci] = sq
+                    if ci == 0:
+                        nc.gpsimd.tensor_tensor(out=gacc[:], in0=src, in1=src, op=ALU.mult)
+                    else:
+                        sq = stage.tile([P, CW], F32, tag="gsq", bufs=GB, name="gsq")
+                        nc.vector.memset(sq[:, 0:1], 0.0)
+                        nc.gpsimd.tensor_tensor(out=sq[:], in0=src, in1=src, op=ALU.mult)
+                        nc.gpsimd.tensor_tensor(out=gacc[:], in0=gacc[:], in1=sq[:], op=ALU.add)
                 elif jb < 3:
                     nc.vector.bn_stats(out=st_ih[:, jb, ci, :], in_=src)
 
@@ -314,6 +318,8 @@ def tile_lstmcell_t_kernel(
                         stat_ih(ci - 1, jb)
                 if nxt < CH:
                     quant(nxt)
+                if ci >= 1 and ci - 1 < GCH:
+                    stat_ih(ci - 1, 3)
                 if D0 <= ci < D0 + NB:
                     dacc = hh_matmul(BL, B, ci - D0, "th")
                     nc.vector.tensor_copy(out=hh_dir[:, ci - D0, BL - BD :], in_=dacc[:])
@@ -325,7 +331,7 @@ def tile_lstmcell_t_kernel(
                         )
                     nc.vector.tensor_copy(out=hh_dir[:, :, 0 : BL - BD], in_=dacc[:])
                 if ci >= 1:
-                    for jb in range(QP, NB):
+                    for jb in range(QP, NB - 1):
                         stat_ih(ci - 1, jb)
                 if ci + 2 < CH:
                     t1(ci + 2, x_sb[ci + 2])
@@ -343,7 +349,7 @@ def tile_lstmcell_t_kernel(
                     nc.tensor.transpose(pt[:], rows[:], ident_b[:])
                     nc.vector.tensor_copy(out=par[:], in_=pt[:, 0:24])
                 if ci == 14:
-                    nc.vector.reduce_sum(out=gsq[:, 0:1], in_=turned[:], axis=AX.X)
+                    nc.vector.reduce_sum(out=gsq[:, 0:1], in_=gacc[:], axis=AX.X)
                 if ci == CH - 1:
                     nc.vector.reciprocal(out=ratio[:], in_=sc[:])
                     nc.vector.tensor_tensor(out=ratio[:], in0=ratio[:], in1=par[:, 4:8], op=ALU.mult)
@@ -359,15 +365,11 @@ def tile_lstmcell_t_kernel(
                 s0 = GPI * (ci - 2)
                 if ci >= 2 and s0 < TILES - DT:
                     if ci == 2:
-                        gram = psum.tile([P, GW + P], F32, tag="g", name="gram")
+                        gram = psum.tile([P, GW], F32, tag="g", name="gram")
                     for s in range(s0, min(s0 + GPI, TILES - DT)):
                         nc.tensor.matmul(
-                            out=gram[:, 0:GW], lhsT=htile(s)[:, 0:H], rhs=htile(s)[:, 0:GW], start=(s == 0), stop=False
+                            out=gram[:, 0:GW], lhsT=htile(s)[:, 0:H], rhs=htile(s)[:, 0:GW], start=(s == 0), stop=(s == TILES - DT - 1)
                         )
-                if 2 <= ci:
-                    for k in ((0, 1) if ci == 2 else (ci - 1,)):
-                        if k < GCH:
-                            add_squares(k, k == GCH - 1)
                 if nxt < CH:
                     mx(nxt)
                 if D0 <= ci < D0 + NB:
@@ -403,8 +405,6 @@ def tile_lstmcell_t_kernel(
                         nc.vector.tensor_copy(out=s1[:, 2 * pair : 2 * pair + 2], in_=ys[pair][:, :, P])
                     nc.vector.reduce_sum(out=t2[:], in_=prod[:], axis=AX.X)
                     hh_small_ops()
-                    turned = psum.tile([P, P], F32, tag="th", name="turned")
-                    nc.tensor.transpose(turned[:], gs[:, GW:], ident_f[:])
 
         late = ctx.enter_context(tc.tile_pool(name="late", bufs=3))
         ve_ih = small("ve_ih")
@@ -691,8 +691,7 @@ def tile_lstmcell_t_kernel(
             c_next[ci] = transposed_f32(("ta", "tb", "th")[ci % 3], gate[1], ci)
 
         cell_normalise(0)
-        for cj in range(OGAP, OGAP + OX):
-            o_gate(cj)
+        o_ahead(OGAP)
         def tanh_next(ci):
             if ci < CH:
                 cell_normalise(ci)
@@ -700,13 +699,15 @@ def tile_lstmcell_t_kernel(
                 nc.scalar.activation(out=tanh_c(ci), in_=c_next[ci][:], func=ACT.Tanh)
 
         c_next_transposed(0)
+        o_transposed(0)
         nc.scalar.activation(out=tanh_c(0), in_=c_next[0][:], func=ACT.Tanh)
         for ci in range(CH):
-            cj = ci + OGAP + OX
+            cj = ci + OGAP
             if cj < CH - 1:
                 o_combine(cj)
             tanh_next(ci + 1)
-            o_transposed(ci)
+            if ci + 1 < CH:
+                o_transposed(ci + 1)
             c_out = late.tile([P, TPC, P], F32, tag="c_out", bufs=OB, name="c_out")
             if ci % 2 == 0 or ci < SC:
                 nc.scalar.copy(out=c_out[:], in_=c_next[ci][:])

@@ -28,14 +28,14 @@ HPAD = 144
 GW = P + 2
 GCH = 11
 SX = 14
-HGAP = 10
+HGAP = 8
 HLAG = 0
 GB = 2
 QP = 2
 OGAP = 4
 OA = 1
 OB = 4
-VADD = (4, 8, 12, 14, 15)
+VADD = (6, 12, 14, 15)
 OM = 0
 SC = 0
 AV = 1
@@ -383,10 +383,10 @@ def tile_lstmcell_t_kernel(
                         )
                 if ci == 11:
                     nc.vector.tensor_copy(out=gs[:], in_=gram[:])
-                    for k in range(2):
-                        nc.vector.tensor_tensor(
-                            out=gs[:, P : P + 1], in0=gs[:, P : P + 1], in1=hsum[:, k : k + 1], op=ALU.add
-                        )
+                    nc.vector.scalar_tensor_tensor(
+                        out=gs[:, P : P + 1], in0=gs[:, P : P + 1], scalar=hsum[:, 0:1], in1=hsum[:, 1:2],
+                        op0=ALU.add, op1=ALU.add,
+                    )
                 if ci == 12:
                     ys = []
                     for pair, tag in enumerate(("th", "g")):
@@ -417,16 +417,19 @@ def tile_lstmcell_t_kernel(
                 out=ve_ih[:, s], in0=mv[:, s, 1], scalar1=0.0, scalar2=EPS, op0=ALU.max, op1=ALU.add
             )
             nc.gpsimd.tensor_tensor(out=rstd_ih[:, s], in0=ve_ih[:, s], in1=neghalf[:, s], op=ALU.pow)
-            nc.vector.tensor_tensor(out=am[:, s], in0=par[:, 4 + first : 4 + last], in1=mv[:, s, 0], op=ALU.mult)
+            nc.vector.scalar_tensor_tensor(
+                out=am[:, s], in0=mv[:, s, 0], scalar=-1.0, in1=par[:, 4 + first : 4 + last], op0=ALU.mult, op1=ALU.mult
+            )
 
         def ih_ratio(first, last):
             s = slice(first, last)
             nc.vector.tensor_tensor(out=ratio[:, s], in0=ratio[:, s], in1=rstd_ih[:, s], op=ALU.mult)
 
-        def ih_bias(first, last):
-            s = slice(first, last)
-            nc.vector.tensor_tensor(out=am[:, s], in0=am[:, s], in1=rstd_ih[:, s], op=ALU.mult)
-            nc.vector.tensor_tensor(out=cst[:, s], in0=cst[:, s], in1=am[:, s], op=ALU.subtract)
+        def ih_bias(jb):
+            s = slice(jb, jb + 1)
+            nc.vector.scalar_tensor_tensor(
+                out=cst[:, s], in0=am[:, s], scalar=rstd_ih[:, s], in1=cst[:, s], op0=ALU.mult, op1=ALU.add
+            )
 
         nc.scalar.activation(out=junk[:, CW:], in_=acc_ih[CH - 1][3][:], func=ACT.Copy, accum_out=gsum[:, CH - 1 : CH])
         square_ih(CH - 1)
@@ -489,11 +492,10 @@ def tile_lstmcell_t_kernel(
                 nc.vector.scalar_tensor_tensor(
                     out=gate[jb][:, b1:b2], in0=ih, scalar=ratio[:, jb : jb + 1], in1=hh, op0=ALU.mult, op1=ALU.add
                 )
-            if ci == CH - 1 and jb == 0:
-                ih_bias(0, 2)
+            if ci == CH - 1:
+                ih_bias(jb)
             if ci == CH - 1 and jb == 1:
                 ih_ratio(2, 4)
-                ih_bias(2, 4)
 
         def squash(ci, jb):
             nc.scalar.activation(
@@ -540,7 +542,6 @@ def tile_lstmcell_t_kernel(
         order = [CH - 1, CH - 2] + list(range(CH - 2))
         first, vset = order[0], {order[n] for n in VADD}
         pe_chunks = [ci for ci in order[1:] if ci not in vset]
-        nv = CW
 
         def cell_square(ci):
             nc.scalar.activation(
@@ -577,28 +578,19 @@ def tile_lstmcell_t_kernel(
             k = pe_chunks[0]
             nc.vector.reduce_sum(out=csum[:, k : k + 1], in_=sums["turned"][:], axis=AX.X)
 
-        def vector_stats(step):
-            if step == 1:
-                nc.vector.tensor_tensor(out=dlt[:], in0=mvc[:, 0:1], in1=negm0[:], op=ALU.add)
-            if step == 2:
-                nc.vector.tensor_tensor(out=dlt[:], in0=dlt[:], in1=dlt[:], op=ALU.mult)
-                nc.vector.tensor_scalar(
-                    out=csum[:, first : first + 1], in0=mvc[:, 0:1], scalar1=float(nv), scalar2=None, op0=ALU.mult
-                )
-            if step == 3:
-                nc.vector.tensor_tensor(out=dlt[:], in0=dlt[:], in1=mvc[:, 1:2], op=ALU.add)
-            if step == 4:
-                nc.vector.tensor_scalar(
-                    out=csq[:, first : first + 1], in0=dlt[:], scalar1=float(nv), scalar2=None, op0=ALU.mult
-                )
+        def first_cell_stats():
+            nc.vector.tensor_scalar(
+                out=csum[:, first : first + 1], in0=mvc[:, 0:1], scalar1=float(CW), scalar2=None, op0=ALU.mult
+            )
+            nc.vector.tensor_scalar(
+                out=csq[:, first : first + 1], in0=mvc[:, 1:2], scalar1=float(CW), scalar2=None, op0=ALU.mult
+            )
 
         for n, ci in enumerate(order):
-            for k, (jb, tag) in enumerate(((0, "m0"), (1, "m1"), (3, "m3"))):
+            for jb, tag in ((0, "m0"), (1, "m1"), (3, "m3")):
                 gate_block(ci, jb, tag)
-                if n == 6:
-                    vector_stats(k + 1)
-                if n == 7 and k == 0:
-                    vector_stats(4)
+            if n == 3:
+                first_cell_stats()
             if n == 0:
                 gate_block(ci, 2, "m2")
             if n >= 1:

@@ -14,33 +14,50 @@ AX = mybir.AxisListType
 
 P = 128
 B, I, H = 8192, 512, 128
+EPS = 1e-5
+FLOPS = 2 * B * I * 4 * H + 2 * B * H * 4 * H
+
 NB = 4
+GF, GI, GO, GG = range(NB)
+MX_ORDER = (GF, GG, GI, GO)
+
 TILES = B // P
 TPC = 4
 CH = TILES // TPC
 CW = TPC * P
-EPS = 1e-5
-DT = TPC + 1
-D0 = 3
-GPI = 6
+LAST = CH - 1
+
+DIRECT = TPC + 1
+DIRECT_COL = (TILES - DIRECT) * P
+LAST_COL = LAST * CW
+PAR = 24
 HG = 16
-HPAD = 144
-GW = P + 2
-GCH = 11
-SX = 14
-HGAP = 8
-HLAG = 0
-GB = 2
-QP = 2
-OGAP = 4
-OA = 1
-OB = 4
-VADD = (6, 12, 14, 15)
-OM = 0
-SC = 0
-AV = 1
-JB_ORDER = (0, 3, 1, 2)
-FLOPS = 2 * B * I * NB * H + 2 * B * H * NB * H
+HW = H + 16
+GW = H + 2
+
+WHH_AT = 1
+GRAM_AT = 2
+GRAM_STEP = 6
+GRAM_END = GRAM_AT + (TILES - DIRECT - 1) // GRAM_STEP
+DIRECT_AT = 3
+C_AT = CH // 2
+GP_CHUNKS = 12
+STATS_FIRST = 2
+
+H_GAP = 9
+ADD_STEP = 7
+O_GAP = 6
+O_EARLY_AT = {11: 0, 14: 1}
+O_EARLY = list(O_EARLY_AT.values())
+SX = ()
+OSK = (0,4,8)
+TA = 0
+SQ0 = 3
+SFE = (1, 2)
+PAR_AT = 7
+CV = tuple(range(1,CH,2))
+DS = ()
+OUT_BUFS = 4
 
 
 def tile_lstmcell_t_kernel(
@@ -50,10 +67,8 @@ def tile_lstmcell_t_kernel(
     xv = x.rearrange("(p s) k -> p s k", s=TILES)
     cv = c.rearrange("(p s) k -> p s k", s=TILES)
     hv = h.rearrange("(p s) k -> p s k", s=TILES)
-    outv = (
-        out_0.rearrange("(p s) k -> p s k", s=TILES),
-        out_1.rearrange("(p s) k -> p s k", s=TILES),
-    )
+    c_outv = out_0.rearrange("(p s) k -> p s k", s=TILES)
+    h_outv = out_1.rearrange("(p s) k -> p s k", s=TILES)
     with ExitStack() as ctx:
         ctx.enter_context(tc.manual_schedule())
         keep = ctx.enter_context(tc.tile_pool(name="keep", bufs=1))
@@ -62,8 +77,8 @@ def tile_lstmcell_t_kernel(
 
         gate = [keep.tile([P, B], F32, name="gate%d" % jb) for jb in range(NB)]
         hT = keep.tile([P, B], BF16)
-        hh_dir = keep.tile([P, NB, DT * P], F32)
-        h_nat = [keep.tile([P, HG, HPAD], BF16, name="h_nat%d" % g) for g in range(TILES // HG)]
+        hh_direct = keep.tile([P, NB, DIRECT * P], F32)
+        h_nat = [keep.tile([P, HG, HW], BF16, name="h_nat%d" % g) for g in range(TILES // HG)]
         w_codes = keep.tile([P, NB * P], U32, align_bytes=64)
         w_scales = keep.tile([P, NB * P], U8, align_bytes=64)
         whh_nat = keep.tile([P, NB, H], BF16)
@@ -72,20 +87,22 @@ def tile_lstmcell_t_kernel(
         ident_f = keep.tile([P, P], F32)
         ident_b = keep.tile([P, P], BF16)
         rows = keep.tile([P, P], BF16)
-        par = keep.tile([P, 24], F32)
-        gs = keep.tile([P, GW], F32)
-        gacc = keep.tile([P, CW], F32)
+        par = keep.tile([P, PAR], F32)
+        p_b, p_gih, p_bih, p_ghh, p_bhh = [par[:, NB * v : NB * (v + 1)] for v in range(5)]
+        p_gc, p_bc = par[:, 5 * NB : 5 * NB + 1], par[:, 5 * NB + 1 : 5 * NB + 2]
+        gram_sb = keep.tile([P, GW], F32)
+        gg_acc = keep.tile([P, CW], F32)
         st_ih = keep.tile([P, NB - 1, CH, 6], F32)
-        gsum = keep.tile([P, CH], F32)
-        gsq = keep.tile([P, 1 + CH - GCH], F32)
-        gred = keep.tile([P, 2], F32)
-        hsum = keep.tile([P, 2], F32)
-        sq_dir = keep.tile([P, 2, NB], F32)
-        csum = keep.tile([P, CH], F32)
-        csq = keep.tile([P, CH], F32)
-        csq_last = keep.tile([P, 1], F32)
+        gg_sum = keep.tile([P, CH], F32)
+        gg_sq = keep.tile([P, 1 + CH - GP_CHUNKS], F32)
+        gg_red = keep.tile([P, 2], F32)
+        h_sum = keep.tile([P, 1], F32)
+        sq_direct = keep.tile([P, 2, NB], F32)
+        cell_sum = keep.tile([P, CH], F32)
+        cell_sq = keep.tile([P, CH], F32)
+        cell_sq_last = keep.tile([P, 1], F32)
         junk = keep.tile([P, 2 * CW], BF16)
-        prod = keep.tile([P, NB, P], F32)
+        prod = keep.tile([P, 2, P], F32)
         neghalf = keep.tile([P, NB], F32)
         warm = keep.tile([P, 1], F32)
         mv = keep.tile([P, NB, 2], F32)
@@ -99,616 +116,650 @@ def tile_lstmcell_t_kernel(
         def blk(jb):
             return slice(jb * P, (jb + 1) * P)
 
-        def htile(s):
+        def h_tile(s):
             return h_nat[s // HG][:, s % HG, :]
 
         def transpose_bf16(tag, tiles):
-            bank = psum.tile([P, CW], BF16, tag=tag, name="bt")
+            bank = psum.tile([P, len(tiles) * P], BF16, tag=tag, name="bank_b")
             for t, src in enumerate(tiles):
                 nc.tensor.transpose(bank[:, t * P : (t + 1) * P], src, ident_b[:])
             return bank
 
-        def hh_matmul(b0, b1, jb, tag):
+        def h_transposed(first, end, tag):
+            return transpose_bf16(tag, [h_tile(s)[:, 0:H] for s in range(first, end)])
+
+        def hh_matmul(first_col, end_col, jb, tag):
             acc = psum.tile([P, CW], F32, tag=tag, name="acc")
             nc.tensor.matmul(
-                out=acc[:, 0 : b1 - b0], lhsT=whhT_b[:, blk(jb)], rhs=hT[:, b0:b1], start=True, stop=True
+                out=acc[:, 0 : end_col - first_col], lhsT=whhT_b[:, blk(jb)], rhs=hT[:, first_col:end_col],
+                start=True, stop=True,
             )
             return acc
-
-        BD = (TILES - DT) * P
-        BL = (CH - 1) * CW
 
         nc.vector.memset(warm[:], 0.0)
         nc.scalar.activation(out=warm[:], in_=warm[:], func=ACT.Sigmoid)
         make_identity(nc, ident_f[:])
         make_identity(nc, ident_b[:])
         nc.vector.memset(rows[:], 0.0)
-        nc.vector.memset(csum[:], 0.0)
-        nc.vector.memset(csq[:], 0.0)
+        nc.vector.memset(cell_sum[:], 0.0)
+        nc.vector.memset(cell_sq[:], 0.0)
         nc.vector.memset(neghalf[:], -0.5)
         for g in range(TILES // HG):
-            nc.vector.memset(h_nat[g][:, :, H:HPAD], 1.0)
+            nc.vector.memset(h_nat[g][:, :, H:HW], 1.0)
 
         with tc.tile_pool(name="stage", bufs=2) as stage:
             x_sb = {}
-            banks = {}
+            words_in = {}
             grp = {}
             codes = {}
             scales = {}
-            acc_ih = {}
+            ih_bank = {}
 
             def load_x(ci, pieces=1):
                 x_sb[ci] = stage.tile([P, TPC, I], BF16, tag="xs", bufs=4, name="x_sb")
                 n = TPC // pieces
-                for k in range(0, TPC, n):
+                for t in range(0, TPC, n):
                     nc.sync.dma_start(
-                        out=x_sb[ci][:, k : k + n, :], in_=xv[:, ci * TPC + k : ci * TPC + k + n, :]
+                        out=x_sb[ci][:, t : t + n, :], in_=xv[:, ci * TPC + t : ci * TPC + t + n, :]
                     )
 
             def load_h(g):
                 nc.sync.dma_start(out=h_nat[g][:, :, 0:H], in_=hv[:, g * HG : (g + 1) * HG, :])
 
-            def t1(key, src, tags=("ta", "tb")):
-                pair = []
+            def load_c(g):
+                c_nat[g] = cpool.tile([P, HG, H], BF16, tag="cn", bufs=4, name="c_nat")
+                nc.sync.dma_start(out=c_nat[g][:], in_=cv[:, g * HG : (g + 1) * HG, :])
+
+            def words_transposed(key, src, tags=("ta", "tb")):
+                words_in[key] = []
                 for half, tag in enumerate(tags):
-                    xt = psum.tile([P, 2, 2 * P], F32, tag=tag, name="xt")
+                    bank = psum.tile([P, 2, 2 * P], F32, tag=tag, name="bank_w")
                     for a in range(2):
-                        sw = src[:, 2 * half + a, :].bitcast(F32)
+                        words = src[:, 2 * half + a, :].bitcast(F32)
                         for u in range(2):
-                            nc.tensor.transpose(xt[:, u, a * P : (a + 1) * P], sw[:, u : 2 * P : 2], ident_f[:])
-                    pair.append(xt)
-                banks[key] = pair
+                            nc.tensor.transpose(bank[:, u, blk(a)], words[:, u : 2 * P : 2], ident_f[:])
+                    words_in[key].append(bank)
 
             def new_grp(key):
                 grp[key] = stage.tile([P, 4 * CW], BF16, tag="grp", bufs=2, align_bytes=64, name="grp")
 
-            def evac(key, half, on_scalar):
+            def words_out(key, half, copy):
                 words = grp[key][:].bitcast(F32).rearrange("p (r u) -> p r u", u=2)
-                dst = words[:, half * 2 * P : (half + 1) * 2 * P, :]
-                src = banks[key][half][:].rearrange("p u r -> p r u")
-                if on_scalar:
-                    nc.scalar.copy(out=dst, in_=src)
-                else:
-                    nc.vector.tensor_copy(out=dst, in_=src)
-
-            def quant(key):
-                codes[key] = stage.tile([P, CW], U32, tag="codes", bufs=2, align_bytes=64, name="codes")
-                scales[key] = stage.tile([P, CW], U8, tag="scales", bufs=2, align_bytes=64, name="scales")
-                nc.vector.quantize_mx(
-                    out=codes[key][:].bitcast(FP8X4), scales=scales[key][:], in_=grp[key][:]
+                copy(
+                    out=words[:, half * 2 * P : (half + 1) * 2 * P, :],
+                    in_=words_in[key][half][:].rearrange("p u r -> p r u"),
                 )
 
-            def mx(ci):
-                acc_ih[ci] = {}
-                for jb in JB_ORDER:
+            def quantise(ci):
+                codes[ci] = stage.tile([P, CW], U32, tag="codes", bufs=2, align_bytes=64, name="codes")
+                scales[ci] = stage.tile([P, CW], U8, tag="scales", bufs=2, align_bytes=64, name="scales")
+                nc.vector.quantize_mx(out=codes[ci][:].bitcast(FP8X4), scales=scales[ci][:], in_=grp[ci][:])
+
+            def ih_matmul(ci):
+                ih_bank[ci] = {}
+                for pos, jb in enumerate(MX_ORDER):
                     acc = psum.tile([P, CW], F32, tag="m%d" % jb, name="acc")
                     nc.tensor.matmul_mx(
                         out=acc[:],
-                        lhsT=w_codes[:, blk(jb)].bitcast(FP8X4),
-                        lhsT_scale=w_scales[:, blk(jb)],
+                        lhsT=w_codes[:, blk(pos)].bitcast(FP8X4),
+                        lhsT_scale=w_scales[:, blk(pos)],
                         rhs=codes[ci][:].bitcast(FP8X4),
                         rhs_scale=scales[ci][:],
                         start=True,
                         stop=True,
                     )
-                    acc_ih[ci][jb] = acc
+                    ih_bank[ci][jb] = acc
 
-            def square_ih(ci):
+            def gg_square(ci):
+                k = 1 + ci - GP_CHUNKS
                 nc.scalar.activation(
-                    out=junk[:, 0:CW], in_=acc_ih[ci][3][:], func=ACT.Square, accum_out=gsq[:, 1 + ci - GCH : 2 + ci - GCH]
+                    out=junk[:, 0:CW], in_=ih_bank[ci][GG][:], func=ACT.Square, accum_out=gg_sq[:, k : k + 1]
                 )
 
-            def copy_ih(ci):
-                for jb in JB_ORDER:
-                    if jb == 3:
+            def ih_copied(ci):
+                for jb in MX_ORDER:
+                    if jb == GG:
                         nc.scalar.activation(
-                            out=gate[jb][:, cols(ci)], in_=acc_ih[ci][jb][:], func=ACT.Copy,
-                            accum_out=gsum[:, ci : ci + 1],
+                            out=gate[jb][:, cols(ci)], in_=ih_bank[ci][jb][:], func=ACT.Copy,
+                            accum_out=gg_sum[:, ci : ci + 1],
                         )
-                        if ci >= GCH:
-                            square_ih(ci)
+                        if ci >= GP_CHUNKS:
+                            gg_square(ci)
                     else:
-                        nc.scalar.copy(out=gate[jb][:, cols(ci)], in_=acc_ih[ci][jb][:])
+                        nc.scalar.copy(out=gate[jb][:, cols(ci)], in_=ih_bank[ci][jb][:])
 
-            squares = {}
+            def ih_stats(ci, jb):
+                src = ih_bank[ci][jb][:] if ci == LAST else gate[jb][:, cols(ci)]
+                nc.vector.bn_stats(out=st_ih[:, jb, ci, :], in_=src)
 
-            def on_gpsimd(ci, jb):
-                return ci < GCH and jb == 3
+            gg_new = {}
 
-            def add_squares(ci, last):
-                for t in range(TPC):
-                    nc.tensor.matmul(
-                        out=gram[:, GW:], lhsT=squares[ci][:, t * P : (t + 1) * P], rhs=ident_f[:],
-                        start=False, stop=(last and t == TPC - 1), is_transpose=True,
-                    )
+            def gg_added(ci):
+                nc.gpsimd.tensor_tensor(out=gg_acc[:], in0=gg_acc[:], in1=gg_new.pop(ci)[:], op=ALU.add)
 
-            def stat_ih(ci, jb):
-                src = acc_ih[ci][jb][:] if ci == CH - 1 else gate[jb][:, cols(ci)]
-                if on_gpsimd(ci, jb):
-                    if ci == 0:
-                        nc.gpsimd.tensor_tensor(out=gacc[:], in0=src, in1=src, op=ALU.mult)
-                    else:
-                        sq = stage.tile([P, CW], F32, tag="gsq", bufs=GB, name="gsq")
-                        nc.vector.memset(sq[:, 0:1], 0.0)
-                        nc.gpsimd.tensor_tensor(out=sq[:], in0=src, in1=src, op=ALU.mult)
-                        nc.gpsimd.tensor_tensor(out=gacc[:], in0=gacc[:], in1=sq[:], op=ALU.add)
-                elif jb < 3:
-                    nc.vector.bn_stats(out=st_ih[:, jb, ci, :], in_=src)
+            def gg_gate(ci):
+                gg_new[ci] = stage.tile([P, CW], F32, tag="gsq", bufs=3, name="sq")
+                nc.vector.memset(gg_new[ci][:, 0:1], 0.0)
+
+            def gg_squared(ci):
+                src = gate[GG][:, cols(ci)]
+                if ci == 0:
+                    nc.gpsimd.tensor_tensor(out=gg_acc[:], in0=src, in1=src, op=ALU.mult)
+                else:
+                    nc.gpsimd.tensor_tensor(out=gg_new[ci][:], in0=src, in1=src, op=ALU.mult)
+                if ci >= 2:
+                    gg_added(ci - 1)
+                if ci == GP_CHUNKS - 1:
+                    gg_added(ci)
 
             w_sb = stage.tile([P, NB, I], BF16, tag="xs", bufs=4, name="w_sb")
             wv = w_ih.rearrange("(jb m) k -> m jb k", m=P)
-            for half in (slice(0, 2), slice(2, 4)):
-                nc.sync.dma_start(out=w_sb[:, half, :], in_=wv[:, half, :])
-            load_x(0, 2)
-            load_x(1)
-            for v, vec in enumerate((b, g_ih, b_ih, g_hh, b_hh)):
-                nc.sync.dma_start(
-                    out=rows[NB * v : NB * (v + 1), :], in_=vec.rearrange("(r m) -> r m", m=P)
-                )
-            nc.sync.dma_start(out=rows[20:21, :], in_=g_c.rearrange("(r m) -> r m", m=P))
-            nc.sync.dma_start(out=rows[21:22, :], in_=b_c.rearrange("(r m) -> r m", m=P))
-            load_x(2)
-            nc.sync.dma_start(out=whh_nat[:], in_=w_hh.rearrange("(jb m) k -> m jb k", m=P))
 
-            t1("w", w_sb)
+            def load_w(pos):
+                nc.sync.dma_start(out=w_sb[:, pos, :], in_=wv[:, MX_ORDER[pos], :])
+
+            load_w(0)
+            load_x(0, TPC)
+            for pos in range(1, NB):
+                load_w(pos)
+            load_x(1)
+            load_x(2)
+
+            w_grp = stage.tile([P, 4 * CW], BF16, tag="grp", bufs=2, align_bytes=64, name="grp")
+            w_bank = {}
+
+            def w_transposed(first, end, tag):
+                bank = psum.tile([P, 2, (end - first) * P], F32, tag=tag, name="bank_w")
+                for pos in range(first, end):
+                    words = w_sb[:, pos, :].bitcast(F32)
+                    for u in range(2):
+                        nc.tensor.transpose(bank[:, u, blk(pos - first)], words[:, u : 2 * P : 2], ident_f[:])
+                w_bank[first] = bank
+
+            def w_out(first, end):
+                words = w_grp[:].bitcast(F32).rearrange("p (r u) -> p r u", u=2)
+                nc.scalar.copy(out=words[:, first * P : end * P, :], in_=w_bank[first][:].rearrange("p u r -> p r u"))
+
+            def w_quantised(first, end):
+                s = slice(first * P, end * P)
+                nc.vector.quantize_mx(
+                    out=w_codes[:, s].bitcast(FP8X4), scales=w_scales[:, s], in_=w_grp[:, first * CW : end * CW]
+                )
+
+            w_transposed(0, 1, "th")
+            words_transposed(0, x_sb[0])
+            w_transposed(1, 3, "g")
+            w_transposed(3, 4, "m2")
             load_x(3)
+            nc.sync.dma_start(out=whh_nat[:], in_=w_hh.rearrange("(jb m) k -> m jb k", m=P))
             load_h(TILES // HG - 1)
-            t1(0, x_sb[0], ("th", "g"))
             load_x(4)
-            new_grp("w")
-            evac("w", 0, True)
-            evac("w", 1, True)
+            w_out(0, 1)
+            w_quantised(0, 1)
             new_grp(0)
-            evac(0, 0, False)
-            nc.vector.quantize_mx(out=w_codes[:].bitcast(FP8X4), scales=w_scales[:], in_=grp["w"][:])
-            evac(0, 1, True)
-            quant(0)
-            t1(1, x_sb[1])
+            words_out(0, 0, nc.scalar.copy)
+            words_out(0, 1, nc.vector.tensor_copy)
+            w_out(1, 3)
+            w_out(3, 4)
+            quantise(0)
+            w_quantised(1, 3)
+            w_quantised(3, 4)
+            words_transposed(1, x_sb[1])
             load_x(5)
-            mx(0)
+            ih_matmul(0)
 
             c_nat = {}
 
-            def load_c(cg):
-                c_nat[cg] = cpool.tile([P, HG, H], BF16, tag="cn", bufs=4, name="c_nat")
-                nc.sync.dma_start(out=c_nat[cg][:], in_=cv[:, cg * HG : (cg + 1) * HG, :])
-
-            t2 = small("t2")
-            s1 = small("s1")
-            bsum = small("bsum")
+            hh_sq = small("hh_sq")
+            hh_sum = small("hh_sum")
+            bias_sum = small("bias_sum")
             mean_hh = small("mean_hh")
-            msq = small("msq")
+            mean_sq = small("mean_sq")
             var_hh = small("var_hh")
             rstd_hh = small("rstd_hh")
             a_hh = small("a_hh")
-            zfix = small("zfix")
+            tiny = small("tiny")
             sc = small("sc")
             ratio = small("ratio")
             cst = small("cst")
 
-            def hh_small_ops():
-                e = nc.gpsimd
-                e.tensor_tensor(out=t2[:], in0=t2[:], in1=sq_dir[:, 0, :], op=ALU.add)
-                e.tensor_tensor(out=t2[:], in0=t2[:], in1=sq_dir[:, 1, :], op=ALU.add)
-                e.tensor_scalar(out=mean_hh[:], in0=s1[:], scalar1=1.0 / B, scalar2=0.0, op0=ALU.mult, op1=ALU.add)
-                e.tensor_tensor(out=msq[:], in0=mean_hh[:], in1=mean_hh[:], op=ALU.mult)
-                e.tensor_scalar(out=t2[:], in0=t2[:], scalar1=1.0 / B, scalar2=0.0, op0=ALU.mult, op1=ALU.add)
-                e.tensor_tensor(out=var_hh[:], in0=t2[:], in1=msq[:], op=ALU.subtract)
-                e.tensor_scalar(out=var_hh[:], in0=var_hh[:], scalar1=0.0, scalar2=EPS, op0=ALU.max, op1=ALU.add)
-                e.tensor_tensor(out=rstd_hh[:], in0=var_hh[:], in1=neghalf[:], op=ALU.pow)
-                e.tensor_tensor(out=a_hh[:], in0=par[:, 12:16], in1=rstd_hh[:], op=ALU.mult)
-                e.tensor_scalar(
-                    out=zfix[:], in0=a_hh[:], scalar1=0.0, scalar2=1e-30, op0=ALU.is_equal, op1=ALU.mult
-                )
-                e.tensor_tensor(out=sc[:], in0=a_hh[:], in1=zfix[:], op=ALU.add)
-                e.tensor_tensor(out=bsum[:], in0=par[:, 0:4], in1=par[:, 8:12], op=ALU.add)
-                e.tensor_tensor(out=bsum[:], in0=bsum[:], in1=par[:, 16:20], op=ALU.add)
-                e.tensor_tensor(out=cst[:], in0=a_hh[:], in1=mean_hh[:], op=ALU.mult)
-                e.tensor_tensor(out=cst[:], in0=bsum[:], in1=cst[:], op=ALU.subtract)
+            def hh_scale():
+                def tt(out, in0, in1, op):
+                    nc.gpsimd.tensor_tensor(out=out[:], in0=in0, in1=in1, op=op)
 
-            gram = None
+                def ts(out, in0, scalar1, op0, scalar2, op1):
+                    nc.gpsimd.tensor_scalar(out=out[:], in0=in0, scalar1=scalar1, scalar2=scalar2, op0=op0, op1=op1)
+
+                tt(hh_sq, hh_sq[:], sq_direct[:, 0, :], ALU.add)
+                tt(hh_sq, hh_sq[:], sq_direct[:, 1, :], ALU.add)
+                ts(mean_hh, hh_sum[:], 1.0 / B, ALU.mult, 0.0, ALU.add)
+                tt(mean_sq, mean_hh[:], mean_hh[:], ALU.mult)
+                ts(hh_sq, hh_sq[:], 1.0 / B, ALU.mult, 0.0, ALU.add)
+                tt(var_hh, hh_sq[:], mean_sq[:], ALU.subtract)
+                ts(var_hh, var_hh[:], 0.0, ALU.max, EPS, ALU.add)
+                tt(rstd_hh, var_hh[:], neghalf[:], ALU.pow)
+                tt(a_hh, p_ghh, rstd_hh[:], ALU.mult)
+                ts(tiny, a_hh[:], 0.0, ALU.is_equal, 1e-30, ALU.mult)
+                tt(sc, a_hh[:], tiny[:], ALU.add)
+                tt(bias_sum, p_b, p_bih, ALU.add)
+                tt(bias_sum, bias_sum[:], p_bhh, ALU.add)
+                tt(cst, a_hh[:], mean_hh[:], ALU.mult)
+                tt(cst, bias_sum[:], cst[:], ALU.subtract)
+
+            gram_tiles = list(range(TILES - HG, TILES - DIRECT)) + list(range(TILES - HG))
             for ci in range(CH):
                 nxt = ci + 1
                 if nxt < CH:
                     new_grp(nxt)
-                    evac(nxt, 0, True)
-                    evac(nxt, 1, nxt >= SX)
-                if ci >= 1:
-                    for jb in range(QP):
-                        stat_ih(ci - 1, jb)
+                    words_out(nxt, 0, nc.scalar.copy)
+                if ci in SFE:
+                    for jb in range(STATS_FIRST):
+                        ih_stats(ci - 1, jb)
                 if nxt < CH:
-                    quant(nxt)
-                if ci >= 1 and ci - 1 < GCH:
-                    stat_ih(ci - 1, 3)
-                if D0 <= ci < D0 + NB:
-                    dacc = hh_matmul(BL, B, ci - D0, "th")
-                    nc.vector.tensor_copy(out=hh_dir[:, ci - D0, BL - BD :], in_=dacc[:])
-                if ci == D0 + NB:
-                    dacc = psum.tile([P, NB, P], F32, tag="th", name="dacc")
+                    words_out(nxt, 1, nc.scalar.copy if nxt in SX else nc.vector.tensor_copy)
+                if ci >= 1 and ci not in SFE:
+                    for jb in range(STATS_FIRST):
+                        ih_stats(ci - 1, jb)
+                if ci == WHH_AT + 1:
+                    nc.vector.tensor_copy(out=whhT_b[:], in_=whh_bank[:])
+                    nc.gpsimd.tensor_scalar(
+                        out=whhT_f[:], in0=whhT_b[:], scalar1=1.0, scalar2=0.0, op0=ALU.mult, op1=ALU.add
+                    )
+                if 2 <= ci <= GP_CHUNKS:
+                    gg_gate(ci - 1)
+                if nxt < CH:
+                    quantise(nxt)
+                if 1 <= ci <= GP_CHUNKS:
+                    gg_squared(ci - 1)
+                if DIRECT_AT <= ci < DIRECT_AT + NB:
+                    hh_bank = hh_matmul(LAST_COL, B, ci - DIRECT_AT, "th")
+                    (nc.scalar.copy if ci - DIRECT_AT in DS else nc.vector.tensor_copy)(out=hh_direct[:, ci - DIRECT_AT, LAST_COL - DIRECT_COL :], in_=hh_bank[:])
+                if ci == DIRECT_AT + NB:
+                    hh_bank = psum.tile([P, NB, P], F32, tag="th", name="hh_bank")
                     for jb in range(NB):
                         nc.tensor.matmul(
-                            out=dacc[:, jb, :], lhsT=whhT_b[:, blk(jb)], rhs=hT[:, BD:BL], start=True, stop=True
+                            out=hh_bank[:, jb, :], lhsT=whhT_b[:, blk(jb)], rhs=hT[:, DIRECT_COL:LAST_COL],
+                            start=True, stop=True,
                         )
-                    nc.vector.tensor_copy(out=hh_dir[:, :, 0 : BL - BD], in_=dacc[:])
+                    nc.vector.tensor_copy(out=hh_direct[:, :, 0 : LAST_COL - DIRECT_COL], in_=hh_bank[:])
                 if ci >= 1:
-                    for jb in range(QP, NB - 1):
-                        stat_ih(ci - 1, jb)
+                    for jb in range(STATS_FIRST, NB - 1):
+                        ih_stats(ci - 1, jb)
                 if ci + 2 < CH:
-                    t1(ci + 2, x_sb[ci + 2])
+                    words_transposed(ci + 2, x_sb[ci + 2])
                     if ci + 6 < CH:
                         load_x(ci + 6)
-                if ci in (0, 2, 4):
+                if ci % 2 == 0 and ci // 2 < TILES // HG - 1:
                     load_h(ci // 2)
-                if 8 <= ci < 12:
-                    load_c(ci - 8)
-                if ci == 1:
-                    wt = transpose_bf16("g", [whh_nat[:, jb, :] for jb in range(NB)])
-                    nc.vector.tensor_copy(out=whhT_b[:], in_=wt[:])
-                    nc.gpsimd.tensor_copy(out=whhT_f[:], in_=whhT_b[:])
-                    pt = psum.tile([P, P], BF16, tag="th", name="pt")
-                    nc.tensor.transpose(pt[:], rows[:], ident_b[:])
-                    nc.vector.tensor_copy(out=par[:], in_=pt[:, 0:24])
-                if ci == 14:
-                    nc.vector.reduce_sum(out=gsq[:, 0:1], in_=gacc[:], axis=AX.X)
-                if ci == CH - 1:
+                if C_AT <= ci < C_AT + TILES // HG:
+                    load_c(ci - C_AT)
+                if ci == PAR_AT:
+                    for v, vec in enumerate((b, g_ih, b_ih, g_hh, b_hh)):
+                        nc.sync.dma_start(out=rows[NB * v : NB * (v + 1), :], in_=vec.rearrange("(r m) -> r m", m=P))
+                    for v, vec in enumerate((g_c, b_c)):
+                        nc.sync.dma_start(out=rows[5 * NB + v : 5 * NB + v + 1, :], in_=vec.rearrange("(r m) -> r m", m=P))
+                if ci == PAR_AT + 2:
+                    turned = psum.tile([P, P], BF16, tag="th", name="turned")
+                    nc.tensor.transpose(turned[:], rows[:], ident_b[:])
+                    nc.vector.tensor_copy(out=par[:], in_=turned[:, 0:PAR])
+                if ci == WHH_AT:
+                    turned = transpose_bf16("g", [whh_nat[:, jb, :] for jb in range(NB)])
+                    whh_bank = turned
+                if ci == LAST - 1:
+                    nc.scalar.activation(out=junk[:, CW:], in_=gg_acc[:], func=ACT.Copy, accum_out=gg_sq[:, 0:1])
+                if ci == LAST:
                     nc.vector.reciprocal(out=ratio[:], in_=sc[:])
-                    nc.vector.tensor_tensor(out=ratio[:], in0=ratio[:], in1=par[:, 4:8], op=ALU.mult)
-                if ci < CH - 1:
-                    copy_ih(ci)
-                if ci == 2:
-                    for k, (tag, s0, s9) in enumerate((("th", TILES - TPC, TILES), ("g", TILES - DT, TILES - TPC))):
-                        ht = transpose_bf16(tag, [htile(s)[:, 0:H] for s in range(s0, s9)])
-                        nc.scalar.activation(
-                            out=hT[:, s0 * P : s9 * P], in_=ht[:, 0 : (s9 - s0) * P], func=ACT.Copy,
-                            accum_out=hsum[:, k : k + 1],
-                        )
-                s0 = GPI * (ci - 2)
-                if ci >= 2 and s0 < TILES - DT:
-                    if ci == 2:
-                        gram = psum.tile([P, GW], F32, tag="g", name="gram")
-                    for s in range(s0, min(s0 + GPI, TILES - DT)):
+                    nc.vector.tensor_tensor(out=ratio[:], in0=ratio[:], in1=p_gih, op=ALU.mult)
+                else:
+                    ih_copied(ci)
+                if ci == GRAM_AT:
+                    turned = h_transposed(TILES - DIRECT, TILES, "th")
+                    nc.scalar.activation(
+                        out=hT[:, DIRECT_COL:], in_=turned[:], func=ACT.Copy, accum_out=h_sum[:]
+                    )
+                    gram = psum.tile([P, GW], F32, tag="g", name="gram")
+                if GRAM_AT <= ci <= GRAM_END:
+                    first = GRAM_STEP * (ci - GRAM_AT)
+                    for s in gram_tiles[first : first + GRAM_STEP]:
                         nc.tensor.matmul(
-                            out=gram[:, 0:GW], lhsT=htile(s)[:, 0:H], rhs=htile(s)[:, 0:GW], start=(s == 0), stop=(s == TILES - DT - 1)
+                            out=gram[:], lhsT=h_tile(s)[:, 0:H], rhs=h_tile(s)[:, 0:GW],
+                            start=(s == gram_tiles[0]), stop=(s == gram_tiles[-1]),
                         )
                 if nxt < CH:
-                    mx(nxt)
-                if D0 <= ci < D0 + NB:
+                    ih_matmul(nxt)
+                if DIRECT_AT <= ci < DIRECT_AT + NB:
+                    jb = ci - DIRECT_AT
                     nc.scalar.activation(
-                        out=junk[:, 0:CW], in_=dacc[:], func=ACT.Square, accum_out=sq_dir[:, 0, ci - D0 : ci - D0 + 1]
+                        out=junk[:, 0:CW], in_=hh_bank[:], func=ACT.Square, accum_out=sq_direct[:, 0, jb : jb + 1]
                     )
-                if ci == D0 + NB:
+                if ci == DIRECT_AT + NB:
                     for jb in range(NB):
                         nc.scalar.activation(
-                            out=junk[:, blk(jb)], in_=dacc[:, jb, :], func=ACT.Square, accum_out=sq_dir[:, 1, jb : jb + 1]
+                            out=junk[:, blk(jb)], in_=hh_bank[:, jb, :], func=ACT.Square,
+                            accum_out=sq_direct[:, 1, jb : jb + 1],
                         )
-                if ci == 11:
-                    nc.vector.tensor_copy(out=gs[:], in_=gram[:])
-                    nc.vector.scalar_tensor_tensor(
-                        out=gs[:, P : P + 1], in0=gs[:, P : P + 1], scalar=hsum[:, 0:1], in1=hsum[:, 1:2],
-                        op0=ALU.add, op1=ALU.add,
+                if ci == GRAM_END:
+                    nc.vector.tensor_copy(out=gram_sb[:], in_=gram[:])
+                    nc.vector.tensor_tensor(
+                        out=gram_sb[:, H : H + 1], in0=gram_sb[:, H : H + 1], in1=h_sum[:], op=ALU.add
                     )
-                if ci == 12:
-                    ys = []
+                if ci == GRAM_END + 1:
+                    gw_banks = []
                     for pair, tag in enumerate(("th", "g")):
-                        y = psum.tile([P, 2, GW], F32, tag=tag, name="y")
+                        gw = psum.tile([P, 2, GW], F32, tag=tag, name="gw")
                         for a in range(2):
                             nc.tensor.matmul(
-                                out=y[:, a, :], lhsT=whhT_f[:, blk(2 * pair + a)], rhs=gs[:, 0:GW], start=True, stop=True
+                                out=gw[:, a, :], lhsT=whhT_f[:, blk(2 * pair + a)], rhs=gram_sb[:],
+                                start=True, stop=True,
                             )
-                        ys.append(y)
-                if ci == 13:
-                    for pair in range(2):
-                        nc.vector.tensor_tensor(
-                            out=prod[:, 2 * pair : 2 * pair + 2, :], in0=ys[pair][:, :, 0:P],
-                            in1=whh_nat[:, 2 * pair : 2 * pair + 2, :], op=ALU.mult,
-                        )
-                        nc.vector.tensor_copy(out=s1[:, 2 * pair : 2 * pair + 2], in_=ys[pair][:, :, P])
-                    nc.vector.reduce_sum(out=t2[:], in_=prod[:], axis=AX.X)
-                    hh_small_ops()
+                        gw_banks.append(gw)
+                if ci == GRAM_END + 2:
+                    for pair, gw in enumerate(gw_banks):
+                        for a in range(2):
+                            jb = 2 * pair + a
+                            nc.vector.scalar_tensor_tensor(
+                                out=prod[:, a, :], in0=gw[:, a, 0:H], scalar=1.0, in1=whh_nat[:, jb, :],
+                                op0=ALU.mult, op1=ALU.mult, accum_out=hh_sq[:, jb : jb + 1],
+                            )
+                        nc.vector.tensor_copy(out=hh_sum[:, 2 * pair : 2 * pair + 2], in_=gw[:, :, H])
+                    hh_scale()
 
-        late = ctx.enter_context(tc.tile_pool(name="late", bufs=3))
-        ve_ih = small("ve_ih")
+        late = ctx.enter_context(tc.tile_pool(name="late", bufs=OUT_BUFS))
+        var_ih = small("var_ih")
         rstd_ih = small("rstd_ih")
-        am = small("am")
+        neg_gmean = small("neg_gmean")
 
-        def ih_scale(first, last):
-            s = slice(first, last)
+        def ih_rstd(first, end):
+            s = slice(first, end)
             nc.vector.tensor_scalar(
-                out=ve_ih[:, s], in0=mv[:, s, 1], scalar1=0.0, scalar2=EPS, op0=ALU.max, op1=ALU.add
+                out=var_ih[:, s], in0=mv[:, s, 1], scalar1=0.0, scalar2=EPS, op0=ALU.max, op1=ALU.add
             )
-            nc.gpsimd.tensor_tensor(out=rstd_ih[:, s], in0=ve_ih[:, s], in1=neghalf[:, s], op=ALU.pow)
+            nc.gpsimd.tensor_tensor(out=rstd_ih[:, s], in0=var_ih[:, s], in1=neghalf[:, s], op=ALU.pow)
             nc.vector.scalar_tensor_tensor(
-                out=am[:, s], in0=mv[:, s, 0], scalar=-1.0, in1=par[:, 4 + first : 4 + last], op0=ALU.mult, op1=ALU.mult
+                out=neg_gmean[:, s], in0=mv[:, s, 0], scalar=-1.0, in1=p_gih[:, s], op0=ALU.mult, op1=ALU.mult
             )
 
-        def ih_ratio(first, last):
-            s = slice(first, last)
+        def ih_ratio(first, end):
+            s = slice(first, end)
             nc.vector.tensor_tensor(out=ratio[:, s], in0=ratio[:, s], in1=rstd_ih[:, s], op=ALU.mult)
 
         def ih_bias(jb):
             s = slice(jb, jb + 1)
             nc.vector.scalar_tensor_tensor(
-                out=cst[:, s], in0=am[:, s], scalar=rstd_ih[:, s], in1=cst[:, s], op0=ALU.mult, op1=ALU.add
+                out=cst[:, s], in0=neg_gmean[:, s], scalar=rstd_ih[:, s], in1=cst[:, s], op0=ALU.mult, op1=ALU.add
             )
 
-        nc.scalar.activation(out=junk[:, CW:], in_=acc_ih[CH - 1][3][:], func=ACT.Copy, accum_out=gsum[:, CH - 1 : CH])
-        square_ih(CH - 1)
-        stat_ih(CH - 1, 0)
-        stat_ih(CH - 1, 1)
-        nc.vector.bn_aggr(out=mv[:, 0, :], in_=st_ih[:, 0, :, :].rearrange("p c s -> p (c s)"))
-        nc.vector.bn_aggr(out=mv[:, 1, :], in_=st_ih[:, 1, :, :].rearrange("p c s -> p (c s)"))
-        ih_scale(0, 2)
-        stat_ih(CH - 1, 2)
-        nc.vector.reduce_sum(out=gred[:, 0:1], in_=gsum[:], axis=AX.X)
-        nc.vector.reduce_sum(out=gred[:, 1:2], in_=gsq[:], axis=AX.X)
-        nc.vector.tensor_scalar(
-            out=mv[:, 3, 0:1], in0=gred[:, 0:1], scalar1=1.0 / B, scalar2=None, op0=ALU.mult
+        def ih_mean_var(jb):
+            nc.vector.bn_aggr(out=mv[:, jb, :], in_=st_ih[:, jb, :, :].rearrange("p c s -> p (c s)"))
+
+        nc.scalar.activation(
+            out=junk[:, CW:], in_=ih_bank[LAST][GG][:], func=ACT.Copy, accum_out=gg_sum[:, LAST : LAST + 1]
         )
-        ih_ratio(0, 2)
-        nc.vector.tensor_tensor(out=gred[:, 0:1], in0=mv[:, 3, 0:1], in1=mv[:, 3, 0:1], op=ALU.mult)
-        nc.vector.bn_aggr(out=mv[:, 2, :], in_=st_ih[:, 2, :, :].rearrange("p c s -> p (c s)"))
+        gg_square(LAST)
+        ih_stats(LAST, GF)
+        ih_stats(LAST, GI)
+        ih_mean_var(GF)
+        ih_mean_var(GI)
+        ih_rstd(GF, GO)
+        ih_stats(LAST, GO)
+        nc.vector.reduce_sum(out=gg_red[:, 0:1], in_=gg_sum[:], axis=AX.X)
+        nc.vector.reduce_sum(out=gg_red[:, 1:2], in_=gg_sq[:], axis=AX.X)
+        nc.vector.tensor_scalar(out=mv[:, GG, 0:1], in0=gg_red[:, 0:1], scalar1=1.0 / B, scalar2=None, op0=ALU.mult)
+        ih_ratio(GF, GO)
+        nc.vector.tensor_tensor(out=gg_red[:, 0:1], in0=mv[:, GG, 0:1], in1=mv[:, GG, 0:1], op=ALU.mult)
+        ih_mean_var(GO)
         nc.vector.scalar_tensor_tensor(
-            out=mv[:, 3, 1:2], in0=gred[:, 1:2], scalar=1.0 / B, in1=gred[:, 0:1], op0=ALU.mult, op1=ALU.subtract
+            out=mv[:, GG, 1:2], in0=gg_red[:, 1:2], scalar=1.0 / B, in1=gg_red[:, 0:1], op0=ALU.mult, op1=ALU.subtract
         )
-        ih_scale(2, 4)
+        ih_rstd(GO, NB)
 
         c_bank = {}
 
-        def c_transposed(q):
-            tiles = [c_nat[q // TPC][:, (q % TPC) * TPC + t, :] for t in range(TPC)]
-            c_bank[q] = transpose_bf16(("ta", "tb", "th")[len(c_bank) % 3], tiles)
+        def c_transposed(ci):
+            tiles = [c_nat[s // HG][:, s % HG, :] for s in range(ci * TPC, (ci + 1) * TPC)]
+            c_bank[ci] = transpose_bf16(("ta", "tb", "th")[len(c_bank) % 3], tiles)
 
-        def h_transposed(s0, s9, tag):
-            ht = transpose_bf16(tag, [htile(s)[:, 0:H] for s in range(s0, s9)])
-            nc.scalar.copy(out=hT[:, s0 * P : s9 * P], in_=ht[:, 0 : (s9 - s0) * P])
+        def h_chunk(ci, tag):
+            first, end = ci * TPC, min((ci + 1) * TPC, TILES - DIRECT)
+            turned = h_transposed(first, end, tag)
+            nc.scalar.copy(out=hT[:, first * P : end * P], in_=turned[:, 0 : (end - first) * P])
 
-        c_transposed(CH - 1)
-        def h_chunk(q, tag):
-            h_transposed(q * TPC, min((q + 1) * TPC, TILES - DT), tag)
+        order = [LAST, LAST - 1] + list(range(LAST - 1))
+        for k, ci in enumerate([LAST - 1] + list(range(H_GAP))):
+            h_chunk(ci, ("tb", "th", "g", "ta")[k % 4])
+        c_transposed(LAST)
 
-        for q in [CH - 2] + list(range(HGAP)):
-            h_chunk(q, ("g", "tb", "th")[q % 3])
+        shift = small("shift", 1)
+        offset = small("offset", 1)
+        sums_sb = keep.tile([P, P], F32)
 
-        negm0 = small("negm0", 1)
-        dlt = small("dlt", 1)
-        mvc = small("mvc", 2)
-        st_c = keep.tile([P, 6], F32)
-        part = keep.tile([P, P], F32)
+        def ratio_added(ih, hh, jb, first_col, end_col):
+            nc.vector.scalar_tensor_tensor(
+                out=gate[jb][:, first_col:end_col], in0=ih, scalar=ratio[:, jb : jb + 1], in1=hh,
+                op0=ALU.mult, op1=ALU.add,
+            )
 
-        ahead = {}
+        def combine_direct(ci, jb):
+            first_col, end_col = max(ci * CW, DIRECT_COL), (ci + 1) * CW
+            ih = ih_bank[ci][jb][:] if ci == LAST else gate[jb][:, first_col:end_col]
+            ratio_added(ih, hh_direct[:, jb, first_col - DIRECT_COL : end_col - DIRECT_COL], jb, first_col, end_col)
 
-        def combine(ci, jb, tag):
-            b0, b9 = ci * CW, (ci + 1) * CW
-            pieces = []
-            if b0 < BD:
-                b1 = min(b9, BD)
-                hh = ahead.pop((ci, jb)) if (ci, jb) in ahead else hh_matmul(b0, b1, jb, tag)
-                pieces.append((b0, b1, gate[jb][:, b0:b1], hh[:, 0 : b1 - b0]))
-            if b9 > BD:
-                b1 = max(b0, BD)
-                ih = acc_ih[ci][jb][:] if ci == CH - 1 else gate[jb][:, b1:b9]
-                pieces.append((b1, b9, ih, hh_dir[:, jb, b1 - BD : b9 - BD]))
-            for b1, b2, ih, hh in pieces:
-                nc.vector.scalar_tensor_tensor(
-                    out=gate[jb][:, b1:b2], in0=ih, scalar=ratio[:, jb : jb + 1], in1=hh, op0=ALU.mult, op1=ALU.add
-                )
-            if ci == CH - 1:
-                ih_bias(jb)
-            if ci == CH - 1 and jb == 1:
-                ih_ratio(2, 4)
+        def hh_chunk(ci, jb, tag):
+            return hh_matmul(ci * CW, min((ci + 1) * CW, DIRECT_COL), jb, tag)
+
+        def combine(ci, jb, hh):
+            first_col, end_col = ci * CW, min((ci + 1) * CW, DIRECT_COL)
+            ratio_added(gate[jb][:, first_col:end_col], hh[:, 0 : end_col - first_col], jb, first_col, end_col)
 
         def squash(ci, jb):
             nc.scalar.activation(
                 out=gate[jb][:, cols(ci)], in_=gate[jb][:, cols(ci)],
-                func=(ACT.Tanh if jb == 3 else ACT.Sigmoid),
-                scale=sc[:, jb : jb + 1], bias=cst[:, jb : jb + 1],
+                func=(ACT.Tanh if jb == GG else ACT.Sigmoid), scale=sc[:, jb : jb + 1], bias=cst[:, jb : jb + 1],
             )
 
-        def gate_block(ci, jb, tag):
-            combine(ci, jb, tag)
-            squash(ci, jb)
+        def o_product(ci):
+            return hh_chunk(ci, GO, ("m2", "m3")[ci % 2])
 
-        def o_ahead(ci):
-            ahead[(ci, 2)] = hh_matmul(ci * CW, (ci + 1) * CW, 2, ("m2", "m3")[ci % 2])
-
-        def o_combine(ci):
-            combine(ci, 2, ("m2", "m3")[ci % 2])
-
-        def o_gate(ci):
-            o_combine(ci)
-            squash(ci, 2)
+        def o_gate(ci, hh):
+            combine(ci, GO, hh)
+            squash(ci, GO)
 
         def forget_product(ci):
             nc.vector.tensor_tensor(
-                out=gate[0][:, cols(ci)], in0=c_bank[ci][:], in1=gate[0][:, cols(ci)], op=ALU.mult
+                out=gate[GF][:, cols(ci)], in0=c_bank[ci][:], in1=gate[GF][:, cols(ci)], op=ALU.mult
             )
 
         def input_product(engine, ci):
             engine.tensor_tensor(
-                out=gate[1][:, cols(ci)], in0=gate[1][:, cols(ci)], in1=gate[3][:, cols(ci)], op=ALU.mult
+                out=gate[GI][:, cols(ci)], in0=gate[GI][:, cols(ci)], in1=gate[GG][:, cols(ci)], op=ALU.mult
             )
 
-        def add_on_gpsimd(ci):
+        def cell_add_gpsimd(ci):
             nc.gpsimd.tensor_tensor(
-                out=gate[0][:, cols(ci)], in0=gate[0][:, cols(ci)], in1=gate[1][:, cols(ci)], op=ALU.add
+                out=gate[GF][:, cols(ci)], in0=gate[GF][:, cols(ci)], in1=gate[GI][:, cols(ci)], op=ALU.add
             )
 
-        def add_on_vector(ci):
+        def cell_add_vector(ci):
             nc.vector.scalar_tensor_tensor(
-                out=gate[0][:, cols(ci)], in0=gate[0][:, cols(ci)], scalar=1.0, in1=gate[1][:, cols(ci)],
-                op0=ALU.mult, op1=ALU.add, accum_out=csum[:, ci : ci + 1],
+                out=gate[GF][:, cols(ci)], in0=gate[GF][:, cols(ci)], scalar=1.0, in1=gate[GI][:, cols(ci)],
+                op0=ALU.mult, op1=ALU.add, accum_out=cell_sum[:, ci : ci + 1],
             )
 
-        order = [CH - 1, CH - 2] + list(range(CH - 2))
-        first, vset = order[0], {order[n] for n in VADD}
-        pe_chunks = [ci for ci in order[1:] if ci not in vset]
+        on_vector = [order[n] for n in range(CH) if n % ADD_STEP == 0 or n >= CH - 2]
+        on_tensor = [ci for ci in order if ci not in on_vector]
 
-        def cell_square(ci):
+        def cell_squared(ci):
             nc.scalar.activation(
-                out=junk[:, 0:CW], in_=gate[0][:, cols(ci)], func=ACT.Square, bias=negm0[:], scale=1.0,
-                accum_out=csq_last[:] if ci == order[-1] else csq[:, ci : ci + 1],
+                out=junk[:, 0:CW], in_=gate[GF][:, cols(ci)], func=ACT.Square, bias=shift[:], scale=1.0,
+                accum_out=cell_sq_last[:] if ci == order[-1] else cell_sq[:, ci : ci + 1],
             )
 
-        sums = {}
-
-        def cell_stats(ci):
-            if ci == first:
-                nc.vector.bn_stats(out=st_c[:], in_=gate[0][:, cols(ci)])
-                nc.vector.bn_aggr(out=mvc[:], in_=st_c[:])
-                nc.vector.tensor_scalar(out=negm0[:], in0=mvc[:, 0:1], scalar1=-1.0, scalar2=None, op0=ALU.mult)
-                return
-            cell_square(ci)
-
-        def cell_sum(ci):
-            if ci == pe_chunks[0]:
-                sums["acc"] = psum.tile([P, P], F32, tag="g", name="sums")
+        def cell_summed(ci, sums):
             for t in range(TPC):
                 nc.tensor.matmul(
-                    out=sums["acc"][:], lhsT=gate[0][:, ci * CW + t * P : ci * CW + (t + 1) * P], rhs=ident_f[:],
-                    start=(ci == pe_chunks[0] and t == 0), stop=(ci == pe_chunks[-1] and t == TPC - 1),
+                    out=sums[:], lhsT=gate[GF][:, ci * CW + t * P : ci * CW + (t + 1) * P], rhs=ident_f[:],
+                    start=(ci == on_tensor[0] and t == 0), stop=(ci == on_tensor[-1] and t == TPC - 1),
                     is_transpose=True,
                 )
 
-        def sums_out():
-            nc.vector.tensor_copy(out=part[:], in_=sums["acc"][:])
-            sums["turned"] = psum.tile([P, P], F32, tag="g", name="turned")
-            nc.tensor.transpose(sums["turned"][:], part[:], ident_f[:])
-
-        def sums_reduced():
-            k = pe_chunks[0]
-            nc.vector.reduce_sum(out=csum[:, k : k + 1], in_=sums["turned"][:], axis=AX.X)
-
-        def first_cell_stats():
-            nc.vector.tensor_scalar(
-                out=csum[:, first : first + 1], in0=mvc[:, 0:1], scalar1=float(CW), scalar2=None, op0=ALU.mult
-            )
-            nc.vector.tensor_scalar(
-                out=csq[:, first : first + 1], in0=mvc[:, 1:2], scalar1=float(CW), scalar2=None, op0=ALU.mult
-            )
-
         for n, ci in enumerate(order):
-            for jb, tag in ((0, "m0"), (1, "m1"), (3, "m3")):
-                gate_block(ci, jb, tag)
-            if n == 3:
-                first_cell_stats()
+            if n == 1:
+                for jb in range(NB):
+                    combine_direct(ci, jb)
+            for jb in (GF, GI, GG):
+                if n == 0:
+                    combine_direct(ci, jb)
+                    ih_bias(jb)
+                    if jb == GI:
+                        ih_ratio(GO, NB)
+                else:
+                    combine(ci, jb, hh_chunk(ci, jb, "m%d" % jb))
+                squash(ci, jb)
             if n == 0:
-                gate_block(ci, 2, "m2")
+                combine_direct(ci, GO)
+                ih_bias(GO)
+                squash(ci, GO)
             if n >= 1:
                 forget_product(order[n - 1])
                 input_product(nc.gpsimd, order[n - 1])
-                if order[n - 1] not in vset:
-                    add_on_gpsimd(order[n - 1])
-            if n >= 2 and order[n - 2] in vset:
-                add_on_vector(order[n - 2])
+                if order[n - 1] not in on_vector:
+                    cell_add_gpsimd(order[n - 1])
+            if n >= 2 and order[n - 2] in on_vector:
+                cell_add_vector(order[n - 2])
+            if n == 2:
+                nc.vector.tensor_scalar(
+                    out=shift[:], in0=cell_sum[:, order[0] : order[0] + 1], scalar1=-1.0 / CW, scalar2=None, op0=ALU.mult
+                )
             if n + 1 < CH:
                 c_transposed(order[n + 1])
-            if n >= 2:
-                cell_stats(order[n - 2])
-            if 4 <= n and order[n - 3] in pe_chunks:
-                cell_sum(order[n - 3])
-            if n + HGAP < CH - 2:
-                h_chunk(n + HGAP, "m2")
+            if n + H_GAP < CH - 2:
+                h_chunk(n + H_GAP, "g" if n in (0, 2) else "m2")
+            if n in O_EARLY_AT:
+                combine(O_EARLY_AT[n], GO, hh_chunk(O_EARLY_AT[n], GO, "m2"))
+            if n >= SQ0:
+                cell_squared(order[n - SQ0])
+            if n == 4:
+                sums = psum.tile([P, P], F32, tag="g", name="sums")
+            if n >= 4 and order[n - 3] in on_tensor:
+                cell_summed(order[n - 3], sums)
 
-        o_bank = {}
+        sum_rest = small("sum_rest", 1)
+        sum_turned = small("sum_turned", 1)
+        sq_total = small("sq_total", 1)
+        negmean = small("negmean", 1)
+        gneg = small("gneg", 1)
+        var_c = small("var_c", 1)
+        rstd_c = small("rstd_c", 1)
+        a_c = small("a_c", 1)
+        k_c = small("k_c", 1)
+        cell_summed(order[-3], sums)
+        forget_product(order[-1])
+        input_product(nc.vector, order[-1])
+        nc.vector.tensor_copy(out=sums_sb[:], in_=sums[:])
+        sums_turned = psum.tile([P, P], F32, tag="g", name="sums_turned")
+        nc.tensor.transpose(sums_turned[:], sums_sb[:], ident_f[:])
+        cell_add_vector(order[-2])
+        if SQ0 == 3:
+            cell_squared(order[-3])
+        cell_squared(order[-2])
+        cell_add_vector(order[-1])
+        cell_squared(order[-1])
+        for k in O_EARLY:
+            squash(k, GO)
+        o_hh = {}
+        for k in range(len(O_EARLY), min(O_GAP, len(O_EARLY) + 2)):
+            o_hh[k] = o_product(k)
+        nc.vector.reduce_sum(out=sum_turned[:], in_=sums_turned[:], axis=AX.X)
+        nc.vector.reduce_sum(out=sum_rest[:], in_=cell_sum[:], axis=AX.X)
+        nc.vector.reduce_sum(out=sq_total[:], in_=cell_sq[:], axis=AX.X)
+        nc.vector.tensor_scalar(
+            out=negmean[:], in0=sum_rest[:], scalar1=sum_turned[:], scalar2=-1.0 / B, op0=ALU.add, op1=ALU.mult
+        )
+        nc.vector.tensor_scalar(
+            out=sq_total[:], in0=sq_total[:], scalar1=1.0 / B, scalar2=EPS, op0=ALU.mult, op1=ALU.add
+        )
+        nc.vector.tensor_tensor(out=offset[:], in0=shift[:], in1=negmean[:], op=ALU.subtract)
+        nc.vector.tensor_tensor(out=gneg[:], in0=negmean[:], in1=p_gc, op=ALU.mult)
+        nc.vector.scalar_tensor_tensor(
+            out=sq_total[:], in0=offset[:], scalar=offset[:], in1=sq_total[:], op0=ALU.mult, op1=ALU.subtract
+        )
+        nc.vector.scalar_tensor_tensor(
+            out=var_c[:], in0=cell_sq_last[:], scalar=1.0 / B, in1=sq_total[:], op0=ALU.mult, op1=ALU.subtract
+        )
+        nc.gpsimd.tensor_tensor(out=rstd_c[:], in0=var_c[:], in1=neghalf[:, 0:1], op=ALU.pow)
+        for k in o_hh:
+            o_gate(k, o_hh[k])
+        nc.vector.tensor_tensor(out=a_c[:], in0=p_gc, in1=rstd_c[:], op=ALU.mult)
+        nc.vector.scalar_tensor_tensor(
+            out=k_c[:], in0=gneg[:], scalar=rstd_c[:], in1=p_bc, op0=ALU.mult, op1=ALU.add
+        )
+
+        c_turned = {}
+        o_turned = {}
 
         def transposed_f32(tag, src, ci):
-            bank = psum.tile([P, TPC, P], F32, tag=tag, name="ot")
+            bank = psum.tile([P, TPC, P], F32, tag=tag, name="bank_f")
             for t in range(TPC):
                 nc.tensor.transpose(bank[:, t, :], src[:, ci * CW + t * P : ci * CW + (t + 1) * P], ident_f[:])
             return bank
 
         def o_transposed(ci):
-            o_bank[ci] = transposed_f32(("m0", "m1", "g")[ci % 3], gate[2], ci)
+            o_turned[ci] = transposed_f32(("m0", "m1", "g")[ci % 3], gate[GO], ci)
 
-        s1c = small("s1c", 1)
-        s2c = small("s2c", 1)
-        negmean = small("negmean", 1)
-        ve_c = small("ve_c", 1)
-        rstd_c = small("rstd_c", 1)
-        a_c = small("a_c", 1)
-        k_c = small("k_c", 1)
-        for ci in range(OA):
-            o_ahead(ci)
-        if order[-3] in pe_chunks:
-            cell_sum(order[-3])
-        add_on_vector(order[-2])
-        forget_product(order[-1])
-        input_product(nc.vector, order[-1])
-        sums_out()
-        add_on_vector(order[-1])
-        cell_square(order[-2])
-        cell_square(order[-1])
-        o_gate(0)
-        sums_reduced()
-        nc.vector.reduce_sum(out=s1c[:], in_=csum[:], axis=AX.X)
-        nc.vector.reduce_sum(out=s2c[:], in_=csq[:], axis=AX.X)
-        o_gate(1)
-        nc.vector.scalar_tensor_tensor(
-            out=dlt[:], in0=s1c[:], scalar=1.0 / B, in1=negm0[:], op0=ALU.mult, op1=ALU.add
-        )
-        nc.vector.tensor_scalar(out=negmean[:], in0=s1c[:], scalar1=-1.0 / B, scalar2=None, op0=ALU.mult)
-        nc.vector.tensor_scalar(out=s2c[:], in0=s2c[:], scalar1=1.0 / B, scalar2=EPS, op0=ALU.mult, op1=ALU.add)
-        nc.vector.tensor_tensor(out=dlt[:], in0=dlt[:], in1=dlt[:], op=ALU.mult)
-        if OM:
-            o_gate(2)
-        nc.vector.tensor_tensor(out=s2c[:], in0=s2c[:], in1=dlt[:], op=ALU.subtract)
-        nc.vector.scalar_tensor_tensor(
-            out=ve_c[:], in0=csq_last[:], scalar=1.0 / B, in1=s2c[:], op0=ALU.mult, op1=ALU.add
-        )
-        nc.gpsimd.tensor_tensor(out=rstd_c[:], in0=ve_c[:], in1=neghalf[:, 0:1], op=ALU.pow)
-        for ci in range(2 + OM, OGAP):
-            o_gate(ci)
-        nc.vector.tensor_tensor(out=a_c[:], in0=par[:, 20:21], in1=rstd_c[:], op=ALU.mult)
-        nc.vector.scalar_tensor_tensor(
-            out=k_c[:], in0=a_c[:], scalar=negmean[:], in1=par[:, 21:22], op0=ALU.mult, op1=ALU.add
-        )
-
-        def tanh_c(ci):
-            return gate[3][:, cols(ci)].rearrange("p (t h) -> p t h", t=TPC)
-
-        def h_product(ci):
-            h_out = late.tile([P, TPC, P], F32, tag="h_out", bufs=OB, name="h_out")
-            nc.vector.tensor_tensor(out=h_out[:], in0=o_bank[ci][:], in1=tanh_c(ci), op=ALU.mult)
-            nc.sync.dma_start(out=outv[1][:, ci * TPC : (ci + 1) * TPC, :], in_=h_out[:])
-
-        c_next = {}
-
-        def cell_normalise(ci):
-            (nc.vector if ci < AV else nc.gpsimd).tensor_scalar(
-                out=gate[1][:, cols(ci)], in0=gate[0][:, cols(ci)], scalar1=a_c[:], scalar2=k_c[:],
+        def cell_normalised(engine, ci):
+            engine.tensor_scalar(
+                out=gate[GI][:, cols(ci)], in0=gate[GF][:, cols(ci)], scalar1=a_c[:], scalar2=k_c[:],
                 op0=ALU.mult, op1=ALU.add,
             )
 
-        def c_next_transposed(ci):
-            c_next[ci] = transposed_f32(("ta", "tb", "th")[ci % 3], gate[1], ci)
+        def c_transposed_out(ci):
+            c_turned[ci] = transposed_f32(("ta", "tb", "th")[ci % 3], gate[GI], ci)
 
-        cell_normalise(0)
-        o_ahead(OGAP)
-        def tanh_next(ci):
-            if ci < CH:
-                cell_normalise(ci)
-                c_next_transposed(ci)
-                nc.scalar.activation(out=tanh_c(ci), in_=c_next[ci][:], func=ACT.Tanh)
+        def tanh_c(ci):
+            return gate[GG][:, cols(ci)].rearrange("p (t m) -> p t m", t=TPC)
 
-        c_next_transposed(0)
+        def tanh_made(ci):
+            nc.scalar.activation(out=tanh_c(ci), in_=c_turned[ci][:], func=ACT.Tanh)
+
+        first_o = len(O_EARLY) + len(o_hh)
+        o_hh = {k: o_product(k) for k in range(first_o, first_o + 2)}
+        oc = first_o
+        cell_normalised(nc.vector, 0)
+        c_transposed_out(0)
         o_transposed(0)
-        nc.scalar.activation(out=tanh_c(0), in_=c_next[0][:], func=ACT.Tanh)
+
+        def o_ahead(k):
+            if k < LAST:
+                o_hh[k] = o_product(k)
+
+        for oc in range(first_o, O_GAP):
+            o_gate(oc, o_hh.pop(oc))
+            o_ahead(oc + 2)
+            if oc == first_o + TA:
+                tanh_made(0)
+        oc = O_GAP
         for ci in range(CH):
-            cj = ci + OGAP
-            if cj < CH - 1:
-                o_combine(cj)
-            tanh_next(ci + 1)
+            o_now = oc < LAST and ci not in OSK
+            if o_now:
+                combine(oc, GO, o_hh.pop(oc))
             if ci + 1 < CH:
+                cell_normalised(nc.gpsimd, ci + 1)
+                c_transposed_out(ci + 1)
+                tanh_made(ci + 1)
+                assert oc > ci + 1 or ci + 1 >= LAST
                 o_transposed(ci + 1)
-            c_out = late.tile([P, TPC, P], F32, tag="c_out", bufs=OB, name="c_out")
-            if ci % 2 == 0 or ci < SC:
-                nc.scalar.copy(out=c_out[:], in_=c_next[ci][:])
+            if o_now:
+                o_ahead(oc + 2)
+            c_out = late.tile([P, TPC, P], F32, tag="c_out", bufs=OUT_BUFS, name="c_out")
+            if ci not in CV:
+                nc.scalar.copy(out=c_out[:], in_=c_turned[ci][:])
             else:
-                nc.vector.tensor_copy(out=c_out[:], in_=c_next[ci][:])
-            nc.sync.dma_start(out=outv[0][:, ci * TPC : (ci + 1) * TPC, :], in_=c_out[:])
-            if cj < CH - 1:
-                squash(cj, 2)
-            if ci >= HLAG:
-                h_product(ci - HLAG)
-        for ci in range(CH - HLAG, CH):
-            h_product(ci)
+                nc.vector.tensor_copy(out=c_out[:], in_=c_turned[ci][:])
+            nc.sync.dma_start(out=c_outv[:, ci * TPC : (ci + 1) * TPC, :], in_=c_out[:])
+            if o_now:
+                squash(oc, GO)
+                oc += 1
+            h_out = late.tile([P, TPC, P], F32, tag="h_out", bufs=OUT_BUFS, name="h_out")
+            nc.vector.tensor_tensor(out=h_out[:], in0=o_turned[ci][:], in1=tanh_c(ci), op=ALU.mult)
+            nc.sync.dma_start(out=h_outv[:, ci * TPC : (ci + 1) * TPC, :], in_=h_out[:])
+        assert oc == LAST

from contextlib import ExitStack

import concourse.mybir as mybir
from concourse.masks import make_identity

F32 = mybir.dt.float32
BF16 = mybir.dt.bfloat16
U32 = mybir.dt.uint32
U8 = mybir.dt.uint8
FP8X4 = mybir.dt.float8_e4m3fn_x4
ACT = mybir.ActivationFunctionType
ALU = mybir.AluOpType
AX = mybir.AxisListType

P = 128
B, I, H = 8192, 512, 128
EPS = 1e-5
FLOPS = 2 * B * I * 4 * H + 2 * B * H * 4 * H

NB = 4
GF, GI, GO, GG = range(NB)
MX_ORDER = (GF, GG, GI, GO)

TILES = B // P
TPC = 4
CH = TILES // TPC
CW = TPC * P
LAST = CH - 1

DIRECT = TPC + 1
DIRECT_COL = (TILES - DIRECT) * P
LAST_COL = LAST * CW
PAR = 24
HG = 16
HW = H + 16
GW = H + 2

WHH_AT = 1
GRAM_AT = 2
GRAM_STEP = 6
GRAM_END = GRAM_AT + (TILES - DIRECT - 1) // GRAM_STEP
DIRECT_AT = 3
C_AT = CH // 2
GP_CHUNKS = 12
STATS_FIRST = 2

H_GAP = 9
ADD_STEP = 7
O_GAP = 6
O_EARLY_AT = {11: 0, 14: 1}
O_EARLY = list(O_EARLY_AT.values())
SX = ()
OSK = (0,4,8)
TA = 0
SQ0 = 3
SFE = (1, 2)
PAR_AT = 7
CV = tuple(range(1,CH,2))
DS = ()
OUT_BUFS = 4


def tile_lstmcell_t_kernel(
    tc, x, c, h, w_ih, w_hh, b, g_ih, b_ih, g_hh, b_hh, g_c, b_c, out_0, out_1
):
    nc = tc.nc
    xv = x.rearrange("(p s) k -> p s k", s=TILES)
    cv = c.rearrange("(p s) k -> p s k", s=TILES)
    hv = h.rearrange("(p s) k -> p s k", s=TILES)
    c_outv = out_0.rearrange("(p s) k -> p s k", s=TILES)
    h_outv = out_1.rearrange("(p s) k -> p s k", s=TILES)
    with ExitStack() as ctx:
        ctx.enter_context(tc.manual_schedule())
        keep = ctx.enter_context(tc.tile_pool(name="keep", bufs=1))
        psum = ctx.enter_context(tc.psum_pool(name="psum", bufs=1))
        cpool = ctx.enter_context(tc.tile_pool(name="cpool", bufs=4))

        gate = [keep.tile([P, B], F32, name="gate%d" % jb) for jb in range(NB)]
        hT = keep.tile([P, B], BF16)
        hh_direct = keep.tile([P, NB, DIRECT * P], F32)
        h_nat = [keep.tile([P, HG, HW], BF16, name="h_nat%d" % g) for g in range(TILES // HG)]
        w_codes = keep.tile([P, NB * P], U32, align_bytes=64)
        w_scales = keep.tile([P, NB * P], U8, align_bytes=64)
        whh_nat = keep.tile([P, NB, H], BF16)
        whhT_b = keep.tile([P, NB * P], BF16)
        whhT_f = keep.tile([P, NB * P], F32)
        ident_f = keep.tile([P, P], F32)
        ident_b = keep.tile([P, P], BF16)
        rows = keep.tile([P, P], BF16)
        par = keep.tile([P, PAR], F32)
        p_b, p_gih, p_bih, p_ghh, p_bhh = [par[:, NB * v : NB * (v + 1)] for v in range(5)]
        p_gc, p_bc = par[:, 5 * NB : 5 * NB + 1], par[:, 5 * NB + 1 : 5 * NB + 2]
        gram_sb = keep.tile([P, GW], F32)
        gg_acc = keep.tile([P, CW], F32)
        st_ih = keep.tile([P, NB - 1, CH, 6], F32)
        gg_sum = keep.tile([P, CH], F32)
        gg_sq = keep.tile([P, 1 + CH - GP_CHUNKS], F32)
        gg_red = keep.tile([P, 2], F32)
        h_sum = keep.tile([P, 1], F32)
        sq_direct = keep.tile([P, 2, NB], F32)
        cell_sum = keep.tile([P, CH], F32)
        cell_sq = keep.tile([P, CH], F32)
        cell_sq_last = keep.tile([P, 1], F32)
        junk = keep.tile([P, 2 * CW], BF16)
        prod = keep.tile([P, 2, P], F32)
        neghalf = keep.tile([P, NB], F32)
        warm = keep.tile([P, 1], F32)
        mv = keep.tile([P, NB, 2], F32)

        def small(name, width=NB):
            return keep.tile([P, width], F32, name=name)

        def cols(ci):
            return slice(ci * CW, (ci + 1) * CW)

        def blk(jb):
            return slice(jb * P, (jb + 1) * P)

        def h_tile(s):
            return h_nat[s // HG][:, s % HG, :]

        def transpose_bf16(tag, tiles):
            bank = psum.tile([P, len(tiles) * P], BF16, tag=tag, name="bank_b")
            for t, src in enumerate(tiles):
                nc.tensor.transpose(bank[:, t * P : (t + 1) * P], src, ident_b[:])
            return bank

        def h_transposed(first, end, tag):
            return transpose_bf16(tag, [h_tile(s)[:, 0:H] for s in range(first, end)])

        def hh_matmul(first_col, end_col, jb, tag):
            acc = psum.tile([P, CW], F32, tag=tag, name="acc")
            nc.tensor.matmul(
                out=acc[:, 0 : end_col - first_col], lhsT=whhT_b[:, blk(jb)], rhs=hT[:, first_col:end_col],
                start=True, stop=True,
            )
            return acc

        nc.vector.memset(warm[:], 0.0)
        nc.scalar.activation(out=warm[:], in_=warm[:], func=ACT.Sigmoid)
        make_identity(nc, ident_f[:])
        make_identity(nc, ident_b[:])
        nc.vector.memset(rows[:], 0.0)
        nc.vector.memset(cell_sum[:], 0.0)
        nc.vector.memset(cell_sq[:], 0.0)
        nc.vector.memset(neghalf[:], -0.5)
        for g in range(TILES // HG):
            nc.vector.memset(h_nat[g][:, :, H:HW], 1.0)

        with tc.tile_pool(name="stage", bufs=2) as stage:
            x_sb = {}
            words_in = {}
            grp = {}
            codes = {}
            scales = {}
            ih_bank = {}

            def load_x(ci, pieces=1):
                x_sb[ci] = stage.tile([P, TPC, I], BF16, tag="xs", bufs=4, name="x_sb")
                n = TPC // pieces
                for t in range(0, TPC, n):
                    nc.sync.dma_start(
                        out=x_sb[ci][:, t : t + n, :], in_=xv[:, ci * TPC + t : ci * TPC + t + n, :]
                    )

            def load_h(g):
                nc.sync.dma_start(out=h_nat[g][:, :, 0:H], in_=hv[:, g * HG : (g + 1) * HG, :])

            def load_c(g):
                c_nat[g] = cpool.tile([P, HG, H], BF16, tag="cn", bufs=4, name="c_nat")
                nc.sync.dma_start(out=c_nat[g][:], in_=cv[:, g * HG : (g + 1) * HG, :])

            def words_transposed(key, src, tags=("ta", "tb")):
                words_in[key] = []
                for half, tag in enumerate(tags):
                    bank = psum.tile([P, 2, 2 * P], F32, tag=tag, name="bank_w")
                    for a in range(2):
                        words = src[:, 2 * half + a, :].bitcast(F32)
                        for u in range(2):
                            nc.tensor.transpose(bank[:, u, blk(a)], words[:, u : 2 * P : 2], ident_f[:])
                    words_in[key].append(bank)

            def new_grp(key):
                grp[key] = stage.tile([P, 4 * CW], BF16, tag="grp", bufs=2, align_bytes=64, name="grp")

            def words_out(key, half, copy):
                words = grp[key][:].bitcast(F32).rearrange("p (r u) -> p r u", u=2)
                copy(
                    out=words[:, half * 2 * P : (half + 1) * 2 * P, :],
                    in_=words_in[key][half][:].rearrange("p u r -> p r u"),
                )

            def quantise(ci):
                codes[ci] = stage.tile([P, CW], U32, tag="codes", bufs=2, align_bytes=64, name="codes")
                scales[ci] = stage.tile([P, CW], U8, tag="scales", bufs=2, align_bytes=64, name="scales")
                nc.vector.quantize_mx(out=codes[ci][:].bitcast(FP8X4), scales=scales[ci][:], in_=grp[ci][:])

            def ih_matmul(ci):
                ih_bank[ci] = {}
                for pos, jb in enumerate(MX_ORDER):
                    acc = psum.tile([P, CW], F32, tag="m%d" % jb, name="acc")
                    nc.tensor.matmul_mx(
                        out=acc[:],
                        lhsT=w_codes[:, blk(pos)].bitcast(FP8X4),
                        lhsT_scale=w_scales[:, blk(pos)],
                        rhs=codes[ci][:].bitcast(FP8X4),
                        rhs_scale=scales[ci][:],
                        start=True,
                        stop=True,
                    )
                    ih_bank[ci][jb] = acc

            def gg_square(ci):
                k = 1 + ci - GP_CHUNKS
                nc.scalar.activation(
                    out=junk[:, 0:CW], in_=ih_bank[ci][GG][:], func=ACT.Square, accum_out=gg_sq[:, k : k + 1]
                )

            def ih_copied(ci):
                for jb in MX_ORDER:
                    if jb == GG:
                        nc.scalar.activation(
                            out=gate[jb][:, cols(ci)], in_=ih_bank[ci][jb][:], func=ACT.Copy,
                            accum_out=gg_sum[:, ci : ci + 1],
                        )
                        if ci >= GP_CHUNKS:
                            gg_square(ci)
                    else:
                        nc.scalar.copy(out=gate[jb][:, cols(ci)], in_=ih_bank[ci][jb][:])

            def ih_stats(ci, jb):
                src = ih_bank[ci][jb][:] if ci == LAST else gate[jb][:, cols(ci)]
                nc.vector.bn_stats(out=st_ih[:, jb, ci, :], in_=src)

            gg_new = {}

            def gg_added(ci):
                nc.gpsimd.tensor_tensor(out=gg_acc[:], in0=gg_acc[:], in1=gg_new.pop(ci)[:], op=ALU.add)

            def gg_gate(ci):
                gg_new[ci] = stage.tile([P, CW], F32, tag="gsq", bufs=3, name="sq")
                nc.vector.memset(gg_new[ci][:, 0:1], 0.0)

            def gg_squared(ci):
                src = gate[GG][:, cols(ci)]
                if ci == 0:
                    nc.gpsimd.tensor_tensor(out=gg_acc[:], in0=src, in1=src, op=ALU.mult)
                else:
                    nc.gpsimd.tensor_tensor(out=gg_new[ci][:], in0=src, in1=src, op=ALU.mult)
                if ci >= 2:
                    gg_added(ci - 1)
                if ci == GP_CHUNKS - 1:
                    gg_added(ci)

            w_sb = stage.tile([P, NB, I], BF16, tag="xs", bufs=4, name="w_sb")
            wv = w_ih.rearrange("(jb m) k -> m jb k", m=P)

            def load_w(pos):
                nc.sync.dma_start(out=w_sb[:, pos, :], in_=wv[:, MX_ORDER[pos], :])

            load_w(0)
            load_x(0, TPC)
            for pos in range(1, NB):
                load_w(pos)
            load_x(1)
            load_x(2)

            w_grp = stage.tile([P, 4 * CW], BF16, tag="grp", bufs=2, align_bytes=64, name="grp")
            w_bank = {}

            def w_transposed(first, end, tag):
                bank = psum.tile([P, 2, (end - first) * P], F32, tag=tag, name="bank_w")
                for pos in range(first, end):
                    words = w_sb[:, pos, :].bitcast(F32)
                    for u in range(2):
                        nc.tensor.transpose(bank[:, u, blk(pos - first)], words[:, u : 2 * P : 2], ident_f[:])
                w_bank[first] = bank

            def w_out(first, end):
                words = w_grp[:].bitcast(F32).rearrange("p (r u) -> p r u", u=2)
                nc.scalar.copy(out=words[:, first * P : end * P, :], in_=w_bank[first][:].rearrange("p u r -> p r u"))

            def w_quantised(first, end):
                s = slice(first * P, end * P)
                nc.vector.quantize_mx(
                    out=w_codes[:, s].bitcast(FP8X4), scales=w_scales[:, s], in_=w_grp[:, first * CW : end * CW]
                )

            w_transposed(0, 1, "th")
            words_transposed(0, x_sb[0])
            w_transposed(1, 3, "g")
            w_transposed(3, 4, "m2")
            load_x(3)
            nc.sync.dma_start(out=whh_nat[:], in_=w_hh.rearrange("(jb m) k -> m jb k", m=P))
            load_h(TILES // HG - 1)
            load_x(4)
            w_out(0, 1)
            w_quantised(0, 1)
            new_grp(0)
            words_out(0, 0, nc.scalar.copy)
            words_out(0, 1, nc.vector.tensor_copy)
            w_out(1, 3)
            w_out(3, 4)
            quantise(0)
            w_quantised(1, 3)
            w_quantised(3, 4)
            words_transposed(1, x_sb[1])
            load_x(5)
            ih_matmul(0)

            c_nat = {}

            hh_sq = small("hh_sq")
            hh_sum = small("hh_sum")
            bias_sum = small("bias_sum")
            mean_hh = small("mean_hh")
            mean_sq = small("mean_sq")
            var_hh = small("var_hh")
            rstd_hh = small("rstd_hh")
            a_hh = small("a_hh")
            tiny = small("tiny")
            sc = small("sc")
            ratio = small("ratio")
            cst = small("cst")

            def hh_scale():
                def tt(out, in0, in1, op):
                    nc.gpsimd.tensor_tensor(out=out[:], in0=in0, in1=in1, op=op)

                def ts(out, in0, scalar1, op0, scalar2, op1):
                    nc.gpsimd.tensor_scalar(out=out[:], in0=in0, scalar1=scalar1, scalar2=scalar2, op0=op0, op1=op1)

                tt(hh_sq, hh_sq[:], sq_direct[:, 0, :], ALU.add)
                tt(hh_sq, hh_sq[:], sq_direct[:, 1, :], ALU.add)
                ts(mean_hh, hh_sum[:], 1.0 / B, ALU.mult, 0.0, ALU.add)
                tt(mean_sq, mean_hh[:], mean_hh[:], ALU.mult)
                ts(hh_sq, hh_sq[:], 1.0 / B, ALU.mult, 0.0, ALU.add)
                tt(var_hh, hh_sq[:], mean_sq[:], ALU.subtract)
                ts(var_hh, var_hh[:], 0.0, ALU.max, EPS, ALU.add)
                tt(rstd_hh, var_hh[:], neghalf[:], ALU.pow)
                tt(a_hh, p_ghh, rstd_hh[:], ALU.mult)
                ts(tiny, a_hh[:], 0.0, ALU.is_equal, 1e-30, ALU.mult)
                tt(sc, a_hh[:], tiny[:], ALU.add)
                tt(bias_sum, p_b, p_bih, ALU.add)
                tt(bias_sum, bias_sum[:], p_bhh, ALU.add)
                tt(cst, a_hh[:], mean_hh[:], ALU.mult)
                tt(cst, bias_sum[:], cst[:], ALU.subtract)

            gram_tiles = list(range(TILES - HG, TILES - DIRECT)) + list(range(TILES - HG))
            for ci in range(CH):
                nxt = ci + 1
                if nxt < CH:
                    new_grp(nxt)
                    words_out(nxt, 0, nc.scalar.copy)
                if ci in SFE:
                    for jb in range(STATS_FIRST):
                        ih_stats(ci - 1, jb)
                if nxt < CH:
                    words_out(nxt, 1, nc.scalar.copy if nxt in SX else nc.vector.tensor_copy)
                if ci >= 1 and ci not in SFE:
                    for jb in range(STATS_FIRST):
                        ih_stats(ci - 1, jb)
                if ci == WHH_AT + 1:
                    nc.vector.tensor_copy(out=whhT_b[:], in_=whh_bank[:])
                    nc.gpsimd.tensor_scalar(
                        out=whhT_f[:], in0=whhT_b[:], scalar1=1.0, scalar2=0.0, op0=ALU.mult, op1=ALU.add
                    )
                if 2 <= ci <= GP_CHUNKS:
                    gg_gate(ci - 1)
                if nxt < CH:
                    quantise(nxt)
                if 1 <= ci <= GP_CHUNKS:
                    gg_squared(ci - 1)
                if DIRECT_AT <= ci < DIRECT_AT + NB:
                    hh_bank = hh_matmul(LAST_COL, B, ci - DIRECT_AT, "th")
                    (nc.scalar.copy if ci - DIRECT_AT in DS else nc.vector.tensor_copy)(out=hh_direct[:, ci - DIRECT_AT, LAST_COL - DIRECT_COL :], in_=hh_bank[:])
                if ci == DIRECT_AT + NB:
                    hh_bank = psum.tile([P, NB, P], F32, tag="th", name="hh_bank")
                    for jb in range(NB):
                        nc.tensor.matmul(
                            out=hh_bank[:, jb, :], lhsT=whhT_b[:, blk(jb)], rhs=hT[:, DIRECT_COL:LAST_COL],
                            start=True, stop=True,
                        )
                    nc.vector.tensor_copy(out=hh_direct[:, :, 0 : LAST_COL - DIRECT_COL], in_=hh_bank[:])
                if ci >= 1:
                    for jb in range(STATS_FIRST, NB - 1):
                        ih_stats(ci - 1, jb)
                if ci + 2 < CH:
                    words_transposed(ci + 2, x_sb[ci + 2])
                    if ci + 6 < CH:
                        load_x(ci + 6)
                if ci % 2 == 0 and ci // 2 < TILES // HG - 1:
                    load_h(ci // 2)
                if C_AT <= ci < C_AT + TILES // HG:
                    load_c(ci - C_AT)
                if ci == PAR_AT:
                    for v, vec in enumerate((b, g_ih, b_ih, g_hh, b_hh)):
                        nc.sync.dma_start(out=rows[NB * v : NB * (v + 1), :], in_=vec.rearrange("(r m) -> r m", m=P))
                    for v, vec in enumerate((g_c, b_c)):
                        nc.sync.dma_start(out=rows[5 * NB + v : 5 * NB + v + 1, :], in_=vec.rearrange("(r m) -> r m", m=P))
                if ci == PAR_AT + 2:
                    turned = psum.tile([P, P], BF16, tag="th", name="turned")
                    nc.tensor.transpose(turned[:], rows[:], ident_b[:])
                    nc.vector.tensor_copy(out=par[:], in_=turned[:, 0:PAR])
                if ci == WHH_AT:
                    turned = transpose_bf16("g", [whh_nat[:, jb, :] for jb in range(NB)])
                    whh_bank = turned
                if ci == LAST - 1:
                    nc.scalar.activation(out=junk[:, CW:], in_=gg_acc[:], func=ACT.Copy, accum_out=gg_sq[:, 0:1])
                if ci == LAST:
                    nc.vector.reciprocal(out=ratio[:], in_=sc[:])
                    nc.vector.tensor_tensor(out=ratio[:], in0=ratio[:], in1=p_gih, op=ALU.mult)
                else:
                    ih_copied(ci)
                if ci == GRAM_AT:
                    turned = h_transposed(TILES - DIRECT, TILES, "th")
                    nc.scalar.activation(
                        out=hT[:, DIRECT_COL:], in_=turned[:], func=ACT.Copy, accum_out=h_sum[:]
                    )
                    gram = psum.tile([P, GW], F32, tag="g", name="gram")
                if GRAM_AT <= ci <= GRAM_END:
                    first = GRAM_STEP * (ci - GRAM_AT)
                    for s in gram_tiles[first : first + GRAM_STEP]:
                        nc.tensor.matmul(
                            out=gram[:], lhsT=h_tile(s)[:, 0:H], rhs=h_tile(s)[:, 0:GW],
                            start=(s == gram_tiles[0]), stop=(s == gram_tiles[-1]),
                        )
                if nxt < CH:
                    ih_matmul(nxt)
                if DIRECT_AT <= ci < DIRECT_AT + NB:
                    jb = ci - DIRECT_AT
                    nc.scalar.activation(
                        out=junk[:, 0:CW], in_=hh_bank[:], func=ACT.Square, accum_out=sq_direct[:, 0, jb : jb + 1]
                    )
                if ci == DIRECT_AT + NB:
                    for jb in range(NB):
                        nc.scalar.activation(
                            out=junk[:, blk(jb)], in_=hh_bank[:, jb, :], func=ACT.Square,
                            accum_out=sq_direct[:, 1, jb : jb + 1],
                        )
                if ci == GRAM_END:
                    nc.vector.tensor_copy(out=gram_sb[:], in_=gram[:])
                    nc.vector.tensor_tensor(
                        out=gram_sb[:, H : H + 1], in0=gram_sb[:, H : H + 1], in1=h_sum[:], op=ALU.add
                    )
                if ci == GRAM_END + 1:
                    gw_banks = []
                    for pair, tag in enumerate(("th", "g")):
                        gw = psum.tile([P, 2, GW], F32, tag=tag, name="gw")
                        for a in range(2):
                            nc.tensor.matmul(
                                out=gw[:, a, :], lhsT=whhT_f[:, blk(2 * pair + a)], rhs=gram_sb[:],
                                start=True, stop=True,
                            )
                        gw_banks.append(gw)
                if ci == GRAM_END + 2:
                    for pair, gw in enumerate(gw_banks):
                        for a in range(2):
                            jb = 2 * pair + a
                            nc.vector.scalar_tensor_tensor(
                                out=prod[:, a, :], in0=gw[:, a, 0:H], scalar=1.0, in1=whh_nat[:, jb, :],
                                op0=ALU.mult, op1=ALU.mult, accum_out=hh_sq[:, jb : jb + 1],
                            )
                        nc.vector.tensor_copy(out=hh_sum[:, 2 * pair : 2 * pair + 2], in_=gw[:, :, H])
                    hh_scale()

        late = ctx.enter_context(tc.tile_pool(name="late", bufs=OUT_BUFS))
        var_ih = small("var_ih")
        rstd_ih = small("rstd_ih")
        neg_gmean = small("neg_gmean")

        def ih_rstd(first, end):
            s = slice(first, end)
            nc.vector.tensor_scalar(
                out=var_ih[:, s], in0=mv[:, s, 1], scalar1=0.0, scalar2=EPS, op0=ALU.max, op1=ALU.add
            )
            nc.gpsimd.tensor_tensor(out=rstd_ih[:, s], in0=var_ih[:, s], in1=neghalf[:, s], op=ALU.pow)
            nc.vector.scalar_tensor_tensor(
                out=neg_gmean[:, s], in0=mv[:, s, 0], scalar=-1.0, in1=p_gih[:, s], op0=ALU.mult, op1=ALU.mult
            )

        def ih_ratio(first, end):
            s = slice(first, end)
            nc.vector.tensor_tensor(out=ratio[:, s], in0=ratio[:, s], in1=rstd_ih[:, s], op=ALU.mult)

        def ih_bias(jb):
            s = slice(jb, jb + 1)
            nc.vector.scalar_tensor_tensor(
                out=cst[:, s], in0=neg_gmean[:, s], scalar=rstd_ih[:, s], in1=cst[:, s], op0=ALU.mult, op1=ALU.add
            )

        def ih_mean_var(jb):
            nc.vector.bn_aggr(out=mv[:, jb, :], in_=st_ih[:, jb, :, :].rearrange("p c s -> p (c s)"))

        nc.scalar.activation(
            out=junk[:, CW:], in_=ih_bank[LAST][GG][:], func=ACT.Copy, accum_out=gg_sum[:, LAST : LAST + 1]
        )
        gg_square(LAST)
        ih_stats(LAST, GF)
        ih_stats(LAST, GI)
        ih_mean_var(GF)
        ih_mean_var(GI)
        ih_rstd(GF, GO)
        ih_stats(LAST, GO)
        nc.vector.reduce_sum(out=gg_red[:, 0:1], in_=gg_sum[:], axis=AX.X)
        nc.vector.reduce_sum(out=gg_red[:, 1:2], in_=gg_sq[:], axis=AX.X)
        nc.vector.tensor_scalar(out=mv[:, GG, 0:1], in0=gg_red[:, 0:1], scalar1=1.0 / B, scalar2=None, op0=ALU.mult)
        ih_ratio(GF, GO)
        nc.vector.tensor_tensor(out=gg_red[:, 0:1], in0=mv[:, GG, 0:1], in1=mv[:, GG, 0:1], op=ALU.mult)
        ih_mean_var(GO)
        nc.vector.scalar_tensor_tensor(
            out=mv[:, GG, 1:2], in0=gg_red[:, 1:2], scalar=1.0 / B, in1=gg_red[:, 0:1], op0=ALU.mult, op1=ALU.subtract
        )
        ih_rstd(GO, NB)

        c_bank = {}

        def c_transposed(ci):
            tiles = [c_nat[s // HG][:, s % HG, :] for s in range(ci * TPC, (ci + 1) * TPC)]
            c_bank[ci] = transpose_bf16(("ta", "tb", "th")[len(c_bank) % 3], tiles)

        def h_chunk(ci, tag):
            first, end = ci * TPC, min((ci + 1) * TPC, TILES - DIRECT)
            turned = h_transposed(first, end, tag)
            nc.scalar.copy(out=hT[:, first * P : end * P], in_=turned[:, 0 : (end - first) * P])

        order = [LAST, LAST - 1] + list(range(LAST - 1))
        for k, ci in enumerate([LAST - 1] + list(range(H_GAP))):
            h_chunk(ci, ("tb", "th", "g", "ta")[k % 4])
        c_transposed(LAST)

        shift = small("shift", 1)
        offset = small("offset", 1)
        sums_sb = keep.tile([P, P], F32)

        def ratio_added(ih, hh, jb, first_col, end_col):
            nc.vector.scalar_tensor_tensor(
                out=gate[jb][:, first_col:end_col], in0=ih, scalar=ratio[:, jb : jb + 1], in1=hh,
                op0=ALU.mult, op1=ALU.add,
            )

        def combine_direct(ci, jb):
            first_col, end_col = max(ci * CW, DIRECT_COL), (ci + 1) * CW
            ih = ih_bank[ci][jb][:] if ci == LAST else gate[jb][:, first_col:end_col]
            ratio_added(ih, hh_direct[:, jb, first_col - DIRECT_COL : end_col - DIRECT_COL], jb, first_col, end_col)

        def hh_chunk(ci, jb, tag):
            return hh_matmul(ci * CW, min((ci + 1) * CW, DIRECT_COL), jb, tag)

        def combine(ci, jb, hh):
            first_col, end_col = ci * CW, min((ci + 1) * CW, DIRECT_COL)
            ratio_added(gate[jb][:, first_col:end_col], hh[:, 0 : end_col - first_col], jb, first_col, end_col)

        def squash(ci, jb):
            nc.scalar.activation(
                out=gate[jb][:, cols(ci)], in_=gate[jb][:, cols(ci)],
                func=(ACT.Tanh if jb == GG else ACT.Sigmoid), scale=sc[:, jb : jb + 1], bias=cst[:, jb : jb + 1],
            )

        def o_product(ci):
            return hh_chunk(ci, GO, ("m2", "m3")[ci % 2])

        def o_gate(ci, hh):
            combine(ci, GO, hh)
            squash(ci, GO)

        def forget_product(ci):
            nc.vector.tensor_tensor(
                out=gate[GF][:, cols(ci)], in0=c_bank[ci][:], in1=gate[GF][:, cols(ci)], op=ALU.mult
            )

        def input_product(engine, ci):
            engine.tensor_tensor(
                out=gate[GI][:, cols(ci)], in0=gate[GI][:, cols(ci)], in1=gate[GG][:, cols(ci)], op=ALU.mult
            )

        def cell_add_gpsimd(ci):
            nc.gpsimd.tensor_tensor(
                out=gate[GF][:, cols(ci)], in0=gate[GF][:, cols(ci)], in1=gate[GI][:, cols(ci)], op=ALU.add
            )

        def cell_add_vector(ci):
            nc.vector.scalar_tensor_tensor(
                out=gate[GF][:, cols(ci)], in0=gate[GF][:, cols(ci)], scalar=1.0, in1=gate[GI][:, cols(ci)],
                op0=ALU.mult, op1=ALU.add, accum_out=cell_sum[:, ci : ci + 1],
            )

        on_vector = [order[n] for n in range(CH) if n % ADD_STEP == 0 or n >= CH - 2]
        on_tensor = [ci for ci in order if ci not in on_vector]

        def cell_squared(ci):
            nc.scalar.activation(
                out=junk[:, 0:CW], in_=gate[GF][:, cols(ci)], func=ACT.Square, bias=shift[:], scale=1.0,
                accum_out=cell_sq_last[:] if ci == order[-1] else cell_sq[:, ci : ci + 1],
            )

        def cell_summed(ci, sums):
            for t in range(TPC):
                nc.tensor.matmul(
                    out=sums[:], lhsT=gate[GF][:, ci * CW + t * P : ci * CW + (t + 1) * P], rhs=ident_f[:],
                    start=(ci == on_tensor[0] and t == 0), stop=(ci == on_tensor[-1] and t == TPC - 1),
                    is_transpose=True,
                )

        for n, ci in enumerate(order):
            if n == 1:
                for jb in range(NB):
                    combine_direct(ci, jb)
            for jb in (GF, GI, GG):
                if n == 0:
                    combine_direct(ci, jb)
                    ih_bias(jb)
                    if jb == GI:
                        ih_ratio(GO, NB)
                else:
                    combine(ci, jb, hh_chunk(ci, jb, "m%d" % jb))
                squash(ci, jb)
            if n == 0:
                combine_direct(ci, GO)
                ih_bias(GO)
                squash(ci, GO)
            if n >= 1:
                forget_product(order[n - 1])
                input_product(nc.gpsimd, order[n - 1])
                if order[n - 1] not in on_vector:
                    cell_add_gpsimd(order[n - 1])
            if n >= 2 and order[n - 2] in on_vector:
                cell_add_vector(order[n - 2])
            if n == 2:
                nc.vector.tensor_scalar(
                    out=shift[:], in0=cell_sum[:, order[0] : order[0] + 1], scalar1=-1.0 / CW, scalar2=None, op0=ALU.mult
                )
            if n + 1 < CH:
                c_transposed(order[n + 1])
            if n + H_GAP < CH - 2:
                h_chunk(n + H_GAP, "g" if n in (0, 2) else "m2")
            if n in O_EARLY_AT:
                combine(O_EARLY_AT[n], GO, hh_chunk(O_EARLY_AT[n], GO, "m2"))
            if n >= SQ0:
                cell_squared(order[n - SQ0])
            if n == 4:
                sums = psum.tile([P, P], F32, tag="g", name="sums")
            if n >= 4 and order[n - 3] in on_tensor:
                cell_summed(order[n - 3], sums)

        sum_rest = small("sum_rest", 1)
        sum_turned = small("sum_turned", 1)
        sq_total = small("sq_total", 1)
        negmean = small("negmean", 1)
        gneg = small("gneg", 1)
        var_c = small("var_c", 1)
        rstd_c = small("rstd_c", 1)
        a_c = small("a_c", 1)
        k_c = small("k_c", 1)
        cell_summed(order[-3], sums)
        forget_product(order[-1])
        input_product(nc.vector, order[-1])
        nc.vector.tensor_copy(out=sums_sb[:], in_=sums[:])
        sums_turned = psum.tile([P, P], F32, tag="g", name="sums_turned")
        nc.tensor.transpose(sums_turned[:], sums_sb[:], ident_f[:])
        cell_add_vector(order[-2])
        if SQ0 == 3:
            cell_squared(order[-3])
        cell_squared(order[-2])
        cell_add_vector(order[-1])
        cell_squared(order[-1])
        for k in O_EARLY:
            squash(k, GO)
        o_hh = {}
        for k in range(len(O_EARLY), min(O_GAP, len(O_EARLY) + 2)):
            o_hh[k] = o_product(k)
        nc.vector.reduce_sum(out=sum_turned[:], in_=sums_turned[:], axis=AX.X)
        nc.vector.reduce_sum(out=sum_rest[:], in_=cell_sum[:], axis=AX.X)
        nc.vector.reduce_sum(out=sq_total[:], in_=cell_sq[:], axis=AX.X)
        nc.vector.tensor_scalar(
            out=negmean[:], in0=sum_rest[:], scalar1=sum_turned[:], scalar2=-1.0 / B, op0=ALU.add, op1=ALU.mult
        )
        nc.vector.tensor_scalar(
            out=sq_total[:], in0=sq_total[:], scalar1=1.0 / B, scalar2=EPS, op0=ALU.mult, op1=ALU.add
        )
        nc.vector.tensor_tensor(out=offset[:], in0=shift[:], in1=negmean[:], op=ALU.subtract)
        nc.vector.tensor_tensor(out=gneg[:], in0=negmean[:], in1=p_gc, op=ALU.mult)
        nc.vector.scalar_tensor_tensor(
            out=sq_total[:], in0=offset[:], scalar=offset[:], in1=sq_total[:], op0=ALU.mult, op1=ALU.subtract
        )
        nc.vector.scalar_tensor_tensor(
            out=var_c[:], in0=cell_sq_last[:], scalar=1.0 / B, in1=sq_total[:], op0=ALU.mult, op1=ALU.subtract
        )
        nc.gpsimd.tensor_tensor(out=rstd_c[:], in0=var_c[:], in1=neghalf[:, 0:1], op=ALU.pow)
        for k in o_hh:
            o_gate(k, o_hh[k])
        nc.vector.tensor_tensor(out=a_c[:], in0=p_gc, in1=rstd_c[:], op=ALU.mult)
        nc.vector.scalar_tensor_tensor(
            out=k_c[:], in0=gneg[:], scalar=rstd_c[:], in1=p_bc, op0=ALU.mult, op1=ALU.add
        )

        c_turned = {}
        o_turned = {}

        def transposed_f32(tag, src, ci):
            bank = psum.tile([P, TPC, P], F32, tag=tag, name="bank_f")
            for t in range(TPC):
                nc.tensor.transpose(bank[:, t, :], src[:, ci * CW + t * P : ci * CW + (t + 1) * P], ident_f[:])
            return bank

        def o_transposed(ci):
            o_turned[ci] = transposed_f32(("m0", "m1", "g")[ci % 3], gate[GO], ci)

        def cell_normalised(engine, ci):
            engine.tensor_scalar(
                out=gate[GI][:, cols(ci)], in0=gate[GF][:, cols(ci)], scalar1=a_c[:], scalar2=k_c[:],
                op0=ALU.mult, op1=ALU.add,
            )

        def c_transposed_out(ci):
            c_turned[ci] = transposed_f32(("ta", "tb", "th")[ci % 3], gate[GI], ci)

        def tanh_c(ci):
            return gate[GG][:, cols(ci)].rearrange("p (t m) -> p t m", t=TPC)

        def tanh_made(ci):
            nc.scalar.activation(out=tanh_c(ci), in_=c_turned[ci][:], func=ACT.Tanh)

        first_o = len(O_EARLY) + len(o_hh)
        o_hh = {k: o_product(k) for k in range(first_o, first_o + 2)}
        oc = first_o
        cell_normalised(nc.vector, 0)
        c_transposed_out(0)
        o_transposed(0)

        def o_ahead(k):
            if k < LAST:
                o_hh[k] = o_product(k)

        for oc in range(first_o, O_GAP):
            o_gate(oc, o_hh.pop(oc))
            o_ahead(oc + 2)
            if oc == first_o + TA:
                tanh_made(0)
        oc = O_GAP
        for ci in range(CH):
            o_now = oc < LAST and ci not in OSK
            if o_now:
                combine(oc, GO, o_hh.pop(oc))
            if ci + 1 < CH:
                cell_normalised(nc.gpsimd, ci + 1)
                c_transposed_out(ci + 1)
                tanh_made(ci + 1)
                assert oc > ci + 1 or ci + 1 >= LAST
                o_transposed(ci + 1)
            if o_now:
                o_ahead(oc + 2)
            c_out = late.tile([P, TPC, P], F32, tag="c_out", bufs=OUT_BUFS, name="c_out")
            if ci not in CV:
                nc.scalar.copy(out=c_out[:], in_=c_turned[ci][:])
            else:
                nc.vector.tensor_copy(out=c_out[:], in_=c_turned[ci][:])
            nc.sync.dma_start(out=c_outv[:, ci * TPC : (ci + 1) * TPC, :], in_=c_out[:])
            if o_now:
                squash(oc, GO)
                oc += 1
            h_out = late.tile([P, TPC, P], F32, tag="h_out", bufs=OUT_BUFS, name="h_out")
            nc.vector.tensor_tensor(out=h_out[:], in0=o_turned[ci][:], in1=tanh_c(ci), op=ALU.mult)
            nc.sync.dma_start(out=h_outv[:, ci * TPC : (ci + 1) * TPC, :], in_=h_out[:])
        assert oc == LAST
